import numpy as np
import ml_dtypes


def mxq(x, axis, fmt="e4m3"):
    dtype, down = {"e4m3": (ml_dtypes.float8_e4m3fn, 7), "e5m2": (ml_dtypes.float8_e5m2, 14)}[fmt]
    v = np.moveaxis(np.asarray(x, np.float32).astype(ml_dtypes.bfloat16).astype(np.float64), axis, -1)
    blocks = v.reshape(v.shape[:-1] + (-1, 32))
    amax = np.abs(blocks).max(-1, keepdims=True)
    byte = np.maximum(np.where(amax > 0, np.frexp(amax)[1] - 1 + 127, 0) - down, 1)
    scale = np.exp2(byte - 127.0)
    codes = (blocks / scale).astype(np.float32).astype(dtype).astype(np.float64)
    return np.moveaxis((codes * scale).reshape(v.shape), -1, axis)


WIDE = False


def mx_kscale(k):
    if not WIDE:
        return np.ones(k)
    levels = np.array([10, -10, 5, -5, 0])
    if k % 512:
        return np.exp2(np.random.permutation(np.resize(levels, k // 32))).repeat(32)
    a = np.empty((k // 512, 16))
    for p in range(k // 512):
        a[p, :8] = np.random.permutation(np.resize(levels, 8))
        for g in range(8):
            far = levels[np.abs(levels - a[p, g]) >= 10]
            a[p, g + 8] = far[np.random.randint(len(far))]
    return np.exp2(a.ravel()).repeat(32)


BF16 = ml_dtypes.bfloat16


def bf(x):
    return np.asarray(x, np.float32).astype(BF16)


def f64(x):
    return np.asarray(x).astype(np.float64)


E2M1 = np.array([0.0, 0.5, 1.0, 1.5, 2.0, 3.0, 4.0, 6.0, -0.0, -0.5, -1.0, -1.5, -2.0, -3.0, -4.0, -6.0])


def pack_weight(w, fmt):
    k, n = w.shape
    w = f64(bf(w)).reshape(k // 32, 32, n)
    amax = np.abs(w).max(1)
    if fmt == "e4m3":
        byte = np.frexp(amax)[1] - 1 + 127 - 7
    else:
        mant, ex = np.frexp(amax / 6.0)
        byte = np.where(mant > 0.5, ex, ex - 1) + 127
    byte = np.clip(np.where(amax > 0, byte, 1), 1, 254)
    scaled = (w * np.exp2(127.0 - byte)[:, None, :]).reshape(k, n).astype(np.float32)
    by_word = np.ascontiguousarray(scaled.reshape(k // 512, 128, 4, n).transpose(0, 1, 3, 2))
    if fmt == "e4m3":
        words = by_word.astype(ml_dtypes.float8_e4m3fn).view(np.uint8)
    else:
        c = by_word.astype(ml_dtypes.float4_e2m1fn).view(np.uint8) & 0xF
        words = c[..., 0::2] | (c[..., 1::2] << 4)
    return np.ascontiguousarray(words), np.ascontiguousarray(byte.astype(np.uint8).reshape(k // 512, 16, n))


def unpack_weight(words, scales, fmt):
    g, p, n, _ = words.shape
    if fmt == "e4m3":
        vals = np.ascontiguousarray(words).view(ml_dtypes.float8_e4m3fn).astype(np.float64)
    else:
        nib = np.empty((g, p, n, 4), np.uint8)
        nib[..., 0::2] = words & 0xF
        nib[..., 1::2] = words >> 4
        vals = E2M1[nib]
    vals = vals * np.repeat(np.exp2(scales.astype(np.float64) - 127.0), 8, axis=1)[..., None]
    return vals.transpose(0, 1, 3, 2).reshape(g * 512, n)
def pack4(w):
    words, scales = pack_weight(w, "e2m1")
    return words.reshape(words.shape[0], 128, -1), scales


def unpack4(words, scales):
    return unpack_weight(words.reshape(words.shape[0], 128, -1, 2), scales, "e2m1")


B, T, E, H, DK, C = 1, 1024, 1024, 4, 256, 512
DV = 2 * DK
F = H * DV
EPS = 1e-5


def draw0():
    s, t = mx_kscale(E), mx_kscale(F)
    o = np.random.standard_normal((B, T, H, DV)) * 5.0 * np.exp(0.5 * np.random.standard_normal((B, T, H, 1)))
    x = bf(np.random.standard_normal((B, T, E)) * s)
    Wg_words, Wg_scales = pack4(np.random.standard_normal((E, F)) / np.sqrt(E) / s[:, None] * t)
    gn_weight = bf(1.0 + 0.1 * np.random.standard_normal(DV))
    Wo_words, Wo_scales = pack4(np.random.standard_normal((F, E)) / np.sqrt(F) / t[:, None])
    return {"o_ret": bf(o),
            "x": x,
            "Wg_words": Wg_words,
            "Wg_scales": Wg_scales,
            "gn_weight": gn_weight,
            "Wo_words": Wo_words,
            "Wo_scales": Wo_scales}


def core(o_ret, x, Wg_words, Wg_scales, gn_weight, Wo_words, Wo_scales):
    o = f64(o_ret)
    rms = np.sqrt(np.mean(o * o, axis=-1, keepdims=True) + EPS)
    o = o / rms * f64(gn_weight)
    g = mxq(f64(x), 2, "e4m3") @ unpack4(Wg_words, Wg_scales)
    h = o.reshape(B, T, F) * g
    return mxq(h, 2, "e4m3") @ unpack4(Wo_words, Wo_scales)


def e4m3fn_bytes(y):
    return np.clip(np.asarray(y, np.float64), -448.0, 448.0).astype(np.float32).astype(ml_dtypes.float8_e4m3fn).view(np.uint8)


def e4m3fn_values(b):
    return np.asarray(b, np.uint8).view(ml_dtypes.float8_e4m3fn).astype(np.float64)


def setup_inputs():
    d = draw0()
    x0 = np.asarray(d['x']).astype(np.float64)
    s = (np.max(np.abs(x0), axis=(0, 1), keepdims=True) / 448.0).astype(np.float32)
    out = {}
    for k, v in d.items():
        if k == 'x':
            out['x_bytes'] = e4m3fn_bytes(x0 / s.astype(np.float64))
            out['x_scale'] = s
        else:
            out[k] = v
    return out


def reference(o_ret, x_bytes, x_scale, Wg_words, Wg_scales, gn_weight, Wo_words, Wo_scales):
    return core(o_ret, e4m3fn_values(x_bytes) * x_scale.astype(np.float64), Wg_words, Wg_scales, gn_weight, Wo_words, Wo_scales)

@@ -1,0 +1,379 @@
+from contextlib import ExitStack
+
+import concourse.mybir as mybir
+from concourse.masks import make_identity
+
+F32 = mybir.dt.float32
+BF16 = mybir.dt.bfloat16
+I32 = mybir.dt.int32
+U32 = mybir.dt.uint32
+U8 = mybir.dt.uint8
+E4M3 = mybir.dt.float8_e4m3fn
+FP8X4 = mybir.dt.float8_e4m3fn_x4
+FP4X4 = mybir.dt.float4_e2m1fn_x4
+ACT = mybir.ActivationFunctionType
+ALU = mybir.AluOpType
+
+T, E, H, DV = 1024, 1024, 4, 512
+F = H * DV
+P = 128
+NT = T // P
+GX = E // 512
+GH = F // 512
+EPS = 1e-5
+GCOLS = 256
+NVS = [1,1,1,1,1,1,1,1]
+GM1 = 4
+QX = 0
+LA = 3
+SPOS = 9
+RPOS = 9
+CV = (0,)
+CH = (1,)
+SE = 1
+N1S = 1
+GHS = 1
+GH1 = 1
+FLOPS = 2 * T * E * F * 2
+BYTES = T * F * 2 + T * E + E * 4 + 2 * (E * F // 2 + E * F // 32) + DV * 2 + T * E * 4
+
+
+def tile_multiscaleretention_pc_w4_kernel(
+    tc, o_ret, x_bytes, x_scale, Wg_words, Wg_scales, gn_weight, Wo_words, Wo_scales, out
+):
+    nc = tc.nc
+    o_view = o_ret.rearrange("b (p i) h d -> i p (b h d)", i=NT)
+    x_view = x_bytes.rearrange("b (p i) e -> p (b i) e", i=NT)
+    out_view = out.rearrange("b (p i) e -> i p (b e)", i=NT)
+
+    with ExitStack() as ctx:
+        const = ctx.enter_context(tc.tile_pool(name="const", bufs=1))
+        xpool = ctx.enter_context(tc.tile_pool(name="xpool", bufs=6))
+        hpool = ctx.enter_context(tc.tile_pool(name="hpool", bufs=2))
+        opool = ctx.enter_context(tc.tile_pool(name="opool", bufs=3))
+        psum = ctx.enter_context(tc.psum_pool(name="psum", bufs=7))
+        wpsum = ctx.enter_context(tc.psum_pool(name="wpsum", bufs=1))
+
+        wg_sc = const.tile([P, GX, F], U8, name="wg_sc", align_bytes=64)
+        wo_sc = const.tile([P, GH, E], U8, name="wo_sc", align_bytes=64)
+        nc.vector.memset(wg_sc[:].rearrange("p g n -> p (g n)").bitcast(I32), 0)
+        ident = const.tile([P, P], F32, name="ident")
+        make_identity(nc, ident[:])
+        nc.vector.memset(wo_sc[:].rearrange("p g n -> p (g n)").bitcast(I32), 0)
+
+        ctx.enter_context(tc.manual_schedule())
+
+        x_cuts = [(0, 1), (1, 4), (4, 8)]
+        x_tiles = [
+            const.tile([P, b - a, E], U8, name="xbytes%d" % a) for a, b in x_cuts
+        ]
+        o_tiles = [const.tile([P, F], BF16, name="o%d" % i) for i in range(NT)]
+        wg = [const.tile([P, GX, F], U8, name="wg%d" % k, align_bytes=64) for k in range(2)]
+        wo = [const.tile([P, 2, 2 * E], U8, name="wo%d" % k, align_bytes=64) for k in range(2)]
+        s4 = const.tile([P, GX, 4], F32, name="s4")
+        gnw = const.tile([P, DV], BF16, name="gnw")
+        w4 = const.tile([P, 4], BF16, name="w4")
+        identb = const.tile([P, P], BF16, name="identb")
+        nc.vector.tensor_copy(out=identb[:], in_=ident[:])
+
+        def load_x(k):
+            a, b = x_cuts[k]
+            nc.sync.dma_start(out=x_tiles[k][:], in_=x_view[:, a:b, :])
+
+        def load_scales(sc, hbm):
+            for r in range(4):
+                nc.sync.dma_start(
+                    out=sc[r:P:32, :, :].rearrange("q g n -> q g n").bitcast(I32),
+                    in_=hbm[:, r:16:4, :].rearrange("g q n -> q g n").bitcast(I32),
+                )
+
+        def load_o(i):
+            nc.sync.dma_start(out=o_tiles[i][:], in_=o_view[i])
+
+        wg_v = Wg_words.rearrange("g p n -> p g n")
+        wo_v = Wo_words.rearrange("g p n -> p g n")
+        wg_v = Wg_words.rearrange("g p n -> p g n")
+        wo_v = Wo_words.rearrange("g p n -> p g n")
+        load_x(0)
+        nc.sync.dma_start(out=s4[:], in_=x_scale.rearrange("a b (g p t) -> p (a b g) t", p=P, t=4))
+        nc.sync.dma_start(out=w4[:], in_=gn_weight.rearrange("(p t) -> p t", t=4))
+        load_x(1)
+        load_scales(wg_sc, Wg_scales)
+        nc.sync.dma_start(out=wg[0][:], in_=wg_v[:, :, 0:F])
+        load_o(0)
+        nc.sync.dma_start(out=wg[1][:], in_=wg_v[:, :, F : 2 * F])
+        load_o(1)
+        load_x(2)
+        load_o(2)
+        load_scales(wo_sc, Wo_scales)
+        nc.sync.dma_start(out=wo[0][:], in_=wo_v[:, 0:2, :])
+        nc.sync.dma_start(out=wo[1][:], in_=wo_v[:, 2:4, :])
+        load_o(3)
+        load_o(4)
+        load_o(5)
+        load_o(6)
+        load_o(7)
+
+        xb, xs, xc, xsc = {}, {}, {}, {}
+        ss, rr, ow, hb, hs, hc, hsc = {}, {}, {}, {}, {}, {}, {}
+
+        def bank(name):
+            return psum.tile([P, 512], F32, name=name, tag="bank")
+
+        def x_src(i):
+            for k, (a, b) in enumerate(x_cuts):
+                if a <= i < b:
+                    return x_tiles[k][:, i - a, :]
+
+        def cast_x(i):
+            xb[i] = xpool.tile([P, E], BF16, name="xb", tag="xb", align_bytes=64)
+            src = x_src(i)
+            nc.scalar.copy(out=xb[i][:, 0:512], in_=src[:, 0:512].bitcast(E4M3))
+            if i not in CV:
+                nc.scalar.copy(out=xb[i][:, 512:1024], in_=src[:, 512:1024].bitcast(E4M3))
+            else:
+                nc.vector.tensor_copy(out=xb[i][:, 512:1024], in_=src[:, 512:1024].bitcast(E4M3))
+
+        def transpose_x(i):
+            b = bank("xt")
+            words = xb[i][:].bitcast(F32)
+            for g in range(GX):
+                for u in range(2):
+                    j = 2 * u + g
+                    nc.tensor.transpose(
+                        b[:, P * j : P * (j + 1)], words[:, 256 * g + u : 256 * (g + 1) : 2], ident[:]
+                    )
+            return b
+
+        def scale_x(i, b, passes):
+            if passes[0] == 0:
+                xs[i] = xpool.tile([P, GX, P, 4], BF16, name="xs", tag="xs", align_bytes=64)
+            g0, g1 = passes[0], passes[-1] + 1
+            src = b[:].bitcast(BF16).rearrange("p (u g n e) -> p g n u e", u=2, g=GX, e=2)
+            nc.vector.tensor_tensor(
+                out=xs[i][:, g0:g1].rearrange("p g n (u e) -> p g n u e", u=2),
+                in0=src[:, g0:g1],
+                in1=s4[:, g0:g1, :]
+                .rearrange("p g (u e) -> p g u e", u=2)
+                .unsqueeze(2)
+                .to_broadcast([P, g1 - g0, P, 2, 2]),
+                op=ALU.mult,
+            )
+
+        def quant_x(i, passes):
+            if passes[0] == 0:
+                xc[i] = xpool.tile([P, GX * P], U32, name="xc", tag="xc", align_bytes=64)
+                xsc[i] = xpool.tile([P, GX * P], U8, name="xsc", tag="xsc", align_bytes=64)
+            w = slice(P * passes[0], P * (passes[-1] + 1))
+            nc.vector.quantize_mx(
+                out=xc[i][:, w].bitcast(FP8X4),
+                scales=xsc[i][:, w],
+                in_=xs[i][:, passes[0] : passes[-1] + 1].rearrange("p g n t -> p (g n t)"),
+            )
+
+        def stats(i):
+            ss[i] = hpool.tile([P, H], F32, name="ss", tag="ss")
+            for h in range(H):
+                src = o_tiles[i][:, DV * h : DV * (h + 1)]
+                junk = hpool.tile([P, DV], BF16, name="junk", tag="junk")
+                nc.scalar.activation(out=junk[:], in_=src, func=ACT.Square, accum_out=ss[i][:, h : h + 1])
+            rr[i] = hpool.tile([P, H], F32, name="rr", tag="rr")
+            nc.scalar.activation(
+                out=rr[i][:], in_=ss[i][:], func=ACT.Abs_reciprocal_sqrt, scale=1.0 / DV, bias=EPS
+            )
+
+        def recip(i):
+            pass
+
+        wb = wpsum.tile([P, DV], BF16, name="wb")
+
+        def spread_w():
+            for t in range(4):
+                nc.tensor.transpose(
+                    wb[:, P * t : P * (t + 1)], w4[:, t : t + 1].to_broadcast([P, P]), identb[:]
+                )
+            nc.scalar.copy(
+                out=gnw[:].rearrange("p (n t) -> p n t", t=4),
+                in_=wb[:].rearrange("p (t n) -> p n t", t=4),
+            )
+
+        def alloc_ow(i):
+            if i not in ow:
+                ow[i] = opool.tile([P, F], F32, name="ow", tag="ow")
+
+        def weigh_o_v(i, n_vector):
+            alloc_ow(i)
+            for h in range(n_vector):
+                cols = slice(DV * h, DV * (h + 1))
+                nc.vector.tensor_tensor(
+                    out=ow[i][:, cols].rearrange("p (n t) -> p n t", t=4),
+                    in0=o_tiles[i][:, cols].rearrange("p (n t) -> p n t", t=4),
+                    in1=wb[:].rearrange("p (t n) -> p n t", t=4),
+                    op=ALU.mult,
+                )
+
+        def weigh_o_g(i, n_vector, heads):
+            alloc_ow(i)
+            for h in range(n_vector, H, heads):
+                n = min(heads, H - h)
+                cols = slice(DV * h, DV * (h + n))
+                nc.gpsimd.tensor_tensor(
+                    out=ow[i][:, cols],
+                    in0=o_tiles[i][:, cols],
+                    in1=gnw[:],
+                    op=ALU.mult,
+                )
+
+        def after(tile):
+            token = hpool.tile([P, 1], U32, name="token", tag="token")
+            nc.gpsimd.tensor_copy(out=token[:], in_=tile[:, 0:1])
+
+        gb = {}
+
+        def gate_mm(i, order):
+            for c, g in order:
+                if g == 0:
+                    gb[i, c] = bank("g")
+                nc.tensor.matmul_mx(
+                    out=gb[i, c][:],
+                    lhsT=xc[i][:, P * g : P * (g + 1)].bitcast(FP8X4),
+                    lhsT_scale=xsc[i][:, P * g : P * (g + 1)],
+                    rhs=wg[c // 2][:, g, 1024 * (c % 2) : 1024 * (c % 2) + 1024].bitcast(FP4X4),
+                    rhs_scale=wg_sc[:, g, 512 * c : 512 * (c + 1)],
+                    start=(g == 0),
+                    stop=(g == GX - 1),
+                )
+
+        def gate_mul(i, c):
+            if c == 0:
+                hb[i] = hpool.tile([P, GH, 2, 256], BF16, name="hb", tag="hb", align_bytes=64)
+            gv = gb[i, c][:].rearrange("p (n u e) -> p u n e", u=2, e=2)
+            wv = ow[i][:, 512 * c : 512 * (c + 1)].rearrange("p (n u e) -> p u n e", u=2, e=2)
+            for u in range(2):
+                nc.vector.scalar_tensor_tensor(
+                    out=hb[i][:, c, u].rearrange("p (n e) -> p n e", e=2),
+                    in0=gv[:, u],
+                    scalar=rr[i][:, c : c + 1],
+                    in1=wv[:, u],
+                    op0=ALU.mult,
+                    op1=ALU.mult,
+                )
+
+        def transpose_h(i):
+            hs[i] = hpool.tile([P, GH, P, 4], BF16, name="hs", tag="hs", align_bytes=64)
+            words = hb[i][:].rearrange("p g u n -> p (g u n)").bitcast(F32)
+            dst = hs[i][:].rearrange("p g n t -> p (g n t)").bitcast(F32)
+            for half in range(2):
+                b = bank("ht")
+                for j in range(4):
+                    k = 4 * half + j
+                    nc.tensor.transpose(b[:, P * j : P * (j + 1)], words[:, P * k : P * (k + 1)], ident[:])
+                nc.scalar.copy(
+                    out=dst[:, 512 * half : 512 * (half + 1)].rearrange("p (g n u) -> p g n u", g=2, u=2),
+                    in_=b[:].rearrange("p (g u n) -> p g n u", g=2, u=2),
+                )
+
+        def quant_h(i):
+            hc[i] = hpool.tile([P, GH * P], U32, name="hc", tag="hc", align_bytes=64)
+            hsc[i] = hpool.tile([P, GH * P], U8, name="hsc", tag="hsc", align_bytes=64)
+            nc.vector.quantize_mx(
+                out=hc[i][:].bitcast(FP8X4),
+                scales=hsc[i][:],
+                in_=hs[i][:].rearrange("p g n t -> p (g n t)"),
+            )
+
+        acc = {}
+
+        def project_mm(i, n):
+            acc[i, n] = bank("acc")
+            for g in range(GH):
+                nc.tensor.matmul_mx(
+                    out=acc[i, n][:],
+                    lhsT=hc[i][:, P * g : P * (g + 1)].bitcast(FP8X4),
+                    lhsT_scale=hsc[i][:, P * g : P * (g + 1)],
+                    rhs=wo[g // 2][:, g % 2, E * n : E * (n + 1)].bitcast(FP4X4),
+                    rhs_scale=wo_sc[:, g, 512 * n : 512 * (n + 1)],
+                    start=(g == 0),
+                    stop=(g == GH - 1),
+                )
+
+        def store(i, n):
+            b = acc[i, n]
+            res = opool.tile([P, 512], F32, name="res%d" % n, tag="res%d" % n)
+            if n == 0 or (N1S and i < NT - 1):
+                nc.scalar.copy(out=res[:], in_=b[:])
+            elif i == NT - 1:
+                nc.scalar.copy(out=res[:, 0:256], in_=b[:, 0:256])
+                nc.vector.tensor_copy(out=res[:, 256:512], in_=b[:, 256:512])
+            else:
+                nc.vector.tensor_copy(out=res[:], in_=b[:])
+            nc.sync.dma_start(out=out_view[i][:, 512 * n : 512 * (n + 1)], in_=res[:])
+
+        by_bank = [(c, g) for c in range(4) for g in range(GX)]
+        by_pass = [(c, g) for g in range(GX) for c in range(4)]
+
+        cast_x(0)
+        b = transpose_x(0)
+        for g in range(GX):
+            scale_x(0, b, [g])
+            quant_x(0, [g])
+        spread_w()
+        cast_x(1)
+        b = transpose_x(1)
+        scale_x(1, b, [0, 1])
+        quant_x(1, [0, 1])
+        gate_mm(0, by_bank[:4])
+        cast_x(2)
+        b = transpose_x(2)
+        scale_x(2, b, [0, 1])
+        quant_x(2, [0, 1])
+        gate_mm(0, by_bank[4:])
+        stats(0)
+        weigh_o_v(0, NVS[0])
+        weigh_o_g(0, NVS[0], 1)
+        recip(0)
+        gate_mm(1, by_bank[:GM1])
+        for c in range(4):
+            gate_mul(0, c)
+        stats(1)
+        weigh_o_v(1, NVS[1])
+        weigh_o_g(1, NVS[1], GH1)
+        cast_x(3)
+        recip(1)
+        weigh_o_g(2, NVS[2], GH1)
+        for k in range(0, NT + 1):
+            if 0 <= k - 2 < NT:
+                store(k - 2, 1)
+            if k + 1 < NT:
+                gate_mm(k + 1, by_bank[GM1:] if k == 0 else by_bank)
+                for c in range(4):
+                    gate_mul(k + 1, c)
+            if k + 2 < NT:
+                weigh_o_v(k + 2, NVS[k + 2])
+            if 0 <= k < NT and k < SE:
+                transpose_h(k)
+            if k + 2 < NT:
+                stats(k + 2)
+            if 0 <= k < NT and k >= SE:
+                transpose_h(k)
+            if k + LA < NT:
+                bx = transpose_x(k + LA)
+                scale_x(k + LA, bx, [0, 1])
+                if QX:
+                    quant_x(k + LA, [0, 1])
+            if 0 <= k < NT:
+                quant_h(k)
+            if k + LA < NT and not QX:
+                quant_x(k + LA, [0, 1])
+            if k + 3 < NT:
+                after(xc[k + 3])
+                weigh_o_g(k + 3, NVS[k + 3], GHS)
+            if k + LA + 1 < NT:
+                cast_x(k + LA + 1)
+            if k + 2 < NT:
+                recip(k + 2)
+            if 0 <= k - 1 < NT:
+                project_mm(k - 1, 0)
+                store(k - 1, 0)
+                project_mm(k - 1, 1)
+        store(NT - 1, 1)

@@ -21,19 +21,6 @@ NT = T // P
 GX = E // 512
 GH = F // 512
 EPS = 1e-5
-GCOLS = 256
-NVS = [1,1,1,1,1,1,1,1]
-GM1 = 4
-QX = 0
-LA = 3
-SPOS = 9
-RPOS = 9
-CV = (0,)
-CH = (1,)
-SE = 1
-N1S = 1
-GHS = 1
-GH1 = 1
 FLOPS = 2 * T * E * F * 2
 BYTES = T * F * 2 + T * E + E * 4 + 2 * (E * F // 2 + E * F // 32) + DV * 2 + T * E * 4
 
@@ -45,335 +32,316 @@ def tile_multiscaleretention_pc_w4_kernel(
     o_view = o_ret.rearrange("b (p i) h d -> i p (b h d)", i=NT)
     x_view = x_bytes.rearrange("b (p i) e -> p (b i) e", i=NT)
     out_view = out.rearrange("b (p i) e -> i p (b e)", i=NT)
+    wg_view = Wg_words.rearrange("g p n -> p g n")
+    wo_view = Wo_words.rearrange("g p n -> p g n")
 
     with ExitStack() as ctx:
         const = ctx.enter_context(tc.tile_pool(name="const", bufs=1))
-        xpool = ctx.enter_context(tc.tile_pool(name="xpool", bufs=6))
-        hpool = ctx.enter_context(tc.tile_pool(name="hpool", bufs=2))
-        opool = ctx.enter_context(tc.tile_pool(name="opool", bufs=3))
-        psum = ctx.enter_context(tc.psum_pool(name="psum", bufs=7))
-        wpsum = ctx.enter_context(tc.psum_pool(name="wpsum", bufs=1))
+        work = ctx.enter_context(tc.tile_pool(name="work", bufs=2))
+        psum = ctx.enter_context(tc.psum_pool(name="psum", bufs=1))
+        ctx.enter_context(tc.manual_schedule())
+
+        def bank(tag):
+            return psum.tile([P, 512], F32, name=tag, tag=tag)
 
         wg_sc = const.tile([P, GX, F], U8, name="wg_sc", align_bytes=64)
         wo_sc = const.tile([P, GH, E], U8, name="wo_sc", align_bytes=64)
-        nc.vector.memset(wg_sc[:].rearrange("p g n -> p (g n)").bitcast(I32), 0)
         ident = const.tile([P, P], F32, name="ident")
-        make_identity(nc, ident[:])
-        nc.vector.memset(wo_sc[:].rearrange("p g n -> p (g n)").bitcast(I32), 0)
-
-        ctx.enter_context(tc.manual_schedule())
-
-        x_cuts = [(0, 1), (1, 4), (4, 8)]
-        x_tiles = [
-            const.tile([P, b - a, E], U8, name="xbytes%d" % a) for a, b in x_cuts
-        ]
-        o_tiles = [const.tile([P, F], BF16, name="o%d" % i) for i in range(NT)]
-        wg = [const.tile([P, GX, F], U8, name="wg%d" % k, align_bytes=64) for k in range(2)]
-        wo = [const.tile([P, 2, 2 * E], U8, name="wo%d" % k, align_bytes=64) for k in range(2)]
-        s4 = const.tile([P, GX, 4], F32, name="s4")
+        w_row = const.tile([P, DV], BF16, name="w_row")
+        ones = const.tile([P, P], BF16, name="ones")
         gnw = const.tile([P, DV], BF16, name="gnw")
-        w4 = const.tile([P, 4], BF16, name="w4")
-        identb = const.tile([P, P], BF16, name="identb")
-        nc.vector.tensor_copy(out=identb[:], in_=ident[:])
+        s4 = const.tile([P, GX, 4], F32, name="s4")
+        x_cuts = [(0, 1), (1, 2), (2, 4), (4, 8)]
+        x_tiles = [const.tile([P, b - a, E], U8, name="xbytes%d" % a) for a, b in x_cuts]
+        o_first = [const.tile([P, F // 2], BF16, name="ofirst%d" % j) for j in range(2)]
+        o_tiles = [None] + [const.tile([P, F], BF16, name="o%d" % i) for i in range(1, NT)]
+        wg = [const.tile([P, GX, 2 * DV], U8, name="wg%d" % h, align_bytes=64) for h in range(H)]
+        wo = [const.tile([P, 2, 2 * E], U8, name="wo%d" % k, align_bytes=64) for k in range(2)]
+        shared = [const.tile([P, (H - 1) * DV], F32, name="shared%d" % j, align_bytes=64) for j in range(2)]
+
+        nc.vector.memset(wg_sc[:].rearrange("p g n -> p (g n)").bitcast(I32), 0)
+        nc.vector.memset(w_row[:], 0.0)
+        make_identity(nc, ident[:])
+        nc.vector.memset(ones[:], 1.0)
+        nc.vector.memset(wo_sc[:].rearrange("p g n -> p (g n)").bitcast(I32), 0)
 
         def load_x(k):
             a, b = x_cuts[k]
             nc.sync.dma_start(out=x_tiles[k][:], in_=x_view[:, a:b, :])
 
-        def load_scales(sc, hbm):
+        def load_scales(queue, sc, hbm):
             for r in range(4):
-                nc.sync.dma_start(
-                    out=sc[r:P:32, :, :].rearrange("q g n -> q g n").bitcast(I32),
+                queue.dma_start(
+                    out=sc[r:P:32, :, :].bitcast(I32),
                     in_=hbm[:, r:16:4, :].rearrange("g q n -> q g n").bitcast(I32),
                 )
+
+        def load_wg(h):
+            nc.sync.dma_start(out=wg[h][:], in_=wg_view[:, :, 2 * DV * h : 2 * DV * (h + 1)])
 
         def load_o(i):
             nc.sync.dma_start(out=o_tiles[i][:], in_=o_view[i])
 
-        wg_v = Wg_words.rearrange("g p n -> p g n")
-        wo_v = Wo_words.rearrange("g p n -> p g n")
-        wg_v = Wg_words.rearrange("g p n -> p g n")
-        wo_v = Wo_words.rearrange("g p n -> p g n")
+        def load_o_first(j):
+            nc.sync.dma_start(out=o_first[j][:], in_=o_view[0][:, F // 2 * j : F // 2 * (j + 1)])
+
         load_x(0)
         nc.sync.dma_start(out=s4[:], in_=x_scale.rearrange("a b (g p t) -> p (a b g) t", p=P, t=4))
-        nc.sync.dma_start(out=w4[:], in_=gn_weight.rearrange("(p t) -> p t", t=4))
+        load_wg(0)
+        load_scales(nc.sync, wg_sc, Wg_scales)
+        nc.sync.dma_start(out=w_row[0:1, :], in_=gn_weight.rearrange("(a n) -> a n", a=1))
         load_x(1)
-        load_scales(wg_sc, Wg_scales)
-        nc.sync.dma_start(out=wg[0][:], in_=wg_v[:, :, 0:F])
-        load_o(0)
-        nc.sync.dma_start(out=wg[1][:], in_=wg_v[:, :, F : 2 * F])
-        load_o(1)
+        load_o_first(0)
+        load_wg(1)
+        load_o_first(1)
+        load_wg(2)
+        load_wg(3)
         load_x(2)
+        load_o(1)
+        load_scales(nc.sync, wo_sc, Wo_scales)
+        nc.sync.dma_start(out=wo[0][:], in_=wo_view[:, 0:2, :])
+        nc.sync.dma_start(out=wo[1][:], in_=wo_view[:, 2:4, :])
         load_o(2)
-        load_scales(wo_sc, Wo_scales)
-        nc.sync.dma_start(out=wo[0][:], in_=wo_v[:, 0:2, :])
-        nc.sync.dma_start(out=wo[1][:], in_=wo_v[:, 2:4, :])
-        load_o(3)
-        load_o(4)
-        load_o(5)
-        load_o(6)
-        load_o(7)
+        load_x(3)
+        for i in range(3, NT):
+            load_o(i)
 
-        xb, xs, xc, xsc = {}, {}, {}, {}
-        ss, rr, ow, hb, hs, hc, hsc = {}, {}, {}, {}, {}, {}, {}
+        xb, xt, xc, xsc = {}, {}, {}, {}
+        ss, rr, ow0, hb, ht, hs, hc, hsc, gb, acc = {}, {}, {}, {}, {}, {}, {}, {}, {}, {}
 
-        def bank(name):
-            return psum.tile([P, 512], F32, name=name, tag="bank")
+        def o_cols(i, h, n=1):
+            if i == 0:
+                return o_first[h // 2][:, DV * (h % 2) : DV * (h % 2 + n)]
+            return o_tiles[i][:, DV * h : DV * (h + n)]
 
-        def x_src(i):
-            for k, (a, b) in enumerate(x_cuts):
-                if a <= i < b:
-                    return x_tiles[k][:, i - a, :]
-
-        def cast_x(i):
-            xb[i] = xpool.tile([P, E], BF16, name="xb", tag="xb", align_bytes=64)
-            src = x_src(i)
-            nc.scalar.copy(out=xb[i][:, 0:512], in_=src[:, 0:512].bitcast(E4M3))
-            if i not in CV:
-                nc.scalar.copy(out=xb[i][:, 512:1024], in_=src[:, 512:1024].bitcast(E4M3))
+        def widen_x(i, g, on_vector):
+            k = max(k for k, (a, b) in enumerate(x_cuts) if a <= i)
+            src = x_tiles[k][:, i - x_cuts[k][0], 512 * g : 512 * (g + 1)].bitcast(E4M3)
+            xb[i, g] = work.tile([P, 512], BF16, name="xb%d" % g, tag="xb%d" % g)
+            if on_vector:
+                nc.vector.tensor_copy(out=xb[i, g][:], in_=src)
             else:
-                nc.vector.tensor_copy(out=xb[i][:, 512:1024], in_=src[:, 512:1024].bitcast(E4M3))
+                nc.scalar.copy(out=xb[i, g][:], in_=src)
 
-        def transpose_x(i):
-            b = bank("xt")
-            words = xb[i][:].bitcast(F32)
-            for g in range(GX):
+        def transpose_x(i, passes, tag):
+            b = bank(tag)
+            for j, g in enumerate(passes):
+                xt[i, g] = b
+                words = xb[i, g][:].bitcast(F32)
                 for u in range(2):
-                    j = 2 * u + g
-                    nc.tensor.transpose(
-                        b[:, P * j : P * (j + 1)], words[:, 256 * g + u : 256 * (g + 1) : 2], ident[:]
-                    )
-            return b
+                    col = P * (len(passes) * u + j)
+                    nc.tensor.transpose(b[:, col : col + P], words[:, u:256:2], ident[:])
 
-        def scale_x(i, b, passes):
-            if passes[0] == 0:
-                xs[i] = xpool.tile([P, GX, P, 4], BF16, name="xs", tag="xs", align_bytes=64)
-            g0, g1 = passes[0], passes[-1] + 1
-            src = b[:].bitcast(BF16).rearrange("p (u g n e) -> p g n u e", u=2, g=GX, e=2)
+        def xs_view(i):
+            return shared[i % 2][:, 0 : E // 2].bitcast(BF16)
+
+        def scale_x(i, passes):
+            n = len(passes)
+            g0 = passes[0]
+            src = xt[i, g0][:, 0 : 256 * n].bitcast(BF16).rearrange("p (u g n e) -> p g n u e", u=2, g=n, e=2)
+            dst = xs_view(i)[:, 512 * g0 : 512 * (g0 + n)].rearrange("p (g n u e) -> p g n u e", g=n, u=2, e=2)
             nc.vector.tensor_tensor(
-                out=xs[i][:, g0:g1].rearrange("p g n (u e) -> p g n u e", u=2),
-                in0=src[:, g0:g1],
-                in1=s4[:, g0:g1, :]
+                out=dst,
+                in0=src,
+                in1=s4[:, g0 : g0 + n, :]
                 .rearrange("p g (u e) -> p g u e", u=2)
                 .unsqueeze(2)
-                .to_broadcast([P, g1 - g0, P, 2, 2]),
+                .to_broadcast([P, n, P, 2, 2]),
                 op=ALU.mult,
             )
 
         def quant_x(i, passes):
             if passes[0] == 0:
-                xc[i] = xpool.tile([P, GX * P], U32, name="xc", tag="xc", align_bytes=64)
-                xsc[i] = xpool.tile([P, GX * P], U8, name="xsc", tag="xsc", align_bytes=64)
+                xc[i] = work.tile([P, GX * P], U32, name="xc", tag="xc", align_bytes=64)
+                xsc[i] = work.tile([P, GX * P], U8, name="xsc", tag="xsc", align_bytes=64)
             w = slice(P * passes[0], P * (passes[-1] + 1))
             nc.vector.quantize_mx(
                 out=xc[i][:, w].bitcast(FP8X4),
                 scales=xsc[i][:, w],
-                in_=xs[i][:, passes[0] : passes[-1] + 1].rearrange("p g n t -> p (g n t)"),
+                in_=xs_view(i)[:, 4 * w.start : 4 * w.stop],
             )
 
-        def stats(i):
-            ss[i] = hpool.tile([P, H], F32, name="ss", tag="ss")
-            for h in range(H):
-                src = o_tiles[i][:, DV * h : DV * (h + 1)]
-                junk = hpool.tile([P, DV], BF16, name="junk", tag="junk")
-                nc.scalar.activation(out=junk[:], in_=src, func=ACT.Square, accum_out=ss[i][:, h : h + 1])
-            rr[i] = hpool.tile([P, H], F32, name="rr", tag="rr")
+        def squares(i, h):
+            if h == 0:
+                ss[i] = work.tile([P, H], F32, name="ss", tag="ss")
+                rr[i] = work.tile([P, H], F32, name="rr", tag="rr")
+            junk = work.tile([P, DV], BF16, name="junk", tag="junk")
+            nc.scalar.activation(out=junk[:], in_=o_cols(i, h), func=ACT.Square, accum_out=ss[i][:, h : h + 1])
+
+        def inv_rms(i, h0, h1):
             nc.scalar.activation(
-                out=rr[i][:], in_=ss[i][:], func=ACT.Abs_reciprocal_sqrt, scale=1.0 / DV, bias=EPS
+                out=rr[i][:, h0:h1], in_=ss[i][:, h0:h1], func=ACT.Abs_reciprocal_sqrt, scale=1.0 / DV, bias=EPS
             )
 
-        def recip(i):
-            pass
-
-        wb = wpsum.tile([P, DV], BF16, name="wb")
+        w_bank = bank("w")
 
         def spread_w():
-            for t in range(4):
-                nc.tensor.transpose(
-                    wb[:, P * t : P * (t + 1)], w4[:, t : t + 1].to_broadcast([P, P]), identb[:]
-                )
-            nc.scalar.copy(
-                out=gnw[:].rearrange("p (n t) -> p n t", t=4),
-                in_=wb[:].rearrange("p (t n) -> p n t", t=4),
+            nc.tensor.matmul(w_bank[:], lhsT=ones[:], rhs=w_row[:], start=True, stop=True)
+            nc.scalar.copy(out=gnw[:], in_=w_bank[:])
+
+        def ow_cols(i, h):
+            if h == 0:
+                return ow0[i][:]
+            return shared[i % 2][:, DV * (h - 1) : DV * h]
+
+        def weigh_vector(i, h):
+            if h == 0:
+                ow0[i] = work.tile([P, DV], F32, name="ow0", tag="ow0")
+            nc.vector.tensor_tensor(out=ow_cols(i, h), in0=o_cols(i, h), in1=w_bank[:], op=ALU.mult)
+
+        def weigh_gpsimd(i, h, n):
+            nc.gpsimd.tensor_tensor(
+                out=shared[i % 2][:, DV * (h - 1) : DV * (h - 1 + n)].rearrange("p (h d) -> p h d", h=n),
+                in0=o_cols(i, h, n).rearrange("p (h d) -> p h d", h=n),
+                in1=gnw[:].unsqueeze(1).to_broadcast([P, n, DV]),
+                op=ALU.mult,
             )
 
-        def alloc_ow(i):
-            if i not in ow:
-                ow[i] = opool.tile([P, F], F32, name="ow", tag="ow")
+        def gate_mm(i, h, g):
+            if g == 0:
+                gb[i, h] = bank("g%d" % h)
+            nc.tensor.matmul_mx(
+                out=gb[i, h][:],
+                lhsT=xc[i][:, P * g : P * (g + 1)].bitcast(FP8X4),
+                lhsT_scale=xsc[i][:, P * g : P * (g + 1)],
+                rhs=wg[h][:, g, :].bitcast(FP4X4),
+                rhs_scale=wg_sc[:, g, DV * h : DV * (h + 1)],
+                start=(g == 0),
+                stop=(g == GX - 1),
+            )
 
-        def weigh_o_v(i, n_vector):
-            alloc_ow(i)
-            for h in range(n_vector):
-                cols = slice(DV * h, DV * (h + 1))
-                nc.vector.tensor_tensor(
-                    out=ow[i][:, cols].rearrange("p (n t) -> p n t", t=4),
-                    in0=o_tiles[i][:, cols].rearrange("p (n t) -> p n t", t=4),
-                    in1=wb[:].rearrange("p (t n) -> p n t", t=4),
-                    op=ALU.mult,
-                )
-
-        def weigh_o_g(i, n_vector, heads):
-            alloc_ow(i)
-            for h in range(n_vector, H, heads):
-                n = min(heads, H - h)
-                cols = slice(DV * h, DV * (h + n))
-                nc.gpsimd.tensor_tensor(
-                    out=ow[i][:, cols],
-                    in0=o_tiles[i][:, cols],
-                    in1=gnw[:],
-                    op=ALU.mult,
-                )
-
-        def after(tile):
-            token = hpool.tile([P, 1], U32, name="token", tag="token")
-            nc.gpsimd.tensor_copy(out=token[:], in_=tile[:, 0:1])
-
-        gb = {}
-
-        def gate_mm(i, order):
-            for c, g in order:
-                if g == 0:
-                    gb[i, c] = bank("g")
-                nc.tensor.matmul_mx(
-                    out=gb[i, c][:],
-                    lhsT=xc[i][:, P * g : P * (g + 1)].bitcast(FP8X4),
-                    lhsT_scale=xsc[i][:, P * g : P * (g + 1)],
-                    rhs=wg[c // 2][:, g, 1024 * (c % 2) : 1024 * (c % 2) + 1024].bitcast(FP4X4),
-                    rhs_scale=wg_sc[:, g, 512 * c : 512 * (c + 1)],
-                    start=(g == 0),
-                    stop=(g == GX - 1),
-                )
-
-        def gate_mul(i, c):
-            if c == 0:
-                hb[i] = hpool.tile([P, GH, 2, 256], BF16, name="hb", tag="hb", align_bytes=64)
-            gv = gb[i, c][:].rearrange("p (n u e) -> p u n e", u=2, e=2)
-            wv = ow[i][:, 512 * c : 512 * (c + 1)].rearrange("p (n u e) -> p u n e", u=2, e=2)
+        def gate_mul(i, h):
+            hb[i, h] = work.tile([P, 2, 256], BF16, name="hb%d" % h, tag="hb%d" % h)
+            gv = gb[i, h][:].rearrange("p (n u e) -> p u n e", u=2, e=2)
+            wv = ow_cols(i, h).rearrange("p (n u e) -> p u n e", u=2, e=2)
             for u in range(2):
                 nc.vector.scalar_tensor_tensor(
-                    out=hb[i][:, c, u].rearrange("p (n e) -> p n e", e=2),
+                    out=hb[i, h][:, u].rearrange("p (n e) -> p n e", e=2),
                     in0=gv[:, u],
-                    scalar=rr[i][:, c : c + 1],
+                    scalar=rr[i][:, h : h + 1],
                     in1=wv[:, u],
                     op0=ALU.mult,
                     op1=ALU.mult,
                 )
 
-        def transpose_h(i):
-            hs[i] = hpool.tile([P, GH, P, 4], BF16, name="hs", tag="hs", align_bytes=64)
-            words = hb[i][:].rearrange("p g u n -> p (g u n)").bitcast(F32)
-            dst = hs[i][:].rearrange("p g n t -> p (g n t)").bitcast(F32)
-            for half in range(2):
-                b = bank("ht")
-                for j in range(4):
-                    k = 4 * half + j
-                    nc.tensor.transpose(b[:, P * j : P * (j + 1)], words[:, P * k : P * (k + 1)], ident[:])
-                nc.scalar.copy(
-                    out=dst[:, 512 * half : 512 * (half + 1)].rearrange("p (g n u) -> p g n u", g=2, u=2),
-                    in_=b[:].rearrange("p (g u n) -> p g n u", g=2, u=2),
-                )
+        def transpose_h(i, half, tag):
+            ht[i, half] = bank(tag)
+            for j in range(2):
+                for u in range(2):
+                    col = P * (2 * j + u)
+                    nc.tensor.transpose(
+                        ht[i, half][:, col : col + P], hb[i, 2 * half + j][:, u].bitcast(F32), ident[:]
+                    )
 
-        def quant_h(i):
-            hc[i] = hpool.tile([P, GH * P], U32, name="hc", tag="hc", align_bytes=64)
-            hsc[i] = hpool.tile([P, GH * P], U8, name="hsc", tag="hsc", align_bytes=64)
+        def gather_h(i, half, on_vector=False):
+            hs[i, half] = work.tile([P, 512], F32, name="hs%d" % half, tag="hs%d" % half, align_bytes=64)
+            dst = hs[i, half][:].rearrange("p (g n u) -> p g n u", g=2, u=2)
+            src = ht[i, half][:].rearrange("p (g u n) -> p g n u", g=2, u=2)
+            if on_vector:
+                nc.vector.tensor_copy(out=dst, in_=src)
+            else:
+                nc.scalar.copy(out=dst, in_=src)
+
+        def quant_h(i, half):
+            hc[i, half] = work.tile([P, 2 * P], U32, name="hc%d" % half, tag="hc%d" % half, align_bytes=64)
+            hsc[i, half] = work.tile([P, 2 * P], U8, name="hsc%d" % half, tag="hsc%d" % half, align_bytes=64)
             nc.vector.quantize_mx(
-                out=hc[i][:].bitcast(FP8X4),
-                scales=hsc[i][:],
-                in_=hs[i][:].rearrange("p g n t -> p (g n t)"),
+                out=hc[i, half][:].bitcast(FP8X4), scales=hsc[i, half][:], in_=hs[i, half][:].bitcast(BF16)
             )
 
-        acc = {}
-
-        def project_mm(i, n):
-            acc[i, n] = bank("acc")
-            for g in range(GH):
+        def project_mm(i, c0, c1, passes, tag):
+            if passes[0] == 0:
+                acc[i, c0] = bank(tag)
+            for g in passes:
+                w = slice(P * (g % 2), P * (g % 2 + 1))
                 nc.tensor.matmul_mx(
-                    out=acc[i, n][:],
-                    lhsT=hc[i][:, P * g : P * (g + 1)].bitcast(FP8X4),
-                    lhsT_scale=hsc[i][:, P * g : P * (g + 1)],
-                    rhs=wo[g // 2][:, g % 2, E * n : E * (n + 1)].bitcast(FP4X4),
-                    rhs_scale=wo_sc[:, g, 512 * n : 512 * (n + 1)],
+                    out=acc[i, c0][:, 0 : c1 - c0],
+                    lhsT=hc[i, g // 2][:, w].bitcast(FP8X4),
+                    lhsT_scale=hsc[i, g // 2][:, w],
+                    rhs=wo[g // 2][:, g % 2, 2 * c0 : 2 * c1].bitcast(FP4X4),
+                    rhs_scale=wo_sc[:, g, c0:c1],
                     start=(g == 0),
                     stop=(g == GH - 1),
                 )
 
-        def store(i, n):
-            b = acc[i, n]
-            res = opool.tile([P, 512], F32, name="res%d" % n, tag="res%d" % n)
-            if n == 0 or (N1S and i < NT - 1):
-                nc.scalar.copy(out=res[:], in_=b[:])
-            elif i == NT - 1:
-                nc.scalar.copy(out=res[:, 0:256], in_=b[:, 0:256])
-                nc.vector.tensor_copy(out=res[:, 256:512], in_=b[:, 256:512])
+        def store(i, c0, c1, on_vector=False):
+            res = work.tile([P, 512], F32, name="res", tag="res", bufs=4)
+            if on_vector:
+                nc.vector.tensor_copy(out=res[:, 0 : c1 - c0], in_=acc[i, c0][:, 0 : c1 - c0])
             else:
-                nc.vector.tensor_copy(out=res[:], in_=b[:])
-            nc.sync.dma_start(out=out_view[i][:, 512 * n : 512 * (n + 1)], in_=res[:])
+                nc.scalar.copy(out=res[:, 0 : c1 - c0], in_=acc[i, c0][:, 0 : c1 - c0])
+            nc.sync.dma_start(out=out_view[i][:, c0:c1], in_=res[:, 0 : c1 - c0])
 
-        by_bank = [(c, g) for c in range(4) for g in range(GX)]
-        by_pass = [(c, g) for g in range(GX) for c in range(4)]
+        both = [0, 1]
+        every = [0, 1, 2, 3]
 
-        cast_x(0)
-        b = transpose_x(0)
-        for g in range(GX):
-            scale_x(0, b, [g])
-            quant_x(0, [g])
+        widen_x(0, 0, True)
+        widen_x(0, 1, False)
+        transpose_x(0, [0], "x")
+        transpose_x(0, [1], "a0")
         spread_w()
-        cast_x(1)
-        b = transpose_x(1)
-        scale_x(1, b, [0, 1])
-        quant_x(1, [0, 1])
-        gate_mm(0, by_bank[:4])
-        cast_x(2)
-        b = transpose_x(2)
-        scale_x(2, b, [0, 1])
-        quant_x(2, [0, 1])
-        gate_mm(0, by_bank[4:])
-        stats(0)
-        weigh_o_v(0, NVS[0])
-        weigh_o_g(0, NVS[0], 1)
-        recip(0)
-        gate_mm(1, by_bank[:GM1])
-        for c in range(4):
-            gate_mul(0, c)
-        stats(1)
-        weigh_o_v(1, NVS[1])
-        weigh_o_g(1, NVS[1], GH1)
-        cast_x(3)
-        recip(1)
-        weigh_o_g(2, NVS[2], GH1)
-        for k in range(0, NT + 1):
-            if 0 <= k - 2 < NT:
-                store(k - 2, 1)
+        scale_x(0, [0])
+        scale_x(0, [1])
+        quant_x(0, [0])
+        quant_x(0, [1])
+        widen_x(1, 0, False)
+        widen_x(1, 1, False)
+        transpose_x(1, both, "x")
+        squares(0, 0)
+        squares(0, 1)
+        inv_rms(0, 0, 2)
+        squares(0, 2)
+        squares(0, 3)
+        inv_rms(0, 2, 4)
+        weigh_vector(0, 0)
+        for h in range(1, H):
+            weigh_gpsimd(0, h, 1)
+
+        for k in range(NT):
+            last = k == NT - 1
+            for h in range(H):
+                for g in range(GX):
+                    gate_mm(k, h, g)
             if k + 1 < NT:
-                gate_mm(k + 1, by_bank[GM1:] if k == 0 else by_bank)
-                for c in range(4):
-                    gate_mul(k + 1, c)
+                scale_x(k + 1, both)
+            if k > 0:
+                quant_h(k - 1, 0)
+                quant_h(k - 1, 1)
             if k + 2 < NT:
-                weigh_o_v(k + 2, NVS[k + 2])
-            if 0 <= k < NT and k < SE:
-                transpose_h(k)
+                widen_x(k + 2, 1, True)
+                widen_x(k + 2, 0, False)
+            if k + 1 < NT:
+                quant_x(k + 1, both)
+                weigh_gpsimd(k + 1, 1, H - 1)
+                for h in range(3):
+                    squares(k + 1, h)
+            for h in range(H):
+                gate_mul(k, h)
+            if k > 0:
+                project_mm(k - 1, 0, 512, every, "a0")
+                store(k - 1, 0, 512)
+            if k + 1 < NT:
+                weigh_vector(k + 1, 0)
+                squares(k + 1, 3)
+            if k > 0 and not last:
+                project_mm(k - 1, 512, 1024, every, "a1")
+                store(k - 1, 512, 1024)
+            if k + 1 < NT:
+                inv_rms(k + 1, 0, H)
             if k + 2 < NT:
-                stats(k + 2)
-            if 0 <= k < NT and k >= SE:
-                transpose_h(k)
-            if k + LA < NT:
-                bx = transpose_x(k + LA)
-                scale_x(k + LA, bx, [0, 1])
-                if QX:
-                    quant_x(k + LA, [0, 1])
-            if 0 <= k < NT:
-                quant_h(k)
-            if k + LA < NT and not QX:
-                quant_x(k + LA, [0, 1])
-            if k + 3 < NT:
-                after(xc[k + 3])
-                weigh_o_g(k + 3, NVS[k + 3], GHS)
-            if k + LA + 1 < NT:
-                cast_x(k + LA + 1)
-            if k + 2 < NT:
-                recip(k + 2)
-            if 0 <= k - 1 < NT:
-                project_mm(k - 1, 0)
-                store(k - 1, 0)
-                project_mm(k - 1, 1)
-        store(NT - 1, 1)
+                transpose_x(k + 2, both, "x")
+            for half in range(2):
+                transpose_h(k, half, "g%d" % (2 + half))
+                gather_h(k, half, on_vector=last and half == 1)
+
+        k = NT - 1
+        quant_h(k, 0)
+        quant_h(k, 1)
+        project_mm(k - 1, 512, 1024, every, "a1")
+        store(k - 1, 512, 1024)
+        chunks = [(0, 512, "a0"), (512, 768, "g0"), (768, 1024, "g1")]
+        for passes in ([0, 1], [2, 3]):
+            for c0, c1, tag in chunks:
+                project_mm(k, c0, c1, passes, tag)
+        for j, (c0, c1, tag) in enumerate(chunks):
+            store(k, c0, c1, on_vector=j == 1)

@@ -41,7 +41,11 @@ def tile_multiscaleretention_pc_w4_kernel(
         psum = ctx.enter_context(tc.psum_pool(name="psum", bufs=1))
         ctx.enter_context(tc.manual_schedule())
 
-        def bank(tag):
+        banks_used = []
+
+        def bank():
+            tag = "bank%d" % (len(banks_used) % 7)
+            banks_used.append(tag)
             return psum.tile([P, 512], F32, name=tag, tag=tag)
 
         wg_sc = const.tile([P, GX, F], U8, name="wg_sc", align_bytes=64)
@@ -51,17 +55,17 @@ def tile_multiscaleretention_pc_w4_kernel(
         ones = const.tile([P, P], BF16, name="ones")
         gnw = const.tile([P, DV], BF16, name="gnw")
         s4 = const.tile([P, GX, 4], F32, name="s4")
-        x_cuts = [(0, 1), (1, 2), (2, 4), (4, 8)]
+        x_cuts = [(0, 2), (2, 4), (4, 8)]
         x_tiles = [const.tile([P, b - a, E], U8, name="xbytes%d" % a) for a, b in x_cuts]
         o_first = [const.tile([P, F // 2], BF16, name="ofirst%d" % j) for j in range(2)]
         o_tiles = [None] + [const.tile([P, F], BF16, name="o%d" % i) for i in range(1, NT)]
-        wg = [const.tile([P, GX, 2 * DV], U8, name="wg%d" % h, align_bytes=64) for h in range(H)]
-        wo = [const.tile([P, 2, 2 * E], U8, name="wo%d" % k, align_bytes=64) for k in range(2)]
+        wg = [const.tile([P, GX, F], U8, name="wg%d" % j, align_bytes=64) for j in range(2)]
+        wo = [const.tile([P, GH, E], U8, name="wo%d" % k, align_bytes=64) for k in range(2)]
         shared = [const.tile([P, (H - 1) * DV], F32, name="shared%d" % j, align_bytes=64) for j in range(2)]
 
-        nc.vector.memset(wg_sc[:].rearrange("p g n -> p (g n)").bitcast(I32), 0)
-        nc.vector.memset(w_row[:], 0.0)
+        nc.gpsimd.memset(w_row[:].bitcast(F32), 0.0)
         make_identity(nc, ident[:])
+        nc.vector.memset(wg_sc[:].rearrange("p g n -> p (g n)").bitcast(I32), 0)
         nc.vector.memset(ones[:], 1.0)
         nc.vector.memset(wo_sc[:].rearrange("p g n -> p (g n)").bitcast(I32), 0)
 
@@ -76,8 +80,8 @@ def tile_multiscaleretention_pc_w4_kernel(
                     in_=hbm[:, r:16:4, :].rearrange("g q n -> q g n").bitcast(I32),
                 )
 
-        def load_wg(h):
-            nc.sync.dma_start(out=wg[h][:], in_=wg_view[:, :, 2 * DV * h : 2 * DV * (h + 1)])
+        def load_wg(j):
+            nc.sync.dma_start(out=wg[j][:], in_=wg_view[:, :, F * j : F * (j + 1)])
 
         def load_o(i):
             nc.sync.dma_start(out=o_tiles[i][:], in_=o_view[i])
@@ -87,22 +91,19 @@ def tile_multiscaleretention_pc_w4_kernel(
 
         load_x(0)
         nc.sync.dma_start(out=s4[:], in_=x_scale.rearrange("a b (g p t) -> p (a b g) t", p=P, t=4))
-        load_wg(0)
-        load_scales(nc.sync, wg_sc, Wg_scales)
         nc.sync.dma_start(out=w_row[0:1, :], in_=gn_weight.rearrange("(a n) -> a n", a=1))
-        load_x(1)
+        load_wg(0)
         load_o_first(0)
-        load_wg(1)
+        load_scales(nc.sync, wg_sc, Wg_scales)
         load_o_first(1)
-        load_wg(2)
-        load_wg(3)
-        load_x(2)
+        load_wg(1)
+        load_x(1)
         load_o(1)
-        load_scales(nc.sync, wo_sc, Wo_scales)
-        nc.sync.dma_start(out=wo[0][:], in_=wo_view[:, 0:2, :])
-        nc.sync.dma_start(out=wo[1][:], in_=wo_view[:, 2:4, :])
         load_o(2)
-        load_x(3)
+        load_scales(nc.sync, wo_sc, Wo_scales)
+        nc.sync.dma_start(out=wo[0][:], in_=wo_view[:, :, 0:E])
+        nc.sync.dma_start(out=wo[1][:], in_=wo_view[:, :, E : 2 * E])
+        load_x(2)
         for i in range(3, NT):
             load_o(i)
 
@@ -123,8 +124,8 @@ def tile_multiscaleretention_pc_w4_kernel(
             else:
                 nc.scalar.copy(out=xb[i, g][:], in_=src)
 
-        def transpose_x(i, passes, tag):
-            b = bank(tag)
+        def transpose_x(i, passes):
+            b = bank()
             for j, g in enumerate(passes):
                 xt[i, g] = b
                 words = xb[i, g][:].bitcast(F32)
@@ -173,7 +174,7 @@ def tile_multiscaleretention_pc_w4_kernel(
                 out=rr[i][:, h0:h1], in_=ss[i][:, h0:h1], func=ACT.Abs_reciprocal_sqrt, scale=1.0 / DV, bias=EPS
             )
 
-        w_bank = bank("w")
+        w_bank = psum.tile([P, 512], F32, name="w_bank")
 
         def spread_w():
             nc.tensor.matmul(w_bank[:], lhsT=ones[:], rhs=w_row[:], start=True, stop=True)
@@ -199,19 +200,19 @@ def tile_multiscaleretention_pc_w4_kernel(
 
         def gate_mm(i, h, g):
             if g == 0:
-                gb[i, h] = bank("g%d" % h)
+                gb[i, h] = bank()
             nc.tensor.matmul_mx(
                 out=gb[i, h][:],
                 lhsT=xc[i][:, P * g : P * (g + 1)].bitcast(FP8X4),
                 lhsT_scale=xsc[i][:, P * g : P * (g + 1)],
-                rhs=wg[h][:, g, :].bitcast(FP4X4),
+                rhs=wg[h // 2][:, g, 2 * DV * (h % 2) : 2 * DV * (h % 2 + 1)].bitcast(FP4X4),
                 rhs_scale=wg_sc[:, g, DV * h : DV * (h + 1)],
                 start=(g == 0),
                 stop=(g == GX - 1),
             )
 
         def gate_mul(i, h):
-            hb[i, h] = work.tile([P, 2, 256], BF16, name="hb%d" % h, tag="hb%d" % h)
+            hb[i, h] = work.tile([P, 2, 256], BF16, name="hb%d" % h, tag="hb%d" % h, bufs=3)
             gv = gb[i, h][:].rearrange("p (n u e) -> p u n e", u=2, e=2)
             wv = ow_cols(i, h).rearrange("p (n u e) -> p u n e", u=2, e=2)
             for u in range(2):
@@ -224,8 +225,8 @@ def tile_multiscaleretention_pc_w4_kernel(
                     op1=ALU.mult,
                 )
 
-        def transpose_h(i, half, tag):
-            ht[i, half] = bank(tag)
+        def transpose_h(i, half):
+            ht[i, half] = bank()
             for j in range(2):
                 for u in range(2):
                     col = P * (2 * j + u)
@@ -234,31 +235,36 @@ def tile_multiscaleretention_pc_w4_kernel(
                     )
 
         def gather_h(i, half, on_vector=False):
-            hs[i, half] = work.tile([P, 512], F32, name="hs%d" % half, tag="hs%d" % half, align_bytes=64)
-            dst = hs[i, half][:].rearrange("p (g n u) -> p g n u", g=2, u=2)
+            if half == 0:
+                hs[i] = work.tile([P, 2, 512], F32, name="hs", tag="hs", align_bytes=64)
+            dst = hs[i][:, half].rearrange("p (g n u) -> p g n u", g=2, u=2)
             src = ht[i, half][:].rearrange("p (g u n) -> p g n u", g=2, u=2)
             if on_vector:
                 nc.vector.tensor_copy(out=dst, in_=src)
             else:
                 nc.scalar.copy(out=dst, in_=src)
 
-        def quant_h(i, half):
-            hc[i, half] = work.tile([P, 2 * P], U32, name="hc%d" % half, tag="hc%d" % half, align_bytes=64)
-            hsc[i, half] = work.tile([P, 2 * P], U8, name="hsc%d" % half, tag="hsc%d" % half, align_bytes=64)
+        def quant_h(i, halves):
+            if halves[0] == 0:
+                hc[i] = work.tile([P, GH * P], U32, name="hc", tag="hc", align_bytes=64)
+                hsc[i] = work.tile([P, GH * P], U8, name="hsc", tag="hsc", align_bytes=64)
+            w = slice(2 * P * halves[0], 2 * P * (halves[-1] + 1))
             nc.vector.quantize_mx(
-                out=hc[i, half][:].bitcast(FP8X4), scales=hsc[i, half][:], in_=hs[i, half][:].bitcast(BF16)
+                out=hc[i][:, w].bitcast(FP8X4),
+                scales=hsc[i][:, w],
+                in_=hs[i][:, halves[0] : halves[-1] + 1].rearrange("p a n -> p (a n)").bitcast(BF16),
             )
 
-        def project_mm(i, c0, c1, passes, tag):
+        def project_mm(i, c0, c1, passes):
             if passes[0] == 0:
-                acc[i, c0] = bank(tag)
+                acc[i, c0] = bank()
             for g in passes:
-                w = slice(P * (g % 2), P * (g % 2 + 1))
+                w = slice(P * g, P * (g + 1))
                 nc.tensor.matmul_mx(
                     out=acc[i, c0][:, 0 : c1 - c0],
-                    lhsT=hc[i, g // 2][:, w].bitcast(FP8X4),
-                    lhsT_scale=hsc[i, g // 2][:, w],
-                    rhs=wo[g // 2][:, g % 2, 2 * c0 : 2 * c1].bitcast(FP4X4),
+                    lhsT=hc[i][:, w].bitcast(FP8X4),
+                    lhsT_scale=hsc[i][:, w],
+                    rhs=wo[c0 // 512][:, g, 2 * (c0 % 512) : 2 * (c0 % 512 + c1 - c0)].bitcast(FP4X4),
                     rhs_scale=wo_sc[:, g, c0:c1],
                     start=(g == 0),
                     stop=(g == GH - 1),
@@ -277,16 +283,16 @@ def tile_multiscaleretention_pc_w4_kernel(
 
         widen_x(0, 0, True)
         widen_x(0, 1, False)
-        transpose_x(0, [0], "x")
-        transpose_x(0, [1], "a0")
+        widen_x(1, 0, True)
+        widen_x(1, 1, False)
+        transpose_x(0, [0])
+        transpose_x(0, [1])
         spread_w()
+        transpose_x(1, both)
         scale_x(0, [0])
         scale_x(0, [1])
         quant_x(0, [0])
         quant_x(0, [1])
-        widen_x(1, 0, False)
-        widen_x(1, 1, False)
-        transpose_x(1, both, "x")
         squares(0, 0)
         squares(0, 1)
         inv_rms(0, 0, 2)
@@ -298,50 +304,63 @@ def tile_multiscaleretention_pc_w4_kernel(
             weigh_gpsimd(0, h, 1)
 
         for k in range(NT):
-            last = k == NT - 1
             for h in range(H):
                 for g in range(GX):
                     gate_mm(k, h, g)
             if k + 1 < NT:
                 scale_x(k + 1, both)
-            if k > 0:
-                quant_h(k - 1, 0)
-                quant_h(k - 1, 1)
+            if k >= 2:
+                quant_h(k - 2, [0])
+            if k == 0:
+                for h in range(H - 1):
+                    gate_mul(k, h)
             if k + 2 < NT:
-                widen_x(k + 2, 1, True)
+                widen_x(k + 2, 1, k > 0)
                 widen_x(k + 2, 0, False)
+            if k >= 2:
+                quant_h(k - 2, [1])
             if k + 1 < NT:
                 quant_x(k + 1, both)
-                weigh_gpsimd(k + 1, 1, H - 1)
+                for h in range(1, H):
+                    weigh_gpsimd(k + 1, h, 1)
                 for h in range(3):
                     squares(k + 1, h)
             for h in range(H):
-                gate_mul(k, h)
-            if k > 0:
-                project_mm(k - 1, 0, 512, every, "a0")
-                store(k - 1, 0, 512)
+                if k > 0 or h == H - 1:
+                    gate_mul(k, h)
+            if k == NT - 1:
+                for half in range(2):
+                    transpose_h(k - 1, half)
+                    gather_h(k - 1, half)
+            if k >= 2:
+                project_mm(k - 2, 0, 512, every)
+                store(k - 2, 0, 512)
             if k + 1 < NT:
                 weigh_vector(k + 1, 0)
                 squares(k + 1, 3)
-            if k > 0 and not last:
-                project_mm(k - 1, 512, 1024, every, "a1")
-                store(k - 1, 512, 1024)
+            if k >= 2:
+                project_mm(k - 2, 512, 1024, every)
+                store(k - 2, 512, 1024)
             if k + 1 < NT:
                 inv_rms(k + 1, 0, H)
             if k + 2 < NT:
-                transpose_x(k + 2, both, "x")
-            for half in range(2):
-                transpose_h(k, half, "g%d" % (2 + half))
-                gather_h(k, half, on_vector=last and half == 1)
+                transpose_x(k + 2, both)
+            if 1 <= k < NT - 1:
+                for half in range(2):
+                    transpose_h(k - 1, half)
+                    gather_h(k - 1, half)
 
         k = NT - 1
-        quant_h(k, 0)
-        quant_h(k, 1)
-        project_mm(k - 1, 512, 1024, every, "a1")
+        quant_h(k - 1, both)
+        for half in range(2):
+            transpose_h(k, half)
+            gather_h(k, half)
+        quant_h(k, both)
+        project_mm(k - 1, 0, 512, every)
+        store(k - 1, 0, 512)
+        project_mm(k - 1, 512, 1024, every)
         store(k - 1, 512, 1024)
-        chunks = [(0, 512, "a0"), (512, 768, "g0"), (768, 1024, "g1")]
-        for passes in ([0, 1], [2, 3]):
-            for c0, c1, tag in chunks:
-                project_mm(k, c0, c1, passes, tag)
-        for j, (c0, c1, tag) in enumerate(chunks):
+        chunks = [(0, 512), (512, 768), (768, 1024)]
+        for j, (c0, c1) in enumerate(chunks):
+            project_mm(k, c0, c1, every)
             store(k, c0, c1, on_vector=j == 1)

@@ -54,7 +54,6 @@ def tile_multiscaleretention_pc_w4_kernel(
         w_row = const.tile([P, DV], BF16, name="w_row")
         ones = const.tile([P, P], BF16, name="ones")
         gnw = const.tile([P, DV], BF16, name="gnw")
-        s4 = const.tile([P, GX, 4], F32, name="s4")
         x_cuts = [(0, 2), (2, 4), (4, 8)]
         x_tiles = [const.tile([P, b - a, E], U8, name="xbytes%d" % a) for a, b in x_cuts]
         o_first = [const.tile([P, F // 2], BF16, name="ofirst%d" % j) for j in range(2)]
@@ -62,6 +61,7 @@ def tile_multiscaleretention_pc_w4_kernel(
         wg = [const.tile([P, GX, F], U8, name="wg%d" % j, align_bytes=64) for j in range(2)]
         wo = [const.tile([P, GH, E], U8, name="wo%d" % k, align_bytes=64) for k in range(2)]
         shared = [const.tile([P, (H - 1) * DV], F32, name="shared%d" % j, align_bytes=64) for j in range(2)]
+        s4 = const.tile([P, GX, 4], F32, name="s4")
 
         nc.gpsimd.memset(w_row[:].bitcast(F32), 0.0)
         make_identity(nc, ident[:])

@@ -174,10 +174,16 @@ def tile_multiscaleretention_pc_w4_kernel(
                 out=rr[i][:, h0:h1], in_=ss[i][:, h0:h1], func=ACT.Abs_reciprocal_sqrt, scale=1.0 / DV, bias=EPS
             )
 
+        def by_parity(cols):
+            return cols.rearrange("p (n u e) -> p u n e", u=2, e=2)
+
+        def as_parity(cols):
+            return cols.rearrange("p (u n e) -> p u n e", u=2, e=2)
+
         w_bank = psum.tile([P, 512], F32, name="w_bank")
 
         def spread_w():
-            nc.tensor.matmul(w_bank[:], lhsT=ones[:], rhs=w_row[:], start=True, stop=True)
+            nc.tensor.matmul(w_bank[:], lhsT=ones[:], rhs=by_parity(w_row[:]), start=True, stop=True)
             nc.scalar.copy(out=gnw[:], in_=w_bank[:])
 
         def ow_cols(i, h):
@@ -188,14 +194,13 @@ def tile_multiscaleretention_pc_w4_kernel(
         def weigh_vector(i, h):
             if h == 0:
                 ow0[i] = work.tile([P, DV], F32, name="ow0", tag="ow0")
-            nc.vector.tensor_tensor(out=ow_cols(i, h), in0=o_cols(i, h), in1=w_bank[:], op=ALU.mult)
+            nc.vector.tensor_tensor(
+                out=as_parity(ow_cols(i, h)), in0=by_parity(o_cols(i, h)), in1=as_parity(w_bank[:]), op=ALU.mult
+            )
 
-        def weigh_gpsimd(i, h, n):
+        def weigh_gpsimd(i, h):
             nc.gpsimd.tensor_tensor(
-                out=shared[i % 2][:, DV * (h - 1) : DV * (h - 1 + n)].rearrange("p (h d) -> p h d", h=n),
-                in0=o_cols(i, h, n).rearrange("p (h d) -> p h d", h=n),
-                in1=gnw[:].unsqueeze(1).to_broadcast([P, n, DV]),
-                op=ALU.mult,
+                out=as_parity(ow_cols(i, h)), in0=by_parity(o_cols(i, h)), in1=as_parity(gnw[:]), op=ALU.mult
             )
 
         def gate_mm(i, h, g):
@@ -213,8 +218,8 @@ def tile_multiscaleretention_pc_w4_kernel(
 
         def gate_mul(i, h):
             hb[i, h] = work.tile([P, 2, 256], BF16, name="hb%d" % h, tag="hb%d" % h, bufs=3)
-            gv = gb[i, h][:].rearrange("p (n u e) -> p u n e", u=2, e=2)
-            wv = ow_cols(i, h).rearrange("p (n u e) -> p u n e", u=2, e=2)
+            gv = by_parity(gb[i, h][:])
+            wv = as_parity(ow_cols(i, h))
             for u in range(2):
                 nc.vector.scalar_tensor_tensor(
                     out=hb[i, h][:, u].rearrange("p (n e) -> p n e", e=2),
@@ -271,7 +276,7 @@ def tile_multiscaleretention_pc_w4_kernel(
                 )
 
         def store(i, c0, c1, on_vector=False):
-            res = work.tile([P, 512], F32, name="res", tag="res", bufs=4)
+            res = work.tile([P, 512], F32, name="res", tag="res", bufs=6)
             if on_vector:
                 nc.vector.tensor_copy(out=res[:, 0 : c1 - c0], in_=acc[i, c0][:, 0 : c1 - c0])
             else:
@@ -301,7 +306,7 @@ def tile_multiscaleretention_pc_w4_kernel(
         inv_rms(0, 2, 4)
         weigh_vector(0, 0)
         for h in range(1, H):
-            weigh_gpsimd(0, h, 1)
+            weigh_gpsimd(0, h)
 
         for k in range(NT):
             for h in range(H):
@@ -315,14 +320,14 @@ def tile_multiscaleretention_pc_w4_kernel(
                 for h in range(H - 1):
                     gate_mul(k, h)
             if k + 2 < NT:
-                widen_x(k + 2, 1, k > 0)
+                widen_x(k + 2, 1, False)
                 widen_x(k + 2, 0, False)
             if k >= 2:
                 quant_h(k - 2, [1])
             if k + 1 < NT:
                 quant_x(k + 1, both)
                 for h in range(1, H):
-                    weigh_gpsimd(k + 1, h, 1)
+                    weigh_gpsimd(k + 1, h)
                 for h in range(3):
                     squares(k + 1, h)
             for h in range(H):
@@ -354,7 +359,7 @@ def tile_multiscaleretention_pc_w4_kernel(
         quant_h(k - 1, both)
         for half in range(2):
             transpose_h(k, half)
-            gather_h(k, half)
+            gather_h(k, half, on_vector=half == 1)
         quant_h(k, both)
         project_mm(k - 1, 0, 512, every)
         store(k - 1, 0, 512)

@@ -59,7 +59,7 @@ def tile_multiscaleretention_pc_w4_kernel(
         o_first = [const.tile([P, F // 2], BF16, name="ofirst%d" % j) for j in range(2)]
         o_tiles = [None] + [const.tile([P, F], BF16, name="o%d" % i) for i in range(1, NT)]
         wg = [const.tile([P, GX, F], U8, name="wg%d" % j, align_bytes=64) for j in range(2)]
-        wo = [const.tile([P, GH, E], U8, name="wo%d" % k, align_bytes=64) for k in range(2)]
+        wo = [const.tile([P, 2, 2 * E], U8, name="wo%d" % k, align_bytes=64) for k in range(2)]
         shared = [const.tile([P, (H - 1) * DV], F32, name="shared%d" % j, align_bytes=64) for j in range(2)]
         s4 = const.tile([P, GX, 4], F32, name="s4")
 
@@ -83,6 +83,9 @@ def tile_multiscaleretention_pc_w4_kernel(
         def load_wg(j):
             nc.sync.dma_start(out=wg[j][:], in_=wg_view[:, :, F * j : F * (j + 1)])
 
+        def load_wo(j):
+            nc.sync.dma_start(out=wo[j][:], in_=wo_view[:, 2 * j : 2 * j + 2, :])
+
         def load_o(i):
             nc.sync.dma_start(out=o_tiles[i][:], in_=o_view[i])
 
@@ -100,11 +103,12 @@ def tile_multiscaleretention_pc_w4_kernel(
         load_x(1)
         load_o(1)
         load_o(2)
-        load_scales(nc.sync, wo_sc, Wo_scales)
-        nc.sync.dma_start(out=wo[0][:], in_=wo_view[:, :, 0:E])
-        nc.sync.dma_start(out=wo[1][:], in_=wo_view[:, :, E : 2 * E])
         load_x(2)
-        for i in range(3, NT):
+        load_scales(nc.sync, wo_sc, Wo_scales)
+        load_wo(0)
+        load_wo(1)
+        load_o(3)
+        for i in range(4, NT):
             load_o(i)
 
         xb, xt, xc, xsc = {}, {}, {}, {}
@@ -191,17 +195,21 @@ def tile_multiscaleretention_pc_w4_kernel(
                 return ow0[i][:]
             return shared[i % 2][:, DV * (h - 1) : DV * h]
 
-        def weigh_vector(i, h):
-            if h == 0:
+        def weigh(engine, w, i, h, parities):
+            if i not in ow0:
                 ow0[i] = work.tile([P, DV], F32, name="ow0", tag="ow0")
-            nc.vector.tensor_tensor(
-                out=as_parity(ow_cols(i, h)), in0=by_parity(o_cols(i, h)), in1=as_parity(w_bank[:]), op=ALU.mult
+            engine.tensor_tensor(
+                out=as_parity(ow_cols(i, h))[:, parities],
+                in0=by_parity(o_cols(i, h))[:, parities],
+                in1=as_parity(w)[:, parities],
+                op=ALU.mult,
             )
 
-        def weigh_gpsimd(i, h):
-            nc.gpsimd.tensor_tensor(
-                out=as_parity(ow_cols(i, h)), in0=by_parity(o_cols(i, h)), in1=as_parity(gnw[:]), op=ALU.mult
-            )
+        def weigh_vector(i, h, par=slice(0, 2)):
+            weigh(nc.vector, w_bank[:], i, h, par)
+
+        def weigh_gpsimd(i, h, par=slice(0, 2)):
+            weigh(nc.gpsimd, gnw[:], i, h, par)
 
         def gate_mm(i, h, g):
             if g == 0:
@@ -269,7 +277,7 @@ def tile_multiscaleretention_pc_w4_kernel(
                     out=acc[i, c0][:, 0 : c1 - c0],
                     lhsT=hc[i][:, w].bitcast(FP8X4),
                     lhsT_scale=hsc[i][:, w],
-                    rhs=wo[c0 // 512][:, g, 2 * (c0 % 512) : 2 * (c0 % 512 + c1 - c0)].bitcast(FP4X4),
+                    rhs=wo[g // 2][:, g % 2, 2 * c0 : 2 * c1].bitcast(FP4X4),
                     rhs_scale=wo_sc[:, g, c0:c1],
                     start=(g == 0),
                     stop=(g == GH - 1),
@@ -286,86 +294,241 @@ def tile_multiscaleretention_pc_w4_kernel(
         both = [0, 1]
         every = [0, 1, 2, 3]
 
+        def gate(i, heads):
+            for h in heads:
+                for g in range(GX):
+                    gate_mm(i, h, g)
+
         widen_x(0, 0, True)
         widen_x(0, 1, False)
         widen_x(1, 0, True)
         widen_x(1, 1, False)
         transpose_x(0, [0])
         transpose_x(0, [1])
+        squares(0, 0)
         spread_w()
         transpose_x(1, both)
         scale_x(0, [0])
         scale_x(0, [1])
-        quant_x(0, [0])
-        quant_x(0, [1])
-        squares(0, 0)
+        quant_x(0, both)
         squares(0, 1)
         inv_rms(0, 0, 2)
         squares(0, 2)
         squares(0, 3)
         inv_rms(0, 2, 4)
         weigh_vector(0, 0)
-        for h in range(1, H):
-            weigh_gpsimd(0, h)
-
-        for k in range(NT):
-            for h in range(H):
-                for g in range(GX):
-                    gate_mm(k, h, g)
-            if k + 1 < NT:
-                scale_x(k + 1, both)
-            if k >= 2:
-                quant_h(k - 2, [0])
-            if k == 0:
-                for h in range(H - 1):
-                    gate_mul(k, h)
-            if k + 2 < NT:
-                widen_x(k + 2, 1, False)
-                widen_x(k + 2, 0, False)
-            if k >= 2:
-                quant_h(k - 2, [1])
-            if k + 1 < NT:
-                quant_x(k + 1, both)
-                for h in range(1, H):
-                    weigh_gpsimd(k + 1, h)
-                for h in range(3):
-                    squares(k + 1, h)
-            for h in range(H):
-                if k > 0 or h == H - 1:
-                    gate_mul(k, h)
-            if k == NT - 1:
-                for half in range(2):
-                    transpose_h(k - 1, half)
-                    gather_h(k - 1, half)
-            if k >= 2:
-                project_mm(k - 2, 0, 512, every)
-                store(k - 2, 0, 512)
-            if k + 1 < NT:
-                weigh_vector(k + 1, 0)
-                squares(k + 1, 3)
-            if k >= 2:
-                project_mm(k - 2, 512, 1024, every)
-                store(k - 2, 512, 1024)
-            if k + 1 < NT:
-                inv_rms(k + 1, 0, H)
-            if k + 2 < NT:
-                transpose_x(k + 2, both)
-            if 1 <= k < NT - 1:
-                for half in range(2):
-                    transpose_h(k - 1, half)
-                    gather_h(k - 1, half)
-
-        k = NT - 1
-        quant_h(k - 1, both)
-        for half in range(2):
-            transpose_h(k, half)
-            gather_h(k, half, on_vector=half == 1)
-        quant_h(k, both)
-        project_mm(k - 1, 0, 512, every)
-        store(k - 1, 0, 512)
-        project_mm(k - 1, 512, 1024, every)
-        store(k - 1, 512, 1024)
-        chunks = [(0, 512), (512, 768), (768, 1024)]
-        for j, (c0, c1) in enumerate(chunks):
-            project_mm(k, c0, c1, every)
-            store(k, c0, c1, on_vector=j == 1)
+        weigh_gpsimd(0, 1)
+        weigh_gpsimd(0, 2)
+        weigh_gpsimd(0, 3)
+        gate(0, every)
+        scale_x(1, both)
+        gate_mul(0, 0)
+        gate_mul(0, 1)
+        gate_mul(0, 2)
+        widen_x(2, 0, False)
+        widen_x(2, 1, False)
+        quant_x(1, both)
+        weigh_gpsimd(1, 1)
+        weigh_gpsimd(1, 2)
+        weigh_gpsimd(1, 3)
+        squares(1, 0)
+        squares(1, 1)
+        gate_mul(0, 3)
+        weigh_vector(1, 0)
+        inv_rms(1, 0, 2)
+        squares(1, 2)
+        squares(1, 3)
+        inv_rms(1, 2, 4)
+        transpose_x(2, both)
+        scale_x(2, both)
+        gate(1, every)
+        widen_x(3, 0, False)
+        widen_x(3, 1, False)
+        gate_mul(1, 0)
+        gate_mul(1, 1)
+        quant_x(2, both)
+        weigh_gpsimd(2, 1)
+        weigh_gpsimd(2, 2)
+        weigh_gpsimd(2, 3)
+        squares(2, 0)
+        squares(2, 1)
+        transpose_h(0, 0)
+        gather_h(0, 0)
+        transpose_h(0, 1)
+        gather_h(0, 1)
+        transpose_x(3, both)
+        gate_mul(1, 2)
+        gate_mul(1, 3)
+        weigh_vector(2, 0)
+        inv_rms(2, 0, 2)
+        widen_x(4, 0, False)
+        widen_x(4, 1, False)
+        squares(2, 2)
+        squares(2, 3)
+        inv_rms(2, 2, 4)
+        scale_x(3, both)
+        gate(2, [0, 1])
+        gate_mul(2, 0)
+        gate_mul(2, 1)
+        quant_h(0, both)
+        quant_x(3, both)
+        weigh_gpsimd(3, 1)
+        weigh_gpsimd(3, 2)
+        weigh_gpsimd(3, 3)
+        squares(3, 0)
+        squares(3, 1)
+        transpose_h(1, 0)
+        gather_h(1, 0)
+        transpose_h(1, 1)
+        gather_h(1, 1)
+        transpose_x(4, both)
+        gate(2, [2, 3])
+        gate_mul(2, 2)
+        gate_mul(2, 3)
+        weigh_vector(3, 0)
+        squares(3, 2)
+        squares(3, 3)
+        project_mm(0, 0, 512, every)
+        store(0, 0, 512)
+        inv_rms(3, 0, H)
+        project_mm(0, 512, 1024, every)
+        store(0, 512, 1024)
+        scale_x(4, both)
+        gate(3, every)
+        widen_x(5, 0, False)
+        widen_x(5, 1, False)
+        gate_mul(3, 0)
+        gate_mul(3, 1)
+        quant_h(1, both)
+        quant_x(4, both)
+        weigh_gpsimd(4, 1)
+        weigh_gpsimd(4, 2)
+        weigh_gpsimd(4, 3)
+        squares(4, 0)
+        squares(4, 1)
+        transpose_h(2, 0)
+        gather_h(2, 0)
+        transpose_h(2, 1)
+        gather_h(2, 1)
+        transpose_x(5, both)
+        gate_mul(3, 2)
+        gate_mul(3, 3)
+        weigh_vector(4, 0)
+        squares(4, 2)
+        squares(4, 3)
+        project_mm(1, 0, 512, every)
+        store(1, 0, 512)
+        inv_rms(4, 0, H)
+        project_mm(1, 512, 1024, every)
+        store(1, 512, 1024)
+        scale_x(5, both)
+        gate(4, every)
+        widen_x(6, 0, False)
+        widen_x(6, 1, False)
+        gate_mul(4, 0)
+        gate_mul(4, 1)
+        quant_h(2, both)
+        quant_x(5, both)
+        weigh_gpsimd(5, 1)
+        weigh_gpsimd(5, 2)
+        weigh_gpsimd(5, 3)
+        squares(5, 0)
+        squares(5, 1)
+        transpose_h(3, 0)
+        gather_h(3, 0)
+        transpose_h(3, 1)
+        gather_h(3, 1)
+        transpose_x(6, both)
+        gate_mul(4, 2)
+        gate_mul(4, 3)
+        weigh_vector(5, 0)
+        squares(5, 2)
+        squares(5, 3)
+        project_mm(2, 0, 512, every)
+        store(2, 0, 512)
+        inv_rms(5, 0, H)
+        project_mm(2, 512, 1024, every)
+        store(2, 512, 1024)
+        scale_x(6, both)
+        gate(5, every)
+        widen_x(7, 0, False)
+        widen_x(7, 1, False)
+        gate_mul(5, 0)
+        gate_mul(5, 1)
+        quant_h(3, both)
+        quant_x(6, both)
+        weigh_gpsimd(6, 1)
+        weigh_gpsimd(6, 2)
+        weigh_gpsimd(6, 3)
+        squares(6, 0)
+        squares(6, 1)
+        transpose_h(4, 0)
+        gather_h(4, 0)
+        transpose_h(4, 1)
+        gather_h(4, 1)
+        transpose_x(7, both)
+        gate_mul(5, 2)
+        gate_mul(5, 3)
+        weigh_vector(6, 0)
+        squares(6, 2)
+        squares(6, 3)
+        project_mm(3, 0, 512, every)
+        store(3, 0, 512)
+        inv_rms(6, 0, H)
+        project_mm(3, 512, 1024, every)
+        store(3, 512, 1024)
+        scale_x(7, both)
+        gate(6, every)
+        gate_mul(6, 0)
+        quant_h(4, both)
+        quant_x(7, both)
+        weigh_gpsimd(7, 1)
+        weigh_gpsimd(7, 2)
+        weigh_gpsimd(7, 3)
+        squares(7, 0)
+        squares(7, 1)
+        transpose_h(5, 0)
+        gather_h(5, 0)
+        transpose_h(5, 1)
+        gather_h(5, 1)
+        gate_mul(6, 1)
+        gate_mul(6, 2)
+        gate_mul(6, 3)
+        weigh_vector(7, 0)
+        squares(7, 2)
+        squares(7, 3)
+        project_mm(4, 0, 512, every)
+        store(4, 0, 512)
+        inv_rms(7, 0, H)
+        project_mm(4, 512, 1024, every)
+        store(4, 512, 1024)
+        gate(7, every)
+        quant_h(5, both)
+        transpose_h(6, 0)
+        gather_h(6, 0)
+        transpose_h(6, 1)
+        gather_h(6, 1)
+        gate_mul(7, 0)
+        gate_mul(7, 1)
+        gate_mul(7, 2)
+        gate_mul(7, 3)
+        project_mm(5, 0, 512, every)
+        store(5, 0, 512)
+        project_mm(5, 512, 1024, every)
+        store(5, 512, 1024)
+        quant_h(6, both)
+        transpose_h(7, 0)
+        gather_h(7, 0)
+        transpose_h(7, 1)
+        gather_h(7, 1, on_vector=True)
+        quant_h(7, both)
+        project_mm(6, 0, 512, every)
+        store(6, 0, 512)
+        project_mm(6, 512, 1024, every)
+        store(6, 512, 1024)
+        project_mm(7, 0, 512, every)
+        store(7, 0, 512)
+        project_mm(7, 512, 768, every)
+        store(7, 512, 768, on_vector=True)
+        project_mm(7, 768, 1024, every)
+        store(7, 768, 1024)

@@ -29,7 +29,7 @@ def tile_multiscaleretention_pc_w4_kernel(
     tc, o_ret, x_bytes, x_scale, Wg_words, Wg_scales, gn_weight, Wo_words, Wo_scales, out
 ):
     nc = tc.nc
-    o_view = o_ret.rearrange("b (p i) h d -> i p (b h d)", i=NT)
+    o_view = o_ret.rearrange("b (p i) h d -> p (b i) (h d)", i=NT)
     x_view = x_bytes.rearrange("b (p i) e -> p (b i) e", i=NT)
     out_view = out.rearrange("b (p i) e -> i p (b e)", i=NT)
     wg_view = Wg_words.rearrange("g p n -> p g n")
@@ -57,10 +57,11 @@ def tile_multiscaleretention_pc_w4_kernel(
         x_cuts = [(0, 2), (2, 4), (4, 8)]
         x_tiles = [const.tile([P, b - a, E], U8, name="xbytes%d" % a) for a, b in x_cuts]
         o_first = [const.tile([P, F // 2], BF16, name="ofirst%d" % j) for j in range(2)]
-        o_tiles = [None] + [const.tile([P, F], BF16, name="o%d" % i) for i in range(1, NT)]
+        o_cuts = [(1, 2), (2, 3), (3, 4), (4, 8)]
+        o_tiles = [const.tile([P, b - a, F], BF16, name="o%d" % a) for a, b in o_cuts]
         wg = [const.tile([P, GX, F], U8, name="wg%d" % j, align_bytes=64) for j in range(2)]
         wo = [const.tile([P, 2, 2 * E], U8, name="wo%d" % k, align_bytes=64) for k in range(2)]
-        shared = [const.tile([P, (H - 1) * DV], F32, name="shared%d" % j, align_bytes=64) for j in range(2)]
+        shared = [const.tile([P, (H - 1) * DV], F32, name="shared%d" % j, align_bytes=64) for j in range(3)]
         s4 = const.tile([P, GX, 4], F32, name="s4")
 
         nc.gpsimd.memset(w_row[:].bitcast(F32), 0.0)
@@ -86,11 +87,12 @@ def tile_multiscaleretention_pc_w4_kernel(
         def load_wo(j):
             nc.sync.dma_start(out=wo[j][:], in_=wo_view[:, 2 * j : 2 * j + 2, :])
 
-        def load_o(i):
-            nc.sync.dma_start(out=o_tiles[i][:], in_=o_view[i])
+        def load_o(k):
+            a, b = o_cuts[k]
+            nc.sync.dma_start(out=o_tiles[k][:], in_=o_view[:, a:b, :])
 
         def load_o_first(j):
-            nc.sync.dma_start(out=o_first[j][:], in_=o_view[0][:, F // 2 * j : F // 2 * (j + 1)])
+            nc.sync.dma_start(out=o_first[j][:], in_=o_view[:, 0, F // 2 * j : F // 2 * (j + 1)])
 
         load_x(0)
         nc.sync.dma_start(out=s4[:], in_=x_scale.rearrange("a b (g p t) -> p (a b g) t", p=P, t=4))
@@ -101,15 +103,14 @@ def tile_multiscaleretention_pc_w4_kernel(
         load_o_first(1)
         load_wg(1)
         load_x(1)
+        load_o(0)
         load_o(1)
-        load_o(2)
         load_x(2)
         load_scales(nc.sync, wo_sc, Wo_scales)
         load_wo(0)
         load_wo(1)
+        load_o(2)
         load_o(3)
-        for i in range(4, NT):
-            load_o(i)
 
         xb, xt, xc, xsc = {}, {}, {}, {}
         ss, rr, ow0, hb, ht, hs, hc, hsc, gb, acc = {}, {}, {}, {}, {}, {}, {}, {}, {}, {}
@@ -117,28 +118,28 @@ def tile_multiscaleretention_pc_w4_kernel(
         def o_cols(i, h, n=1):
             if i == 0:
                 return o_first[h // 2][:, DV * (h % 2) : DV * (h % 2 + n)]
-            return o_tiles[i][:, DV * h : DV * (h + n)]
+            k = max(k for k, (a, b) in enumerate(o_cuts) if a <= i)
+            return o_tiles[k][:, i - o_cuts[k][0], DV * h : DV * (h + n)]
 
-        def widen_x(i, g, on_vector):
+        def widen_x(i, vector_cols=0):
             k = max(k for k, (a, b) in enumerate(x_cuts) if a <= i)
-            src = x_tiles[k][:, i - x_cuts[k][0], 512 * g : 512 * (g + 1)].bitcast(E4M3)
-            xb[i, g] = work.tile([P, 512], BF16, name="xb%d" % g, tag="xb%d" % g)
-            if on_vector:
-                nc.vector.tensor_copy(out=xb[i, g][:], in_=src)
-            else:
-                nc.scalar.copy(out=xb[i, g][:], in_=src)
+            src = x_tiles[k][:, i - x_cuts[k][0], :]
+            xb[i] = work.tile([P, E], BF16, name="xb", tag="xb")
+            if vector_cols:
+                nc.vector.tensor_copy(out=xb[i][:, 0:vector_cols], in_=src[:, 0:vector_cols].bitcast(E4M3))
+            nc.scalar.copy(out=xb[i][:, vector_cols:E], in_=src[:, vector_cols:E].bitcast(E4M3))
 
         def transpose_x(i, passes):
             b = bank()
             for j, g in enumerate(passes):
                 xt[i, g] = b
-                words = xb[i, g][:].bitcast(F32)
+                words = xb[i][:, 512 * g : 512 * (g + 1)].bitcast(F32)
                 for u in range(2):
                     col = P * (len(passes) * u + j)
                     nc.tensor.transpose(b[:, col : col + P], words[:, u:256:2], ident[:])
 
         def xs_view(i):
-            return shared[i % 2][:, 0 : E // 2].bitcast(BF16)
+            return shared[i % 3][:, 0 : E // 2].bitcast(BF16)
 
         def scale_x(i, passes):
             n = len(passes)
@@ -168,9 +169,9 @@ def tile_multiscaleretention_pc_w4_kernel(
 
         def squares(i, h):
             if h == 0:
-                ss[i] = work.tile([P, H], F32, name="ss", tag="ss")
-                rr[i] = work.tile([P, H], F32, name="rr", tag="rr")
-            junk = work.tile([P, DV], BF16, name="junk", tag="junk")
+                ss[i] = work.tile([P, H], F32, name="ss", tag="ss", bufs=3)
+                rr[i] = work.tile([P, H], F32, name="rr", tag="rr", bufs=3)
+            junk = work.tile([P, DV], BF16, name="junk", tag="junk", bufs=4)
             nc.scalar.activation(out=junk[:], in_=o_cols(i, h), func=ACT.Square, accum_out=ss[i][:, h : h + 1])
 
         def inv_rms(i, h0, h1):
@@ -190,30 +191,32 @@ def tile_multiscaleretention_pc_w4_kernel(
             nc.tensor.matmul(w_bank[:], lhsT=ones[:], rhs=by_parity(w_row[:]), start=True, stop=True)
             nc.scalar.copy(out=gnw[:], in_=w_bank[:])
 
-        def ow_cols(i, h):
-            if h == 0:
-                return ow0[i][:]
-            return shared[i % 2][:, DV * (h - 1) : DV * h]
+        def head_groups(i):
+            return [[(1, 2), (2, 3), (3, 4)], [(1, 2), (2, 4)]][i] if i < 2 else [(1, 4)]
 
-        def weigh(engine, w, i, h, parities):
-            if i not in ow0:
-                ow0[i] = work.tile([P, DV], F32, name="ow0", tag="ow0")
-            engine.tensor_tensor(
-                out=as_parity(ow_cols(i, h))[:, parities],
-                in0=by_parity(o_cols(i, h))[:, parities],
-                in1=as_parity(w)[:, parities],
-                op=ALU.mult,
+        def ow_head(i, h):
+            if h == 0:
+                return as_parity(ow0[i][:])
+            a, b = [(a, b) for a, b in head_groups(i) if a <= h < b][0]
+            return as_parity(shared[i % 3][:, DV * (a - 1) : DV * (b - 1)])[:, :, P * (h - a) : P * (h - a + 1), :]
+
+        def weigh_vector(i):
+            ow0[i] = work.tile([P, DV], F32, name="ow0", tag="ow0")
+            nc.vector.tensor_tensor(
+                out=ow_head(i, 0), in0=by_parity(o_cols(i, 0)), in1=as_parity(w_bank[:]), op=ALU.mult
             )
 
-        def weigh_vector(i, h, par=slice(0, 2)):
-            weigh(nc.vector, w_bank[:], i, h, par)
-
-        def weigh_gpsimd(i, h, par=slice(0, 2)):
-            weigh(nc.gpsimd, gnw[:], i, h, par)
+        def weigh_gpsimd(i):
+            w = gnw[:].rearrange("p (u c) -> p u c", u=2).unsqueeze(2)
+            for a, b in head_groups(i):
+                nc.gpsimd.tensor_tensor(
+                    out=shared[i % 3][:, DV * (a - 1) : DV * (b - 1)].rearrange("p (u h c) -> p u h c", u=2, h=b - a),
+                    in0=by_parity(o_cols(i, a, b - a)),
+                    in1=w.to_broadcast([P, 2, b - a, DV // 2]),
+                    op=ALU.mult,
+                )
 
         def gate_mm(i, h, g):
-            if g == 0:
-                gb[i, h] = bank()
             nc.tensor.matmul_mx(
                 out=gb[i, h][:],
                 lhsT=xc[i][:, P * g : P * (g + 1)].bitcast(FP8X4),
@@ -227,7 +230,7 @@ def tile_multiscaleretention_pc_w4_kernel(
         def gate_mul(i, h):
             hb[i, h] = work.tile([P, 2, 256], BF16, name="hb%d" % h, tag="hb%d" % h, bufs=3)
             gv = by_parity(gb[i, h][:])
-            wv = as_parity(ow_cols(i, h))
+            wv = ow_head(i, h)
             for u in range(2):
                 nc.vector.scalar_tensor_tensor(
                     out=hb[i, h][:, u].rearrange("p (n e) -> p n e", e=2),
@@ -248,7 +251,7 @@ def tile_multiscaleretention_pc_w4_kernel(
                     )
 
         def gather_h(i, half, on_vector=False):
-            if half == 0:
+            if i not in hs:
                 hs[i] = work.tile([P, 2, 512], F32, name="hs", tag="hs", align_bytes=64)
             dst = hs[i][:, half].rearrange("p (g n u) -> p g n u", g=2, u=2)
             src = ht[i, half][:].rearrange("p (g u n) -> p g n u", g=2, u=2)
@@ -294,227 +297,205 @@ def tile_multiscaleretention_pc_w4_kernel(
         both = [0, 1]
         every = [0, 1, 2, 3]
 
-        def gate(i, heads):
+        def gate(i, heads, banks_for=()):
+            for h in banks_for:
+                gb[i, h] = bank()
             for h in heads:
                 for g in range(GX):
                     gate_mm(i, h, g)
 
-        widen_x(0, 0, True)
-        widen_x(0, 1, False)
-        widen_x(1, 0, True)
-        widen_x(1, 1, False)
+        widen_x(0, 512)
+        widen_x(1, 512)
         transpose_x(0, [0])
         transpose_x(0, [1])
-        squares(0, 0)
         spread_w()
         transpose_x(1, both)
         scale_x(0, [0])
         scale_x(0, [1])
         quant_x(0, both)
+        squares(0, 0)
         squares(0, 1)
         inv_rms(0, 0, 2)
         squares(0, 2)
         squares(0, 3)
         inv_rms(0, 2, 4)
-        weigh_vector(0, 0)
-        weigh_gpsimd(0, 1)
-        weigh_gpsimd(0, 2)
-        weigh_gpsimd(0, 3)
-        gate(0, every)
+        weigh_vector(0)
         scale_x(1, both)
+        weigh_gpsimd(0)
+        gate(0, [0, 1, 3, 2], [0, 1, 2, 3])
         gate_mul(0, 0)
         gate_mul(0, 1)
         gate_mul(0, 2)
-        widen_x(2, 0, False)
-        widen_x(2, 1, False)
+        widen_x(2)
         quant_x(1, both)
-        weigh_gpsimd(1, 1)
-        weigh_gpsimd(1, 2)
-        weigh_gpsimd(1, 3)
+        weigh_gpsimd(1)
         squares(1, 0)
         squares(1, 1)
         gate_mul(0, 3)
-        weigh_vector(1, 0)
-        inv_rms(1, 0, 2)
+        weigh_vector(1)
         squares(1, 2)
         squares(1, 3)
-        inv_rms(1, 2, 4)
+        inv_rms(1, 0, H)
         transpose_x(2, both)
         scale_x(2, both)
-        gate(1, every)
-        widen_x(3, 0, False)
-        widen_x(3, 1, False)
+        gate(1, [1, 0], [0, 1, 2, 3])
+        widen_x(3)
         gate_mul(1, 0)
         gate_mul(1, 1)
         quant_x(2, both)
-        weigh_gpsimd(2, 1)
-        weigh_gpsimd(2, 2)
-        weigh_gpsimd(2, 3)
+        weigh_gpsimd(2)
         squares(2, 0)
         squares(2, 1)
         transpose_h(0, 0)
-        gather_h(0, 0)
         transpose_h(0, 1)
         gather_h(0, 1)
+        gather_h(0, 0)
+        gate(1, [2, 3])
         transpose_x(3, both)
-        gate_mul(1, 2)
         gate_mul(1, 3)
-        weigh_vector(2, 0)
+        gate_mul(1, 2)
+        weigh_vector(2)
         inv_rms(2, 0, 2)
-        widen_x(4, 0, False)
-        widen_x(4, 1, False)
+        widen_x(4)
         squares(2, 2)
         squares(2, 3)
         inv_rms(2, 2, 4)
         scale_x(3, both)
-        gate(2, [0, 1])
+        gate(2, [1, 0], [0, 1, 2, 3])
         gate_mul(2, 0)
-        gate_mul(2, 1)
         quant_h(0, both)
         quant_x(3, both)
-        weigh_gpsimd(3, 1)
-        weigh_gpsimd(3, 2)
-        weigh_gpsimd(3, 3)
+        weigh_gpsimd(3)
         squares(3, 0)
         squares(3, 1)
         transpose_h(1, 0)
-        gather_h(1, 0)
         transpose_h(1, 1)
         gather_h(1, 1)
+        gather_h(1, 0)
+        gate(2, [3, 2])
         transpose_x(4, both)
-        gate(2, [2, 3])
+        gate_mul(2, 1)
         gate_mul(2, 2)
         gate_mul(2, 3)
-        weigh_vector(3, 0)
+        weigh_vector(3)
         squares(3, 2)
         squares(3, 3)
         project_mm(0, 0, 512, every)
-        store(0, 0, 512)
-        inv_rms(3, 0, H)
         project_mm(0, 512, 1024, every)
         store(0, 512, 1024)
+        inv_rms(3, 0, H)
+        store(0, 0, 512)
         scale_x(4, both)
-        gate(3, every)
-        widen_x(5, 0, False)
-        widen_x(5, 1, False)
-        gate_mul(3, 0)
-        gate_mul(3, 1)
+        gate(3, [2, 1, 3, 0], [1, 0, 2, 3])
+        widen_x(5)
         quant_h(1, both)
         quant_x(4, both)
-        weigh_gpsimd(4, 1)
-        weigh_gpsimd(4, 2)
-        weigh_gpsimd(4, 3)
+        weigh_gpsimd(4)
         squares(4, 0)
-        squares(4, 1)
         transpose_h(2, 0)
-        gather_h(2, 0)
         transpose_h(2, 1)
         gather_h(2, 1)
+        gather_h(2, 0)
         transpose_x(5, both)
+        gate_mul(3, 1)
+        gate_mul(3, 0)
         gate_mul(3, 2)
         gate_mul(3, 3)
-        weigh_vector(4, 0)
+        weigh_vector(4)
+        squares(4, 1)
         squares(4, 2)
         squares(4, 3)
         project_mm(1, 0, 512, every)
-        store(1, 0, 512)
-        inv_rms(4, 0, H)
         project_mm(1, 512, 1024, every)
         store(1, 512, 1024)
+        inv_rms(4, 0, H)
+        store(1, 0, 512)
         scale_x(5, both)
-        gate(4, every)
-        widen_x(6, 0, False)
-        widen_x(6, 1, False)
-        gate_mul(4, 0)
-        gate_mul(4, 1)
+        gate(4, [2, 1, 3, 0], [1, 0, 2, 3])
+        widen_x(6)
         quant_h(2, both)
         quant_x(5, both)
-        weigh_gpsimd(5, 1)
-        weigh_gpsimd(5, 2)
-        weigh_gpsimd(5, 3)
+        weigh_gpsimd(5)
         squares(5, 0)
-        squares(5, 1)
         transpose_h(3, 0)
-        gather_h(3, 0)
         transpose_h(3, 1)
         gather_h(3, 1)
+        gather_h(3, 0)
         transpose_x(6, both)
+        gate_mul(4, 1)
+        gate_mul(4, 0)
         gate_mul(4, 2)
         gate_mul(4, 3)
-        weigh_vector(5, 0)
+        weigh_vector(5)
+        squares(5, 1)
         squares(5, 2)
         squares(5, 3)
         project_mm(2, 0, 512, every)
-        store(2, 0, 512)
-        inv_rms(5, 0, H)
         project_mm(2, 512, 1024, every)
         store(2, 512, 1024)
+        inv_rms(5, 0, H)
+        store(2, 0, 512)
         scale_x(6, both)
-        gate(5, every)
-        widen_x(7, 0, False)
-        widen_x(7, 1, False)
-        gate_mul(5, 0)
-        gate_mul(5, 1)
+        gate(5, [2, 1, 3, 0], [1, 0, 2, 3])
+        widen_x(7)
         quant_h(3, both)
         quant_x(6, both)
-        weigh_gpsimd(6, 1)
-        weigh_gpsimd(6, 2)
-        weigh_gpsimd(6, 3)
+        weigh_gpsimd(6)
         squares(6, 0)
-        squares(6, 1)
         transpose_h(4, 0)
-        gather_h(4, 0)
         transpose_h(4, 1)
         gather_h(4, 1)
+        gather_h(4, 0)
         transpose_x(7, both)
+        gate_mul(5, 1)
+        gate_mul(5, 0)
         gate_mul(5, 2)
         gate_mul(5, 3)
-        weigh_vector(6, 0)
+        weigh_vector(6)
+        squares(6, 1)
         squares(6, 2)
         squares(6, 3)
         project_mm(3, 0, 512, every)
-        store(3, 0, 512)
-        inv_rms(6, 0, H)
         project_mm(3, 512, 1024, every)
         store(3, 512, 1024)
+        inv_rms(6, 0, H)
+        store(3, 0, 512)
         scale_x(7, both)
-        gate(6, every)
-        gate_mul(6, 0)
+        gate(6, [2, 1, 3, 0], [1, 0, 2, 3])
         quant_h(4, both)
         quant_x(7, both)
-        weigh_gpsimd(7, 1)
-        weigh_gpsimd(7, 2)
-        weigh_gpsimd(7, 3)
+        weigh_gpsimd(7)
         squares(7, 0)
-        squares(7, 1)
         transpose_h(5, 0)
-        gather_h(5, 0)
         transpose_h(5, 1)
         gather_h(5, 1)
+        gather_h(5, 0)
         gate_mul(6, 1)
+        gate_mul(6, 0)
         gate_mul(6, 2)
         gate_mul(6, 3)
-        weigh_vector(7, 0)
+        weigh_vector(7)
+        squares(7, 1)
         squares(7, 2)
         squares(7, 3)
         project_mm(4, 0, 512, every)
-        store(4, 0, 512)
-        inv_rms(7, 0, H)
         project_mm(4, 512, 1024, every)
         store(4, 512, 1024)
-        gate(7, every)
+        inv_rms(7, 0, H)
+        store(4, 0, 512)
+        gate(7, [1, 0, 2, 3], [1, 0, 2, 3])
         quant_h(5, both)
         transpose_h(6, 0)
-        gather_h(6, 0)
         transpose_h(6, 1)
         gather_h(6, 1)
-        gate_mul(7, 0)
+        gather_h(6, 0)
         gate_mul(7, 1)
+        gate_mul(7, 0)
         gate_mul(7, 2)
         gate_mul(7, 3)
         project_mm(5, 0, 512, every)
-        store(5, 0, 512)
         project_mm(5, 512, 1024, every)
+        store(5, 0, 512)
         store(5, 512, 1024)
         quant_h(6, both)
         transpose_h(7, 0)

@@ -48,20 +48,20 @@ def tile_multiscaleretention_pc_w4_kernel(
             banks_used.append(tag)
             return psum.tile([P, 512], F32, name=tag, tag=tag)
 
-        wg_sc = const.tile([P, GX, F], U8, name="wg_sc", align_bytes=64)
-        wo_sc = const.tile([P, GH, E], U8, name="wo_sc", align_bytes=64)
+        wg_sc = const.tile([P, GX, F], U8, name="wg_sc", align_bytes=256)
+        wo_sc = const.tile([P, GH, E], U8, name="wo_sc", align_bytes=256)
         ident = const.tile([P, P], F32, name="ident")
         w_row = const.tile([P, DV], BF16, name="w_row")
         ones = const.tile([P, P], BF16, name="ones")
         gnw = const.tile([P, DV], BF16, name="gnw")
-        x_cuts = [(0, 2), (2, 4), (4, 8)]
+        x_cuts = [(0, 1), (1, 2), (2, 4), (4, 8)]
         x_tiles = [const.tile([P, b - a, E], U8, name="xbytes%d" % a) for a, b in x_cuts]
         o_first = [const.tile([P, F // 2], BF16, name="ofirst%d" % j) for j in range(2)]
         o_cuts = [(1, 2), (2, 3), (3, 4), (4, 8)]
         o_tiles = [const.tile([P, b - a, F], BF16, name="o%d" % a) for a, b in o_cuts]
-        wg = [const.tile([P, GX, F], U8, name="wg%d" % j, align_bytes=64) for j in range(2)]
-        wo = [const.tile([P, 2, 2 * E], U8, name="wo%d" % k, align_bytes=64) for k in range(2)]
-        shared = [const.tile([P, (H - 1) * DV], F32, name="shared%d" % j, align_bytes=64) for j in range(3)]
+        wg = [const.tile([P, GX, F], U8, name="wg%d" % j, align_bytes=256) for j in range(2)]
+        wo = [const.tile([P, 2, 2 * E], U8, name="wo%d" % k, align_bytes=256) for k in range(2)]
+        shared = [const.tile([P, (H - 1) * DV], F32, name="shared%d" % j, align_bytes=256) for j in range(3)]
         s4 = const.tile([P, GX, 4], F32, name="s4")
 
         nc.gpsimd.memset(w_row[:].bitcast(F32), 0.0)
@@ -97,15 +97,16 @@ def tile_multiscaleretention_pc_w4_kernel(
         load_x(0)
         nc.sync.dma_start(out=s4[:], in_=x_scale.rearrange("a b (g p t) -> p (a b g) t", p=P, t=4))
         nc.sync.dma_start(out=w_row[0:1, :], in_=gn_weight.rearrange("(a n) -> a n", a=1))
+        load_x(1)
         load_wg(0)
         load_o_first(0)
         load_scales(nc.sync, wg_sc, Wg_scales)
         load_o_first(1)
         load_wg(1)
-        load_x(1)
+        load_x(2)
         load_o(0)
         load_o(1)
-        load_x(2)
+        load_x(3)
         load_scales(nc.sync, wo_sc, Wo_scales)
         load_wo(0)
         load_wo(1)
@@ -158,8 +159,8 @@ def tile_multiscaleretention_pc_w4_kernel(
 
         def quant_x(i, passes):
             if passes[0] == 0:
-                xc[i] = work.tile([P, GX * P], U32, name="xc", tag="xc", align_bytes=64)
-                xsc[i] = work.tile([P, GX * P], U8, name="xsc", tag="xsc", align_bytes=64)
+                xc[i] = work.tile([P, GX * P], U32, name="xc", tag="xc", align_bytes=256)
+                xsc[i] = work.tile([P, GX * P], U8, name="xsc", tag="xsc", align_bytes=256)
             w = slice(P * passes[0], P * (passes[-1] + 1))
             nc.vector.quantize_mx(
                 out=xc[i][:, w].bitcast(FP8X4),
@@ -252,7 +253,7 @@ def tile_multiscaleretention_pc_w4_kernel(
 
         def gather_h(i, half, on_vector=False):
             if i not in hs:
-                hs[i] = work.tile([P, 2, 512], F32, name="hs", tag="hs", align_bytes=64)
+                hs[i] = work.tile([P, 2, 512], F32, name="hs", tag="hs", align_bytes=256)
             dst = hs[i][:, half].rearrange("p (g n u) -> p g n u", g=2, u=2)
             src = ht[i, half][:].rearrange("p (g u n) -> p g n u", g=2, u=2)
             if on_vector:
@@ -262,8 +263,8 @@ def tile_multiscaleretention_pc_w4_kernel(
 
         def quant_h(i, halves):
             if halves[0] == 0:
-                hc[i] = work.tile([P, GH * P], U32, name="hc", tag="hc", align_bytes=64)
-                hsc[i] = work.tile([P, GH * P], U8, name="hsc", tag="hsc", align_bytes=64)
+                hc[i] = work.tile([P, GH * P], U32, name="hc", tag="hc", align_bytes=256)
+                hsc[i] = work.tile([P, GH * P], U8, name="hsc", tag="hsc", align_bytes=256)
             w = slice(2 * P * halves[0], 2 * P * (halves[-1] + 1))
             nc.vector.quantize_mx(
                 out=hc[i][:, w].bitcast(FP8X4),
@@ -322,7 +323,7 @@ def tile_multiscaleretention_pc_w4_kernel(
         weigh_vector(0)
         scale_x(1, both)
         weigh_gpsimd(0)
-        gate(0, [0, 1, 3, 2], [0, 1, 2, 3])
+        gate(0, [0, 1, 2, 3], [0, 1, 2, 3])
         gate_mul(0, 0)
         gate_mul(0, 1)
         gate_mul(0, 2)
@@ -502,7 +503,8 @@ def tile_multiscaleretention_pc_w4_kernel(
         gather_h(7, 0)
         transpose_h(7, 1)
         gather_h(7, 1, on_vector=True)
-        quant_h(7, both)
+        quant_h(7, [0])
+        quant_h(7, [1])
         project_mm(6, 0, 512, every)
         store(6, 0, 512)
         project_mm(6, 512, 1024, every)

@@ -41,42 +41,40 @@ def tile_multiscaleretention_pc_w4_kernel(
         psum = ctx.enter_context(tc.psum_pool(name="psum", bufs=1))
         ctx.enter_context(tc.manual_schedule())
 
-        banks_used = []
+        free_banks = ["bank%d" % k for k in range(8)]
+        held = {}
 
-        def bank():
-            tag = "bank%d" % (len(banks_used) % 7)
-            banks_used.append(tag)
+        def take_bank(key, after=None):
+            tag = free_banks[0] if after is None else held[after]
+            free_banks.remove(tag)
+            held[key] = tag
             return psum.tile([P, 512], F32, name=tag, tag=tag)
+
+        def give_bank(key):
+            free_banks.append(held[key])
 
         wg_sc = const.tile([P, GX, F], U8, name="wg_sc", align_bytes=256)
         wo_sc = const.tile([P, GH, E], U8, name="wo_sc", align_bytes=256)
         ident = const.tile([P, P], F32, name="ident")
-        w_row = const.tile([P, DV], BF16, name="w_row")
-        ones = const.tile([P, P], BF16, name="ones")
+        w4 = const.tile([P, 4], BF16, name="w4")
         gnw = const.tile([P, DV], BF16, name="gnw")
-        x_cuts = [(0, 1), (1, 2), (2, 4), (4, 8)]
-        x_tiles = [const.tile([P, b - a, E], U8, name="xbytes%d" % a) for a, b in x_cuts]
-        o_first = [const.tile([P, F // 2], BF16, name="ofirst%d" % j) for j in range(2)]
+        x_cuts = [(0, 1), (1, 2), (2, 3), (3, 5), (5, 8)]
+        x_tiles = [const.tile([P, (b - a) * E], U8, name="xbytes%d" % a) for a, b in x_cuts]
+        o_halves = [[const.tile([P, F // 2], BF16, name="ohalf%d%d" % (i, j)) for j in range(2)] for i in range(1)]
         o_cuts = [(1, 2), (2, 3), (3, 4), (4, 8)]
         o_tiles = [const.tile([P, b - a, F], BF16, name="o%d" % a) for a, b in o_cuts]
         wg = [const.tile([P, GX, F], U8, name="wg%d" % j, align_bytes=256) for j in range(2)]
         wo = [const.tile([P, 2, 2 * E], U8, name="wo%d" % k, align_bytes=256) for k in range(2)]
-        shared = [const.tile([P, (H - 1) * DV], F32, name="shared%d" % j, align_bytes=256) for j in range(3)]
+        shared = [const.tile([P, F], F32, name="shared%d" % j, align_bytes=256) for j in range(3)]
         s4 = const.tile([P, GX, 4], F32, name="s4")
-
-        nc.gpsimd.memset(w_row[:].bitcast(F32), 0.0)
-        make_identity(nc, ident[:])
-        nc.vector.memset(wg_sc[:].rearrange("p g n -> p (g n)").bitcast(I32), 0)
-        nc.vector.memset(ones[:], 1.0)
-        nc.vector.memset(wo_sc[:].rearrange("p g n -> p (g n)").bitcast(I32), 0)
 
         def load_x(k):
             a, b = x_cuts[k]
-            nc.sync.dma_start(out=x_tiles[k][:], in_=x_view[:, a:b, :])
+            nc.sync.dma_start(out=x_tiles[k][:], in_=x_view[:, a:b, :].rearrange("p i e -> p (i e)"))
 
-        def load_scales(queue, sc, hbm):
+        def load_scales(sc, hbm):
             for r in range(4):
-                queue.dma_start(
+                nc.sync.dma_start(
                     out=sc[r:P:32, :, :].bitcast(I32),
                     in_=hbm[:, r:16:4, :].rearrange("g q n -> q g n").bitcast(I32),
                 )
@@ -91,47 +89,39 @@ def tile_multiscaleretention_pc_w4_kernel(
             a, b = o_cuts[k]
             nc.sync.dma_start(out=o_tiles[k][:], in_=o_view[:, a:b, :])
 
-        def load_o_first(j):
-            nc.sync.dma_start(out=o_first[j][:], in_=o_view[:, 0, F // 2 * j : F // 2 * (j + 1)])
+        def load_o_half(i, j):
+            nc.sync.dma_start(out=o_halves[i][j][:], in_=o_view[:, i, F // 2 * j : F // 2 * (j + 1)])
 
-        load_x(0)
-        nc.sync.dma_start(out=s4[:], in_=x_scale.rearrange("a b (g p t) -> p (a b g) t", p=P, t=4))
-        nc.sync.dma_start(out=w_row[0:1, :], in_=gn_weight.rearrange("(a n) -> a n", a=1))
-        load_x(1)
-        load_wg(0)
-        load_o_first(0)
-        load_scales(nc.sync, wg_sc, Wg_scales)
-        load_o_first(1)
-        load_wg(1)
-        load_x(2)
-        load_o(0)
-        load_o(1)
-        load_x(3)
-        load_scales(nc.sync, wo_sc, Wo_scales)
-        load_wo(0)
-        load_wo(1)
-        load_o(2)
-        load_o(3)
+        def load_s4():
+            nc.sync.dma_start(out=s4[:], in_=x_scale.rearrange("a b (g p t) -> p (a b g) t", p=P, t=4))
 
-        xb, xt, xc, xsc = {}, {}, {}, {}
-        ss, rr, ow0, hb, ht, hs, hc, hsc, gb, acc = {}, {}, {}, {}, {}, {}, {}, {}, {}, {}
+        def load_w():
+            nc.sync.dma_start(out=w4[:], in_=gn_weight.rearrange("(p t) -> p t", t=4))
+
+        def zero(sc):
+            nc.vector.memset(sc[:].rearrange("p g n -> p (g n)").bitcast(I32), 0)
+
+        xb, xt, xs, xc, xsc = {}, {}, {}, {}, {}
+        ss, rr, ow, hb, ht, hs, hc, hsc, gb, acc = {}, {}, {}, {}, {}, {}, {}, {}, {}, {}
 
         def o_cols(i, h, n=1):
-            if i == 0:
-                return o_first[h // 2][:, DV * (h % 2) : DV * (h % 2 + n)]
+            if i < len(o_halves):
+                return o_halves[i][h // 2][:, DV * (h % 2) : DV * (h % 2 + n)]
             k = max(k for k, (a, b) in enumerate(o_cuts) if a <= i)
             return o_tiles[k][:, i - o_cuts[k][0], DV * h : DV * (h + n)]
 
-        def widen_x(i, vector_cols=0):
+        def widen_x(i, n=1, vector_cols=0):
             k = max(k for k, (a, b) in enumerate(x_cuts) if a <= i)
-            src = x_tiles[k][:, i - x_cuts[k][0], :]
-            xb[i] = work.tile([P, E], BF16, name="xb", tag="xb")
+            src = x_tiles[k][:, E * (i - x_cuts[k][0]) : E * (i - x_cuts[k][0] + n)]
+            wide = work.tile([P, 2 * E], BF16, name="xb", tag="xb", bufs=3)
+            for j in range(n):
+                xb[i + j] = wide[:, E * j : E * (j + 1)]
             if vector_cols:
-                nc.vector.tensor_copy(out=xb[i][:, 0:vector_cols], in_=src[:, 0:vector_cols].bitcast(E4M3))
-            nc.scalar.copy(out=xb[i][:, vector_cols:E], in_=src[:, vector_cols:E].bitcast(E4M3))
+                nc.vector.tensor_copy(out=wide[:, 0:vector_cols], in_=src[:, 0:vector_cols].bitcast(E4M3))
+            nc.scalar.copy(out=wide[:, vector_cols : n * E], in_=src[:, vector_cols : n * E].bitcast(E4M3))
 
-        def transpose_x(i, passes):
-            b = bank()
+        def transpose_x(i, passes, after=None):
+            b = take_bank(("x", i, passes[0]), after)
             for j, g in enumerate(passes):
                 xt[i, g] = b
                 words = xb[i][:, 512 * g : 512 * (g + 1)].bitcast(F32)
@@ -139,14 +129,11 @@ def tile_multiscaleretention_pc_w4_kernel(
                     col = P * (len(passes) * u + j)
                     nc.tensor.transpose(b[:, col : col + P], words[:, u:256:2], ident[:])
 
-        def xs_view(i):
-            return shared[i % 3][:, 0 : E // 2].bitcast(BF16)
-
         def scale_x(i, passes):
             n = len(passes)
             g0 = passes[0]
             src = xt[i, g0][:, 0 : 256 * n].bitcast(BF16).rearrange("p (u g n e) -> p g n u e", u=2, g=n, e=2)
-            dst = xs_view(i)[:, 512 * g0 : 512 * (g0 + n)].rearrange("p (g n u e) -> p g n u e", g=n, u=2, e=2)
+            dst = xs[i][:, 512 * g0 : 512 * (g0 + n)].rearrange("p (g n u e) -> p g n u e", g=n, u=2, e=2)
             nc.vector.tensor_tensor(
                 out=dst,
                 in0=src,
@@ -156,24 +143,41 @@ def tile_multiscaleretention_pc_w4_kernel(
                 .to_broadcast([P, n, P, 2, 2]),
                 op=ALU.mult,
             )
+            give_bank(("x", i, g0))
 
-        def quant_x(i, passes):
-            if passes[0] == 0:
-                xc[i] = work.tile([P, GX * P], U32, name="xc", tag="xc", align_bytes=256)
-                xsc[i] = work.tile([P, GX * P], U8, name="xsc", tag="xsc", align_bytes=256)
-            w = slice(P * passes[0], P * (passes[-1] + 1))
-            nc.vector.quantize_mx(
-                out=xc[i][:, w].bitcast(FP8X4),
-                scales=xsc[i][:, w],
-                in_=xs_view(i)[:, 4 * w.start : 4 * w.stop],
-            )
+        def quantise(src, tag, bufs=3):
+            words = src.shape[1] // 4
+            codes = work.tile([P, words], U32, name=tag + "c", tag=tag + "c", bufs=bufs, align_bytes=256)
+            scales = work.tile([P, words], U8, name=tag + "s", tag=tag + "s", bufs=bufs, align_bytes=256)
+            nc.vector.quantize_mx(out=codes[:].bitcast(FP8X4), scales=scales[:], in_=src)
+            return codes, scales
 
-        def squares(i, h):
-            if h == 0:
-                ss[i] = work.tile([P, H], F32, name="ss", tag="ss", bufs=3)
-                rr[i] = work.tile([P, H], F32, name="rr", tag="rr", bufs=3)
-            junk = work.tile([P, DV], BF16, name="junk", tag="junk", bufs=4)
-            nc.scalar.activation(out=junk[:], in_=o_cols(i, h), func=ACT.Square, accum_out=ss[i][:, h : h + 1])
+        def note_passes(store_c, store_s, i, passes, codes, scales, first):
+            for j, g in enumerate(passes):
+                w = slice(first + P * j, first + P * (j + 1))
+                store_c[i, g] = codes[:, w]
+                store_s[i, g] = scales[:, w]
+
+        def quant_x(i, passes, tag):
+            codes, scales = quantise(xs[i][:, 512 * passes[0] : 512 * (passes[-1] + 1)], tag, 2)
+            note_passes(xc, xsc, i, passes, codes, scales, 0)
+
+        def quant_h(i, halves, tag):
+            codes, scales = quantise(hs[i][:, 512 * halves[0] : 512 * (halves[-1] + 1)].bitcast(BF16), tag)
+            note_passes(hc, hsc, i, list(range(2 * halves[0], 2 * halves[-1] + 2)), codes, scales, 0)
+
+        def quant_x_pair(i, src):
+            codes, scales = quantise(src.bitcast(BF16), "pair", 1)
+            note_passes(xc, xsc, i, [0, 1], codes, scales, 0)
+            note_passes(xc, xsc, i + 1, [0, 1], codes, scales, GX * P)
+
+        def squares(i, heads):
+            for h in heads:
+                if i not in ss:
+                    ss[i] = work.tile([P, H], F32, name="ss", tag="ss", bufs=4)
+                    rr[i] = work.tile([P, H], F32, name="rr", tag="rr", bufs=4)
+                junk = work.tile([P, DV], BF16, name="junk", tag="junk", bufs=4)
+                nc.scalar.activation(out=junk[:], in_=o_cols(i, h), func=ACT.Square, accum_out=ss[i][:, h : h + 1])
 
         def inv_rms(i, h0, h1):
             nc.scalar.activation(
@@ -186,106 +190,106 @@ def tile_multiscaleretention_pc_w4_kernel(
         def as_parity(cols):
             return cols.rearrange("p (u n e) -> p u n e", u=2, e=2)
 
-        w_bank = psum.tile([P, 512], F32, name="w_bank")
+        w_bank = take_bank("w")
 
         def spread_w():
-            nc.tensor.matmul(w_bank[:], lhsT=ones[:], rhs=by_parity(w_row[:]), start=True, stop=True)
-            nc.scalar.copy(out=gnw[:], in_=w_bank[:])
+            for u in range(2):
+                word = w4[:].bitcast(F32)[:, u : u + 1]
+                nc.tensor.transpose(w_bank[:, P * u : P * (u + 1)], word.to_broadcast([P, P]), ident[:])
 
-        def head_groups(i):
-            return [[(1, 2), (2, 3), (3, 4)], [(1, 2), (2, 4)]][i] if i < 2 else [(1, 4)]
+        def copy_w():
+            nc.scalar.copy(out=gnw[:].bitcast(F32), in_=w_bank[:, 0 : DV // 2])
 
-        def ow_head(i, h):
-            if h == 0:
-                return as_parity(ow0[i][:])
-            a, b = [(a, b) for a, b in head_groups(i) if a <= h < b][0]
-            return as_parity(shared[i % 3][:, DV * (a - 1) : DV * (b - 1)])[:, :, P * (h - a) : P * (h - a + 1), :]
+        def home(i):
+            return shared[i % 3]
 
-        def weigh_vector(i):
-            ow0[i] = work.tile([P, DV], F32, name="ow0", tag="ow0")
-            nc.vector.tensor_tensor(
-                out=ow_head(i, 0), in0=by_parity(o_cols(i, 0)), in1=as_parity(w_bank[:]), op=ALU.mult
-            )
+        def weigh_vector(i, h):
+            mine = work.tile([P, DV], F32, name="own", tag="own", bufs=4)
+            ow[i, h] = as_parity(mine[:])
+            nc.vector.tensor_tensor(out=ow[i, h], in0=by_parity(o_cols(i, h)), in1=as_parity(w_bank[:, 0 : DV // 2].bitcast(BF16)), op=ALU.mult)
 
-        def weigh_gpsimd(i):
+        def weigh_gpsimd(i, a, b, at=None, buf=None):
             w = gnw[:].rearrange("p (u c) -> p u c", u=2).unsqueeze(2)
-            for a, b in head_groups(i):
-                nc.gpsimd.tensor_tensor(
-                    out=shared[i % 3][:, DV * (a - 1) : DV * (b - 1)].rearrange("p (u h c) -> p u h c", u=2, h=b - a),
-                    in0=by_parity(o_cols(i, a, b - a)),
-                    in1=w.to_broadcast([P, 2, b - a, DV // 2]),
-                    op=ALU.mult,
-                )
+            first = a if at is None else at
+            dst = (home(i) if buf is None else buf)[:, DV * first : DV * (first + b - a)]
+            for h in range(a, b):
+                ow[i, h] = as_parity(dst)[:, :, P * (h - a) : P * (h - a + 1), :]
+            nc.gpsimd.tensor_tensor(
+                out=dst.rearrange("p (u h c) -> p u h c", u=2, h=b - a),
+                in0=by_parity(o_cols(i, a, b - a)),
+                in1=w.to_broadcast([P, 2, b - a, DV // 2]),
+                op=ALU.mult,
+            )
 
         def gate_mm(i, h, g):
             nc.tensor.matmul_mx(
                 out=gb[i, h][:],
-                lhsT=xc[i][:, P * g : P * (g + 1)].bitcast(FP8X4),
-                lhsT_scale=xsc[i][:, P * g : P * (g + 1)],
+                lhsT=xc[i, g].bitcast(FP8X4),
+                lhsT_scale=xsc[i, g],
                 rhs=wg[h // 2][:, g, 2 * DV * (h % 2) : 2 * DV * (h % 2 + 1)].bitcast(FP4X4),
                 rhs_scale=wg_sc[:, g, DV * h : DV * (h + 1)],
                 start=(g == 0),
                 stop=(g == GX - 1),
             )
 
-        def gate_mul(i, h):
-            hb[i, h] = work.tile([P, 2, 256], BF16, name="hb%d" % h, tag="hb%d" % h, bufs=3)
-            gv = by_parity(gb[i, h][:])
-            wv = ow_head(i, h)
-            for u in range(2):
-                nc.vector.scalar_tensor_tensor(
-                    out=hb[i, h][:, u].rearrange("p (n e) -> p n e", e=2),
-                    in0=gv[:, u],
-                    scalar=rr[i][:, h : h + 1],
-                    in1=wv[:, u],
-                    op0=ALU.mult,
-                    op1=ALU.mult,
-                )
+        def gate(i, heads, after=None):
+            for n, h in enumerate(heads):
+                gb[i, h] = take_bank(("g", i, h), None if after is None else after[n])
+                for g in range(GX):
+                    gate_mm(i, h, g)
 
-        def transpose_h(i, half):
-            ht[i, half] = bank()
-            for j in range(2):
+        def gate_mul(i, heads):
+            for h in heads:
+                hb[i, h] = work.tile([P, 2, 256], BF16, name="hb%d" % h, tag="hb%d" % h, bufs=3)
+                gv = by_parity(gb[i, h][:])
                 for u in range(2):
-                    col = P * (2 * j + u)
-                    nc.tensor.transpose(
-                        ht[i, half][:, col : col + P], hb[i, 2 * half + j][:, u].bitcast(F32), ident[:]
+                    nc.vector.scalar_tensor_tensor(
+                        out=hb[i, h][:, u].rearrange("p (n e) -> p n e", e=2),
+                        in0=gv[:, u],
+                        scalar=rr[i][:, h : h + 1],
+                        in1=ow[i, h][:, u],
+                        op0=ALU.mult,
+                        op1=ALU.mult,
                     )
+                give_bank(("g", i, h))
+
+        def transpose_h(i, halves, after=None):
+            for n, half in enumerate(halves):
+                ht[i, half] = take_bank(("h", i, half), None if after is None else after[n])
+                for j in range(2):
+                    for u in range(2):
+                        col = P * (2 * j + u)
+                        nc.tensor.transpose(
+                            ht[i, half][:, col : col + P], hb[i, 2 * half + j][:, u].bitcast(F32), ident[:]
+                        )
 
         def gather_h(i, half, on_vector=False):
             if i not in hs:
-                hs[i] = work.tile([P, 2, 512], F32, name="hs", tag="hs", align_bytes=256)
-            dst = hs[i][:, half].rearrange("p (g n u) -> p g n u", g=2, u=2)
+                hs[i] = work.tile([P, F // 2], F32, name="hs", tag="hs", align_bytes=256)[:]
+            dst = hs[i][:, 512 * half : 512 * (half + 1)].rearrange("p (g n u) -> p g n u", g=2, u=2)
             src = ht[i, half][:].rearrange("p (g u n) -> p g n u", g=2, u=2)
             if on_vector:
                 nc.vector.tensor_copy(out=dst, in_=src)
             else:
                 nc.scalar.copy(out=dst, in_=src)
+            give_bank(("h", i, half))
 
-        def quant_h(i, halves):
-            if halves[0] == 0:
-                hc[i] = work.tile([P, GH * P], U32, name="hc", tag="hc", align_bytes=256)
-                hsc[i] = work.tile([P, GH * P], U8, name="hsc", tag="hsc", align_bytes=256)
-            w = slice(2 * P * halves[0], 2 * P * (halves[-1] + 1))
-            nc.vector.quantize_mx(
-                out=hc[i][:, w].bitcast(FP8X4),
-                scales=hsc[i][:, w],
-                in_=hs[i][:, halves[0] : halves[-1] + 1].rearrange("p a n -> p (a n)").bitcast(BF16),
-            )
-
-        def project_mm(i, c0, c1, passes):
-            if passes[0] == 0:
-                acc[i, c0] = bank()
-            for g in passes:
-                w = slice(P * g, P * (g + 1))
+        def project_mm(i, c0, c1, after=None):
+            acc[i, c0] = take_bank(("p", i, c0), after)
+            for g in range(GH):
                 nc.tensor.matmul_mx(
                     out=acc[i, c0][:, 0 : c1 - c0],
-                    lhsT=hc[i][:, w].bitcast(FP8X4),
-                    lhsT_scale=hsc[i][:, w],
+                    lhsT=hc[i, g].bitcast(FP8X4),
+                    lhsT_scale=hsc[i, g],
                     rhs=wo[g // 2][:, g % 2, 2 * c0 : 2 * c1].bitcast(FP4X4),
                     rhs_scale=wo_sc[:, g, c0:c1],
                     start=(g == 0),
                     stop=(g == GH - 1),
                 )
+
+        def project(i):
+            project_mm(i, 0, 512)
+            project_mm(i, 512, 1024)
 
         def store(i, c0, c1, on_vector=False):
             res = work.tile([P, 512], F32, name="res", tag="res", bufs=6)
@@ -293,225 +297,142 @@ def tile_multiscaleretention_pc_w4_kernel(
                 nc.vector.tensor_copy(out=res[:, 0 : c1 - c0], in_=acc[i, c0][:, 0 : c1 - c0])
             else:
                 nc.scalar.copy(out=res[:, 0 : c1 - c0], in_=acc[i, c0][:, 0 : c1 - c0])
+            give_bank(("p", i, c0))
             nc.sync.dma_start(out=out_view[i][:, c0:c1], in_=res[:, 0 : c1 - c0])
 
         both = [0, 1]
         every = [0, 1, 2, 3]
+        for i in range(3, NT):
+            xs[i] = home(i)[:, DV : 2 * DV].bitcast(BF16)
+        xs[0] = home(0)[:, 2 * DV : 3 * DV].bitcast(BF16)
+        xs[1] = home(1)[:, DV : 2 * DV].bitcast(BF16)
+        xs[2] = home(1)[:, 2 * DV : 3 * DV].bitcast(BF16)
 
-        def gate(i, heads, banks_for=()):
-            for h in banks_for:
-                gb[i, h] = bank()
-            for h in heads:
-                for g in range(GX):
-                    gate_mm(i, h, g)
+        nc.vector.memset(ident[:], 0.0)
+        make_identity(nc, ident[:], nomemset=True)
+        zero(wg_sc)
+        zero(wo_sc)
 
-        widen_x(0, 512)
-        widen_x(1, 512)
+        load_x(0)
+        load_w()
+        load_s4()
+        load_x(1)
+        load_o_half(0, 0)
+        load_x(2)
+        load_o_half(0, 1)
+        load_scales(wg_sc, Wg_scales)
+        load_wg(0)
+        load_wg(1)
+        load_o(0)
+        load_x(3)
+        load_o(1)
+        load_scales(wo_sc, Wo_scales)
+        load_wo(0)
+        load_wo(1)
+        load_o(2)
+        load_x(4)
+        load_o(3)
+
+        spread_w()
+        widen_x(0, 1, 512)
+        widen_x(1, 1, 768)
+        copy_w()
+        widen_x(2)
         transpose_x(0, [0])
         transpose_x(0, [1])
-        spread_w()
         transpose_x(1, both)
         scale_x(0, [0])
         scale_x(0, [1])
-        quant_x(0, both)
-        squares(0, 0)
-        squares(0, 1)
-        inv_rms(0, 0, 2)
-        squares(0, 2)
-        squares(0, 3)
-        inv_rms(0, 2, 4)
-        weigh_vector(0)
-        scale_x(1, both)
-        weigh_gpsimd(0)
-        gate(0, [0, 1, 2, 3], [0, 1, 2, 3])
-        gate_mul(0, 0)
-        gate_mul(0, 1)
-        gate_mul(0, 2)
-        widen_x(2)
-        quant_x(1, both)
-        weigh_gpsimd(1)
-        squares(1, 0)
-        squares(1, 1)
-        gate_mul(0, 3)
-        weigh_vector(1)
-        squares(1, 2)
-        squares(1, 3)
-        inv_rms(1, 0, H)
         transpose_x(2, both)
+        weigh_gpsimd(0, 0, 1)
+        squares(0, [0, 1, 2])
+        inv_rms(0, 0, 2)
+        weigh_vector(0, 1)
+        quant_x(0, both, "x")
+        weigh_gpsimd(0, 2, 4)
+        scale_x(1, both)
+        squares(0, [3])
         scale_x(2, both)
-        gate(1, [1, 0], [0, 1, 2, 3])
-        widen_x(3)
-        gate_mul(1, 0)
-        gate_mul(1, 1)
-        quant_x(2, both)
-        weigh_gpsimd(2)
-        squares(2, 0)
-        squares(2, 1)
-        transpose_h(0, 0)
-        transpose_h(0, 1)
-        gather_h(0, 1)
-        gather_h(0, 0)
+        gate(0, every)
+        squares(1, [0])
+        inv_rms(0, 2, 4)
+        gate_mul(0, [0])
+        quant_x_pair(1, home(1)[:, DV : 3 * DV])
+        weigh_gpsimd(1, 1, 4)
+        weigh_gpsimd(2, 1, H)
+        gate(1, [0, 1])
+        gate_mul(0, [1, 2])
         gate(1, [2, 3])
-        transpose_x(3, both)
-        gate_mul(1, 3)
-        gate_mul(1, 2)
-        weigh_vector(2)
-        inv_rms(2, 0, 2)
+        weigh_vector(1, 0)
+        gate_mul(0, [3])
+        squares(1, [1, 2, 3])
+        widen_x(3)
+        inv_rms(1, 0, H)
         widen_x(4)
-        squares(2, 2)
-        squares(2, 3)
-        inv_rms(2, 2, 4)
+        transpose_h(0, both)
+        gate_mul(1, [0])
+        weigh_vector(2, 0)
+        transpose_x(3, both)
+        gather_h(0, 0)
+        gather_h(0, 1)
+        gate(2, [0, 1, 2])
+        gate_mul(1, [1])
+        gate(2, [3])
         scale_x(3, both)
-        gate(2, [1, 0], [0, 1, 2, 3])
-        gate_mul(2, 0)
-        quant_h(0, both)
-        quant_x(3, both)
-        weigh_gpsimd(3)
-        squares(3, 0)
-        squares(3, 1)
-        transpose_h(1, 0)
-        transpose_h(1, 1)
-        gather_h(1, 1)
-        gather_h(1, 0)
-        gate(2, [3, 2])
         transpose_x(4, both)
-        gate_mul(2, 1)
-        gate_mul(2, 2)
-        gate_mul(2, 3)
-        weigh_vector(3)
-        squares(3, 2)
-        squares(3, 3)
-        project_mm(0, 0, 512, every)
-        project_mm(0, 512, 1024, every)
-        store(0, 512, 1024)
-        inv_rms(3, 0, H)
-        store(0, 0, 512)
-        scale_x(4, both)
-        gate(3, [2, 1, 3, 0], [1, 0, 2, 3])
-        widen_x(5)
-        quant_h(1, both)
-        quant_x(4, both)
-        weigh_gpsimd(4)
-        squares(4, 0)
-        transpose_h(2, 0)
-        transpose_h(2, 1)
-        gather_h(2, 1)
-        gather_h(2, 0)
-        transpose_x(5, both)
-        gate_mul(3, 1)
-        gate_mul(3, 0)
-        gate_mul(3, 2)
-        gate_mul(3, 3)
-        weigh_vector(4)
-        squares(4, 1)
-        squares(4, 2)
-        squares(4, 3)
-        project_mm(1, 0, 512, every)
-        project_mm(1, 512, 1024, every)
-        store(1, 512, 1024)
-        inv_rms(4, 0, H)
-        store(1, 0, 512)
-        scale_x(5, both)
-        gate(4, [2, 1, 3, 0], [1, 0, 2, 3])
-        widen_x(6)
-        quant_h(2, both)
-        quant_x(5, both)
-        weigh_gpsimd(5)
-        squares(5, 0)
-        transpose_h(3, 0)
-        transpose_h(3, 1)
-        gather_h(3, 1)
-        gather_h(3, 0)
-        transpose_x(6, both)
-        gate_mul(4, 1)
-        gate_mul(4, 0)
-        gate_mul(4, 2)
-        gate_mul(4, 3)
-        weigh_vector(5)
-        squares(5, 1)
-        squares(5, 2)
-        squares(5, 3)
-        project_mm(2, 0, 512, every)
-        project_mm(2, 512, 1024, every)
-        store(2, 512, 1024)
-        inv_rms(5, 0, H)
-        store(2, 0, 512)
-        scale_x(6, both)
-        gate(5, [2, 1, 3, 0], [1, 0, 2, 3])
-        widen_x(7)
-        quant_h(3, both)
-        quant_x(6, both)
-        weigh_gpsimd(6)
-        squares(6, 0)
-        transpose_h(4, 0)
-        transpose_h(4, 1)
-        gather_h(4, 1)
-        gather_h(4, 0)
-        transpose_x(7, both)
-        gate_mul(5, 1)
-        gate_mul(5, 0)
-        gate_mul(5, 2)
-        gate_mul(5, 3)
-        weigh_vector(6)
-        squares(6, 1)
-        squares(6, 2)
-        squares(6, 3)
-        project_mm(3, 0, 512, every)
-        project_mm(3, 512, 1024, every)
-        store(3, 512, 1024)
-        inv_rms(6, 0, H)
-        store(3, 0, 512)
-        scale_x(7, both)
-        gate(6, [2, 1, 3, 0], [1, 0, 2, 3])
-        quant_h(4, both)
-        quant_x(7, both)
-        weigh_gpsimd(7)
-        squares(7, 0)
-        transpose_h(5, 0)
-        transpose_h(5, 1)
-        gather_h(5, 1)
-        gather_h(5, 0)
-        gate_mul(6, 1)
-        gate_mul(6, 0)
-        gate_mul(6, 2)
-        gate_mul(6, 3)
-        weigh_vector(7)
-        squares(7, 1)
-        squares(7, 2)
-        squares(7, 3)
-        project_mm(4, 0, 512, every)
-        project_mm(4, 512, 1024, every)
-        store(4, 512, 1024)
-        inv_rms(7, 0, H)
-        store(4, 0, 512)
-        gate(7, [1, 0, 2, 3], [1, 0, 2, 3])
-        quant_h(5, both)
-        transpose_h(6, 0)
-        transpose_h(6, 1)
-        gather_h(6, 1)
-        gather_h(6, 0)
-        gate_mul(7, 1)
-        gate_mul(7, 0)
-        gate_mul(7, 2)
-        gate_mul(7, 3)
-        project_mm(5, 0, 512, every)
-        project_mm(5, 512, 1024, every)
-        store(5, 0, 512)
-        store(5, 512, 1024)
-        quant_h(6, both)
-        transpose_h(7, 0)
+        gate_mul(1, [2, 3])
+        squares(2, every)
+        transpose_h(1, both)
+        gather_h(1, 0)
+        inv_rms(2, 0, H)
+        gather_h(1, 1)
+        for k in range(1, 7):
+            order = [1, 0, 2, 3] if k > 1 else every
+            behind = k < 2
+            if k > 1:
+                transpose_h(k, both)
+                if k + 3 < NT:
+                    transpose_x(k + 3, both)
+                for half in both if behind else [1, 0]:
+                    gather_h(k, half)
+            quant_h(k - 1, both, "he")
+            if k + 2 < NT:
+                quant_x(k + 2, both, "x")
+                weigh_gpsimd(k + 2, 1, H)
+            gate_mul(k + 1, order)
+            heads = [("g", k + 1, h) for h in order]
+            turned = [("h", k, 0), ("h", k, 1)]
+            first = turned + heads if behind else heads[:2] + turned + heads[2:]
+            project_mm(k - 1, 0, 512, first[0])
+            project_mm(k - 1, 512, 1024, first[1])
+            if k + 2 < NT:
+                squares(k + 2, [1, 2, 3] if k > 1 else every)
+                gate(k + 2, [1, 2, 3, 0] if behind else [2, 1, 3, 0], first[2:])
+                weigh_vector(k + 2, 0)
+            if k + 3 < NT:
+                scale_x(k + 3, both)
+            store(k - 1, 512, 1024)
+            if k + 2 < NT:
+                inv_rms(k + 2, 0, H)
+            store(k - 1, 0, 512)
+            if k + 4 < NT:
+                widen_x(k + 4)
+            if k + 3 < NT:
+                squares(k + 3, [0])
+        quant_h(6, both, "he")
+        transpose_h(7, [0])
         gather_h(7, 0)
-        transpose_h(7, 1)
-        gather_h(7, 1, on_vector=True)
-        quant_h(7, [0])
-        quant_h(7, [1])
-        project_mm(6, 0, 512, every)
+        transpose_h(7, [1])
+        gather_h(7, 1, True)
+        quant_h(7, [0], "h7a")
+        quant_h(7, [1], "h7b")
+        project_mm(6, 0, 512)
         store(6, 0, 512)
-        project_mm(6, 512, 1024, every)
+        project_mm(6, 512, 1024)
         store(6, 512, 1024)
-        project_mm(7, 0, 512, every)
+        project_mm(7, 0, 512)
         store(7, 0, 512)
-        project_mm(7, 512, 768, every)
-        store(7, 512, 768, on_vector=True)
-        project_mm(7, 768, 1024, every)
+        project_mm(7, 512, 768)
+        store(7, 512, 768, True)
+        project_mm(7, 768, 1024)
         store(7, 768, 1024)

@@ -53,7 +53,7 @@ def tile_multiscaleretention_pc_w4_kernel(
         def give_bank(key):
             free_banks.append(held[key])
 
-        wg_sc = const.tile([P, GX, F], U8, name="wg_sc", align_bytes=256)
+        wg_sc = [const.tile([P, GX, F // 2], U8, name="wg_sc%d" % j, align_bytes=256) for j in range(2)]
         wo_sc = const.tile([P, GH, E], U8, name="wo_sc", align_bytes=256)
         ident = const.tile([P, P], F32, name="ident")
         w4 = const.tile([P, 4], BF16, name="w4")
@@ -78,6 +78,9 @@ def tile_multiscaleretention_pc_w4_kernel(
                     out=sc[r:P:32, :, :].bitcast(I32),
                     in_=hbm[:, r:16:4, :].rearrange("g q n -> q g n").bitcast(I32),
                 )
+
+        def load_wg_scales(j):
+            load_scales(wg_sc[j], Wg_scales[:, :, F // 2 * j : F // 2 * (j + 1)])
 
         def load_wg(j):
             nc.sync.dma_start(out=wg[j][:], in_=wg_view[:, :, F * j : F * (j + 1)])
@@ -227,7 +230,7 @@ def tile_multiscaleretention_pc_w4_kernel(
                 lhsT=xc[i, g].bitcast(FP8X4),
                 lhsT_scale=xsc[i, g],
                 rhs=wg[h // 2][:, g, 2 * DV * (h % 2) : 2 * DV * (h % 2 + 1)].bitcast(FP4X4),
-                rhs_scale=wg_sc[:, g, DV * h : DV * (h + 1)],
+                rhs_scale=wg_sc[h // 2][:, g, DV * (h % 2) : DV * (h % 2 + 1)],
                 start=(g == 0),
                 stop=(g == GX - 1),
             )
@@ -310,7 +313,8 @@ def tile_multiscaleretention_pc_w4_kernel(
 
         nc.vector.memset(ident[:], 0.0)
         make_identity(nc, ident[:], nomemset=True)
-        zero(wg_sc)
+        zero(wg_sc[0])
+        zero(wg_sc[1])
         zero(wo_sc)
 
         load_x(0)
@@ -320,10 +324,11 @@ def tile_multiscaleretention_pc_w4_kernel(
         load_o_half(0, 0)
         load_x(2)
         load_o_half(0, 1)
-        load_scales(wg_sc, Wg_scales)
+        load_wg_scales(0)
         load_wg(0)
-        load_wg(1)
         load_o(0)
+        load_wg_scales(1)
+        load_wg(1)
         load_x(3)
         load_o(1)
         load_scales(wo_sc, Wo_scales)
@@ -369,6 +374,7 @@ def tile_multiscaleretention_pc_w4_kernel(
         widen_x(3)
         inv_rms(1, 0, H)
         widen_x(4)
+        squares(2, [0])
         transpose_h(0, both)
         gate_mul(1, [0])
         weigh_vector(2, 0)
@@ -379,16 +385,18 @@ def tile_multiscaleretention_pc_w4_kernel(
         gate_mul(1, [1])
         gate(2, [3])
         scale_x(3, both)
+        transpose_h(1, [0])
+        gate_mul(1, [2])
         transpose_x(4, both)
-        gate_mul(1, [2, 3])
-        squares(2, every)
-        transpose_h(1, both)
+        gate_mul(1, [3])
+        squares(2, [1, 2, 3])
+        transpose_h(1, [1])
         gather_h(1, 0)
         inv_rms(2, 0, H)
         gather_h(1, 1)
         for k in range(1, 7):
             order = [1, 0, 2, 3] if k > 1 else every
-            behind = k < 2
+            behind = k < 3
             if k > 1:
                 transpose_h(k, both)
                 if k + 3 < NT:
@@ -406,7 +414,7 @@ def tile_multiscaleretention_pc_w4_kernel(
             project_mm(k - 1, 0, 512, first[0])
             project_mm(k - 1, 512, 1024, first[1])
             if k + 2 < NT:
-                squares(k + 2, [1, 2, 3] if k > 1 else every)
+                squares(k + 2, every if behind else [1, 2, 3])
                 gate(k + 2, [1, 2, 3, 0] if behind else [2, 1, 3, 0], first[2:])
                 weigh_vector(k + 2, 0)
             if k + 3 < NT:
@@ -417,7 +425,7 @@ def tile_multiscaleretention_pc_w4_kernel(
             store(k - 1, 0, 512)
             if k + 4 < NT:
                 widen_x(k + 4)
-            if k + 3 < NT:
+            if k + 3 < NT and k > 1:
                 squares(k + 3, [0])
         quant_h(6, both, "he")
         transpose_h(7, [0])
@@ -434,5 +442,7 @@ def tile_multiscaleretention_pc_w4_kernel(
         store(7, 0, 512)
         project_mm(7, 512, 768)
         store(7, 512, 768, True)
-        project_mm(7, 768, 1024)
-        store(7, 768, 1024)
+        project_mm(7, 768, 896)
+        store(7, 768, 896)
+        project_mm(7, 896, 1024)
+        store(7, 896, 1024, True)

@@ -92,6 +92,10 @@ def tile_multiscaleretention_pc_w4_kernel(
             a, b = o_cuts[k]
             nc.sync.dma_start(out=o_tiles[k][:], in_=o_view[:, a:b, :])
 
+        def load_o_second(j):
+            cols = slice(F // 2 * j, F // 2 * (j + 1))
+            nc.sync.dma_start(out=o_tiles[0][:, 0, cols], in_=o_view[:, 1, cols])
+
         def load_o_half(i, j):
             nc.sync.dma_start(out=o_halves[i][j][:], in_=o_view[:, i, F // 2 * j : F // 2 * (j + 1)])
 
@@ -203,13 +207,19 @@ def tile_multiscaleretention_pc_w4_kernel(
         def copy_w():
             nc.scalar.copy(out=gnw[:].bitcast(F32), in_=w_bank[:, 0 : DV // 2])
 
+        def warm_up(n):
+            idle = take_bank("warm")
+            for j in range(n):
+                nc.tensor.matmul(idle[:, P * j : P * (j + 1)], lhsT=ident[:], rhs=ident[:], start=True, stop=True)
+            give_bank("warm")
+
         def home(i):
             return shared[i % 3]
 
-        def weigh_vector(i, h):
+        def weigh_vector(i, h, w=None):
             mine = work.tile([P, DV], F32, name="own", tag="own", bufs=4)
             ow[i, h] = as_parity(mine[:])
-            nc.vector.tensor_tensor(out=ow[i, h], in0=by_parity(o_cols(i, h)), in1=as_parity(w_bank[:, 0 : DV // 2].bitcast(BF16)), op=ALU.mult)
+            nc.vector.tensor_tensor(out=ow[i, h], in0=by_parity(o_cols(i, h)), in1=as_parity(w_bank[:, 0 : DV // 2].bitcast(BF16) if w is None else w[:]), op=ALU.mult)
 
         def weigh_gpsimd(i, a, b, at=None, buf=None):
             w = gnw[:].rearrange("p (u c) -> p u c", u=2).unsqueeze(2)
@@ -326,9 +336,10 @@ def tile_multiscaleretention_pc_w4_kernel(
         load_o_half(0, 1)
         load_wg_scales(0)
         load_wg(0)
-        load_o(0)
+        load_o_second(0)
         load_wg_scales(1)
         load_wg(1)
+        load_o_second(1)
         load_x(3)
         load_o(1)
         load_scales(wo_sc, Wo_scales)
@@ -378,57 +389,71 @@ def tile_multiscaleretention_pc_w4_kernel(
         transpose_h(0, both)
         gate_mul(1, [0])
         weigh_vector(2, 0)
+        give_bank("w")
         transpose_x(3, both)
         gather_h(0, 0)
         gather_h(0, 1)
         gate(2, [0, 1, 2])
         gate_mul(1, [1])
-        gate(2, [3])
-        scale_x(3, both)
         transpose_h(1, [0])
-        gate_mul(1, [2])
+        scale_x(3, both)
         transpose_x(4, both)
+        gate_mul(1, [2])
+        gate(2, [3])
         gate_mul(1, [3])
         squares(2, [1, 2, 3])
         transpose_h(1, [1])
         gather_h(1, 0)
         inv_rms(2, 0, H)
         gather_h(1, 1)
-        for k in range(1, 7):
-            order = [1, 0, 2, 3] if k > 1 else every
-            behind = k < 3
+        for k in range(1, 5):
             if k > 1:
                 transpose_h(k, both)
-                if k + 3 < NT:
-                    transpose_x(k + 3, both)
-                for half in both if behind else [1, 0]:
-                    gather_h(k, half)
+                transpose_x(k + 3, both)
+                gather_h(k, 1)
+                gather_h(k, 0)
             quant_h(k - 1, both, "he")
-            if k + 2 < NT:
-                quant_x(k + 2, both, "x")
-                weigh_gpsimd(k + 2, 1, H)
-            gate_mul(k + 1, order)
-            heads = [("g", k + 1, h) for h in order]
-            turned = [("h", k, 0), ("h", k, 1)]
-            first = turned + heads if behind else heads[:2] + turned + heads[2:]
-            project_mm(k - 1, 0, 512, first[0])
-            project_mm(k - 1, 512, 1024, first[1])
-            if k + 2 < NT:
-                squares(k + 2, every if behind else [1, 2, 3])
-                gate(k + 2, [1, 2, 3, 0] if behind else [2, 1, 3, 0], first[2:])
-                weigh_vector(k + 2, 0)
-            if k + 3 < NT:
-                scale_x(k + 3, both)
+            weigh_vector(k + 2, 0, gnw)
+            quant_x(k + 2, both, "x")
+            weigh_gpsimd(k + 2, 1, H)
+            project_mm(k - 1, 0, 512)
+            project_mm(k - 1, 512, 1024)
+            gate_mul(k + 1, [1, 0, 2, 3] if k > 1 else every)
+            squares(k + 2, [1, 2, 3] if k > 1 else every)
+            gate(k + 2, [2, 1, 3, 0])
+            scale_x(k + 3, both)
             store(k - 1, 512, 1024)
-            if k + 2 < NT:
-                inv_rms(k + 2, 0, H)
+            inv_rms(k + 2, 0, H)
             store(k - 1, 0, 512)
             if k + 4 < NT:
                 widen_x(k + 4)
-            if k + 3 < NT and k > 1:
-                squares(k + 3, [0])
+            squares(k + 3, [0])
+        quant_h(4, both, "he")
+        weigh_vector(7, 0, gnw)
+        quant_x(7, both, "x")
+        weigh_gpsimd(7, 1, H)
+        gate_mul(6, [1, 0])
+        project(4)
+        gate_mul(6, [2, 3])
+        squares(7, [1, 2, 3])
+        transpose_h(5, both)
+        store(4, 0, 512)
+        inv_rms(7, 0, H)
+        transpose_h(6, both)
+        gather_h(5, 1)
+        gather_h(5, 0)
+        gate(7, [1, 0])
+        store(4, 512, 1024)
+        gate(7, [2, 3])
+        gather_h(6, 1)
+        gather_h(6, 0)
+        quant_h(5, both, "he")
+        project(5)
+        gate_mul(7, [1, 0, 2, 3])
+        store(5, 0, 512)
         quant_h(6, both, "he")
         transpose_h(7, [0])
+        store(5, 512, 1024)
         gather_h(7, 0)
         transpose_h(7, [1])
         gather_h(7, 1, True)

@@ -407,20 +407,22 @@ def tile_multiscaleretention_pc_w4_kernel(
         inv_rms(2, 0, H)
         gather_h(1, 1)
         for k in range(1, 5):
+            order = [1, 0, 2, 3] if k > 1 else every
             if k > 1:
-                transpose_h(k, both)
-                transpose_x(k + 3, both)
+                transpose_h(k, both, [("g", k, 3), ("p", k - 2, 0)])
+                transpose_x(k + 3, both, ("p", k - 2, 512))
                 gather_h(k, 1)
                 gather_h(k, 0)
+            turned = [("h", k, 1), ("h", k, 0)] if k > 1 else [("h", k, 0), ("h", k, 1)]
             quant_h(k - 1, both, "he")
             weigh_vector(k + 2, 0, gnw)
             quant_x(k + 2, both, "x")
             weigh_gpsimd(k + 2, 1, H)
-            project_mm(k - 1, 0, 512)
-            project_mm(k - 1, 512, 1024)
-            gate_mul(k + 1, [1, 0, 2, 3] if k > 1 else every)
+            project_mm(k - 1, 0, 512, ("x", k + 2, 0) if k > 1 else None)
+            project_mm(k - 1, 512, 1024, turned[1])
+            gate_mul(k + 1, order)
             squares(k + 2, [1, 2, 3] if k > 1 else every)
-            gate(k + 2, [2, 1, 3, 0])
+            gate(k + 2, [2, 1, 3, 0], [turned[0]] + [("g", k + 1, h) for h in order[:3]])
             scale_x(k + 3, both)
             store(k - 1, 512, 1024)
             inv_rms(k + 2, 0, H)
@@ -432,42 +434,43 @@ def tile_multiscaleretention_pc_w4_kernel(
         weigh_vector(7, 0, gnw)
         quant_x(7, both, "x")
         weigh_gpsimd(7, 1, H)
-        gate_mul(6, [1, 0])
-        project(4)
-        gate_mul(6, [2, 3])
+        project_mm(4, 0, 512, ("g", 5, 3))
+        project_mm(4, 512, 1024, ("x", 7, 0))
+        gate_mul(6, [1, 0, 2, 3])
         squares(7, [1, 2, 3])
-        transpose_h(5, both)
+        transpose_h(5, both, [("p", 3, 0), ("p", 3, 512)])
         store(4, 0, 512)
         inv_rms(7, 0, H)
-        transpose_h(6, both)
+        transpose_h(6, both, [("g", 6, 0), ("g", 6, 2)])
         gather_h(5, 1)
         gather_h(5, 0)
-        gate(7, [1, 0])
+        gate(7, [1, 0], [("g", 6, 1), ("g", 6, 3)])
+        gate(7, [3, 2], [("p", 4, 0), ("h", 5, 0)])
         store(4, 512, 1024)
-        gate(7, [2, 3])
         gather_h(6, 1)
         gather_h(6, 0)
         quant_h(5, both, "he")
-        project(5)
-        gate_mul(7, [1, 0, 2, 3])
+        project_mm(5, 0, 512, ("h", 5, 1))
+        project_mm(5, 512, 1024, ("h", 6, 1))
+        gate_mul(7, [1, 0, 3, 2])
         store(5, 0, 512)
         quant_h(6, both, "he")
-        transpose_h(7, [0])
+        transpose_h(7, [0], [("g", 7, 0)])
         store(5, 512, 1024)
         gather_h(7, 0)
-        transpose_h(7, [1])
+        transpose_h(7, [1], [("g", 7, 2)])
         gather_h(7, 1, True)
         quant_h(7, [0], "h7a")
         quant_h(7, [1], "h7b")
-        project_mm(6, 0, 512)
+        project_mm(6, 0, 512, ("g", 7, 1))
         store(6, 0, 512)
-        project_mm(6, 512, 1024)
+        project_mm(6, 512, 1024, ("g", 7, 3))
         store(6, 512, 1024)
-        project_mm(7, 0, 512)
+        project_mm(7, 0, 512, ("p", 4, 512))
         store(7, 0, 512)
-        project_mm(7, 512, 768)
+        project_mm(7, 512, 768, ("h", 6, 0))
         store(7, 512, 768, True)
-        project_mm(7, 768, 896)
+        project_mm(7, 768, 896, ("h", 7, 1))
         store(7, 768, 896)
-        project_mm(7, 896, 1024)
+        project_mm(7, 896, 1024, ("h", 7, 0))
         store(7, 896, 1024, True)

@@ -430,35 +430,35 @@ def tile_multiscaleretention_pc_w4_kernel(
             if k + 4 < NT:
                 widen_x(k + 4)
             squares(k + 3, [0])
-        quant_h(4, both, "he")
-        weigh_vector(7, 0, gnw)
-        quant_x(7, both, "x")
-        weigh_gpsimd(7, 1, H)
-        project_mm(4, 0, 512, ("g", 5, 3))
-        project_mm(4, 512, 1024, ("x", 7, 0))
-        gate_mul(6, [1, 0, 2, 3])
-        squares(7, [1, 2, 3])
-        transpose_h(5, both, [("p", 3, 0), ("p", 3, 512)])
-        store(4, 0, 512)
-        inv_rms(7, 0, H)
-        transpose_h(6, both, [("g", 6, 0), ("g", 6, 2)])
+        transpose_h(5, both, [("g", 5, 3), ("p", 3, 0)])
         gather_h(5, 1)
         gather_h(5, 0)
-        gate(7, [1, 0], [("g", 6, 1), ("g", 6, 3)])
-        gate(7, [3, 2], [("p", 4, 0), ("h", 5, 0)])
+        quant_h(4, both, "he")
+        quant_x(7, both, "x")
+        weigh_gpsimd(7, 2, H, 1)
+        project_mm(4, 0, 512, ("x", 7, 0))
+        project_mm(4, 512, 1024, ("p", 3, 512))
+        gate_mul(6, [1, 0, 2, 3])
+        squares(7, [1, 2, 3])
+        gate(7, [1, 0, 2, 3], [("h", 5, 0), ("h", 5, 1), ("g", 6, 1), ("g", 6, 0)])
+        weigh_vector(7, 0, gnw)
+        weigh_vector(7, 1, gnw)
         store(4, 512, 1024)
+        inv_rms(7, 0, H)
+        store(4, 0, 512)
+        transpose_h(6, both, [("g", 6, 3), ("g", 6, 2)])
         gather_h(6, 1)
         gather_h(6, 0)
         quant_h(5, both, "he")
-        project_mm(5, 0, 512, ("h", 5, 1))
-        project_mm(5, 512, 1024, ("h", 6, 1))
-        gate_mul(7, [1, 0, 3, 2])
+        project_mm(5, 0, 512, ("p", 4, 0))
+        project_mm(5, 512, 1024, ("p", 4, 512))
+        gate_mul(7, [1, 0, 2, 3])
         store(5, 0, 512)
         quant_h(6, both, "he")
         transpose_h(7, [0], [("g", 7, 0)])
-        store(5, 512, 1024)
-        gather_h(7, 0)
         transpose_h(7, [1], [("g", 7, 2)])
+        gather_h(7, 0)
+        store(5, 512, 1024)
         gather_h(7, 1, True)
         quant_h(7, [0], "h7a")
         quant_h(7, [1], "h7b")
@@ -466,7 +466,7 @@ def tile_multiscaleretention_pc_w4_kernel(
         store(6, 0, 512)
         project_mm(6, 512, 1024, ("g", 7, 3))
         store(6, 512, 1024)
-        project_mm(7, 0, 512, ("p", 4, 512))
+        project_mm(7, 0, 512, ("h", 6, 1))
         store(7, 0, 512)
         project_mm(7, 512, 768, ("h", 6, 0))
         store(7, 512, 768, True)

@@ -18,11 +18,16 @@ T, E, H, DV = 1024, 1024, 4, 512
 F = H * DV
 P = 128
 NT = T // P
-GX = E // 512
-GH = F // 512
+PASS = 512
+BANK = 512
+GX = E // PASS
+GH = F // PASS
 EPS = 1e-5
 FLOPS = 2 * T * E * F * 2
 BYTES = T * F * 2 + T * E + E * 4 + 2 * (E * F // 2 + E * F // 32) + DV * 2 + T * E * 4
+
+VECTOR_COLS_TILE0 = 320
+VECTOR_COLS_TILE1 = 640
 
 
 def tile_multiscaleretention_pc_w4_kernel(
@@ -48,7 +53,7 @@ def tile_multiscaleretention_pc_w4_kernel(
             tag = free_banks[0] if after is None else held[after]
             free_banks.remove(tag)
             held[key] = tag
-            return psum.tile([P, 512], F32, name=tag, tag=tag)
+            return psum.tile([P, BANK], F32, name=tag, tag=tag)
 
         def give_bank(key):
             free_banks.append(held[key])
@@ -60,17 +65,20 @@ def tile_multiscaleretention_pc_w4_kernel(
         gnw = const.tile([P, DV], BF16, name="gnw")
         x_cuts = [(0, 1), (1, 2), (2, 3), (3, 5), (5, 8)]
         x_tiles = [const.tile([P, (b - a) * E], U8, name="xbytes%d" % a) for a, b in x_cuts]
-        o_halves = [[const.tile([P, F // 2], BF16, name="ohalf%d%d" % (i, j)) for j in range(2)] for i in range(1)]
+        o_first = [const.tile([P, F // 2], BF16, name="ofirst%d" % j) for j in range(2)]
         o_cuts = [(1, 2), (2, 3), (3, 4), (4, 8)]
         o_tiles = [const.tile([P, b - a, F], BF16, name="o%d" % a) for a, b in o_cuts]
         wg = [const.tile([P, GX, F], U8, name="wg%d" % j, align_bytes=256) for j in range(2)]
-        wo = [const.tile([P, 2, 2 * E], U8, name="wo%d" % k, align_bytes=256) for k in range(2)]
+        wo = [const.tile([P, 2, 2 * E], U8, name="wo%d" % j, align_bytes=256) for j in range(2)]
         shared = [const.tile([P, F], F32, name="shared%d" % j, align_bytes=256) for j in range(3)]
         s4 = const.tile([P, GX, 4], F32, name="s4")
 
-        def load_x(k):
-            a, b = x_cuts[k]
-            nc.sync.dma_start(out=x_tiles[k][:], in_=x_view[:, a:b, :].rearrange("p i e -> p (i e)"))
+        def slots(i, first, n=1):
+            return shared[i % 3][:, DV * first : DV * (first + n)]
+
+        def load_x(cut):
+            a, b = x_cuts[cut]
+            nc.sync.dma_start(out=x_tiles[cut][:], in_=x_view[:, a:b, :].rearrange("p i e -> p (i e)"))
 
         def load_scales(sc, hbm):
             for r in range(4):
@@ -79,116 +87,101 @@ def tile_multiscaleretention_pc_w4_kernel(
                     in_=hbm[:, r:16:4, :].rearrange("g q n -> q g n").bitcast(I32),
                 )
 
-        def load_wg_scales(j):
-            load_scales(wg_sc[j], Wg_scales[:, :, F // 2 * j : F // 2 * (j + 1)])
-
         def load_wg(j):
+            load_scales(wg_sc[j], Wg_scales[:, :, F // 2 * j : F // 2 * (j + 1)])
             nc.sync.dma_start(out=wg[j][:], in_=wg_view[:, :, F * j : F * (j + 1)])
 
-        def load_wo(j):
-            nc.sync.dma_start(out=wo[j][:], in_=wo_view[:, 2 * j : 2 * j + 2, :])
+        def load_wo():
+            load_scales(wo_sc, Wo_scales)
+            for j in range(2):
+                nc.sync.dma_start(out=wo[j][:], in_=wo_view[:, 2 * j : 2 * j + 2, :])
 
-        def load_o(k):
-            a, b = o_cuts[k]
-            nc.sync.dma_start(out=o_tiles[k][:], in_=o_view[:, a:b, :])
+        def load_o(cut):
+            a, b = o_cuts[cut]
+            nc.sync.dma_start(out=o_tiles[cut][:], in_=o_view[:, a:b, :])
 
-        def load_o_second(j):
+        def load_o_heads(i, j):
             cols = slice(F // 2 * j, F // 2 * (j + 1))
-            nc.sync.dma_start(out=o_tiles[0][:, 0, cols], in_=o_view[:, 1, cols])
+            dst = o_first[j][:] if i == 0 else o_tiles[0][:, 0, cols]
+            nc.sync.dma_start(out=dst, in_=o_view[:, i, cols])
 
-        def load_o_half(i, j):
-            nc.sync.dma_start(out=o_halves[i][j][:], in_=o_view[:, i, F // 2 * j : F // 2 * (j + 1)])
+        def zero(sc, odd_pieces=False):
+            words = sc.rearrange("p g n -> p (g n)").bitcast(I32)
+            n = words.shape[1]
+            cuts = [0, n // 2 - 1, n] if odd_pieces else [0, n]
+            for j in range(len(cuts) - 1):
+                nc.vector.memset(words[:, cuts[j] : cuts[j + 1]], 0)
 
-        def load_s4():
-            nc.sync.dma_start(out=s4[:], in_=x_scale.rearrange("a b (g p t) -> p (a b g) t", p=P, t=4))
-
-        def load_w():
-            nc.sync.dma_start(out=w4[:], in_=gn_weight.rearrange("(p t) -> p t", t=4))
-
-        def zero(sc):
-            nc.vector.memset(sc[:].rearrange("p g n -> p (g n)").bitcast(I32), 0)
-
-        xb, xt, xs, xc, xsc = {}, {}, {}, {}, {}
-        ss, rr, ow, hb, ht, hs, hc, hsc, gb, acc = {}, {}, {}, {}, {}, {}, {}, {}, {}, {}
+        x_wide, x_turned, x_scaled, x_codes, x_exps = {}, {}, {}, {}, {}
+        sumsq, inv, ow, g_bank = {}, {}, {}, {}
+        h_rows, h_turned, h_gathered, h_codes, h_exps, acc = {}, {}, {}, {}, {}, {}
 
         def o_cols(i, h, n=1):
-            if i < len(o_halves):
-                return o_halves[i][h // 2][:, DV * (h % 2) : DV * (h % 2 + n)]
-            k = max(k for k, (a, b) in enumerate(o_cuts) if a <= i)
-            return o_tiles[k][:, i - o_cuts[k][0], DV * h : DV * (h + n)]
+            if i == 0:
+                return o_first[h // 2][:, DV * (h % 2) : DV * (h % 2 + n)]
+            cut = max(c for c, (a, b) in enumerate(o_cuts) if a <= i)
+            return o_tiles[cut][:, i - o_cuts[cut][0], DV * h : DV * (h + n)]
 
-        def widen_x(i, n=1, vector_cols=0):
-            k = max(k for k, (a, b) in enumerate(x_cuts) if a <= i)
-            src = x_tiles[k][:, E * (i - x_cuts[k][0]) : E * (i - x_cuts[k][0] + n)]
-            wide = work.tile([P, 2 * E], BF16, name="xb", tag="xb", bufs=3)
-            for j in range(n):
-                xb[i + j] = wide[:, E * j : E * (j + 1)]
+        def widen_x(i, c0=0, c1=E, vector_cols=0):
+            cut = max(c for c, (a, b) in enumerate(x_cuts) if a <= i)
+            src = x_tiles[cut][:, E * (i - x_cuts[cut][0]) : E * (i - x_cuts[cut][0] + 1)].bitcast(E4M3)
+            if c0 == 0:
+                x_wide[i] = work.tile([P, E], BF16, name="x_wide", tag="x_wide", bufs=3)
+            mid = c0 + vector_cols
             if vector_cols:
-                nc.vector.tensor_copy(out=wide[:, 0:vector_cols], in_=src[:, 0:vector_cols].bitcast(E4M3))
-            nc.scalar.copy(out=wide[:, vector_cols : n * E], in_=src[:, vector_cols : n * E].bitcast(E4M3))
+                nc.vector.tensor_copy(out=x_wide[i][:, c0:mid], in_=src[:, c0:mid])
+            nc.scalar.copy(out=x_wide[i][:, mid:c1], in_=src[:, mid:c1])
 
         def transpose_x(i, passes, after=None):
-            b = take_bank(("x", i, passes[0]), after)
+            bank = take_bank(("x", i, passes[0]), after)
             for j, g in enumerate(passes):
-                xt[i, g] = b
-                words = xb[i][:, 512 * g : 512 * (g + 1)].bitcast(F32)
+                x_turned[i, g] = bank
+                words = x_wide[i][:, PASS * g : PASS * (g + 1)].bitcast(F32)
                 for u in range(2):
                     col = P * (len(passes) * u + j)
-                    nc.tensor.transpose(b[:, col : col + P], words[:, u:256:2], ident[:])
+                    nc.tensor.transpose(bank[:, col : col + P], words[:, u : 2 * P : 2], ident[:])
 
         def scale_x(i, passes):
-            n = len(passes)
-            g0 = passes[0]
-            src = xt[i, g0][:, 0 : 256 * n].bitcast(BF16).rearrange("p (u g n e) -> p g n u e", u=2, g=n, e=2)
-            dst = xs[i][:, 512 * g0 : 512 * (g0 + n)].rearrange("p (g n u e) -> p g n u e", g=n, u=2, e=2)
+            n, g0 = len(passes), passes[0]
+            src = x_turned[i, g0][:, 0 : 2 * P * n].bitcast(BF16)
+            dst = x_scaled[i][:, PASS * g0 : PASS * (g0 + n)]
+            scale = s4[:, g0 : g0 + n, :].rearrange("p g (u e) -> p g u e", u=2).unsqueeze(2)
             nc.vector.tensor_tensor(
-                out=dst,
-                in0=src,
-                in1=s4[:, g0 : g0 + n, :]
-                .rearrange("p g (u e) -> p g u e", u=2)
-                .unsqueeze(2)
-                .to_broadcast([P, n, P, 2, 2]),
+                out=dst.rearrange("p (g n u e) -> p g n u e", g=n, u=2, e=2),
+                in0=src.rearrange("p (u g n e) -> p g n u e", u=2, g=n, e=2),
+                in1=scale.to_broadcast([P, n, P, 2, 2]),
                 op=ALU.mult,
             )
             give_bank(("x", i, g0))
 
-        def quantise(src, tag, bufs=3):
+        def quantise(src, tag, bufs, codes_of, exps_of, keys):
             words = src.shape[1] // 4
             codes = work.tile([P, words], U32, name=tag + "c", tag=tag + "c", bufs=bufs, align_bytes=256)
-            scales = work.tile([P, words], U8, name=tag + "s", tag=tag + "s", bufs=bufs, align_bytes=256)
-            nc.vector.quantize_mx(out=codes[:].bitcast(FP8X4), scales=scales[:], in_=src)
-            return codes, scales
+            exps = work.tile([P, words], U8, name=tag + "s", tag=tag + "s", bufs=bufs, align_bytes=256)
+            nc.vector.quantize_mx(out=codes[:].bitcast(FP8X4), scales=exps[:], in_=src)
+            for j, key in enumerate(keys):
+                codes_of[key] = codes[:, P * j : P * (j + 1)]
+                exps_of[key] = exps[:, P * j : P * (j + 1)]
 
-        def note_passes(store_c, store_s, i, passes, codes, scales, first):
-            for j, g in enumerate(passes):
-                w = slice(first + P * j, first + P * (j + 1))
-                store_c[i, g] = codes[:, w]
-                store_s[i, g] = scales[:, w]
-
-        def quant_x(i, passes, tag):
-            codes, scales = quantise(xs[i][:, 512 * passes[0] : 512 * (passes[-1] + 1)], tag, 2)
-            note_passes(xc, xsc, i, passes, codes, scales, 0)
+        def quant_x(i):
+            quantise(x_scaled[i], "xq", 2, x_codes, x_exps, [(i, g) for g in range(GX)])
 
         def quant_h(i, halves, tag):
-            codes, scales = quantise(hs[i][:, 512 * halves[0] : 512 * (halves[-1] + 1)].bitcast(BF16), tag)
-            note_passes(hc, hsc, i, list(range(2 * halves[0], 2 * halves[-1] + 2)), codes, scales, 0)
-
-        def quant_x_pair(i, src):
-            codes, scales = quantise(src.bitcast(BF16), "pair", 1)
-            note_passes(xc, xsc, i, [0, 1], codes, scales, 0)
-            note_passes(xc, xsc, i + 1, [0, 1], codes, scales, GX * P)
+            src = h_gathered[i][:, BANK * halves[0] : BANK * (halves[-1] + 1)].bitcast(BF16)
+            keys = [(i, g) for g in range(2 * halves[0], 2 * halves[-1] + 2)]
+            quantise(src, tag, 3, h_codes, h_exps, keys)
 
         def squares(i, heads):
             for h in heads:
-                if i not in ss:
-                    ss[i] = work.tile([P, H], F32, name="ss", tag="ss", bufs=4)
-                    rr[i] = work.tile([P, H], F32, name="rr", tag="rr", bufs=4)
-                junk = work.tile([P, DV], BF16, name="junk", tag="junk", bufs=4)
-                nc.scalar.activation(out=junk[:], in_=o_cols(i, h), func=ACT.Square, accum_out=ss[i][:, h : h + 1])
+                if i not in sumsq:
+                    sumsq[i] = work.tile([P, H], F32, name="sumsq", tag="sumsq", bufs=4)
+                    inv[i] = work.tile([P, H], F32, name="inv", tag="inv", bufs=4)
+                sq = work.tile([P, DV], BF16, name="sq", tag="sq", bufs=4)
+                nc.scalar.activation(out=sq[:], in_=o_cols(i, h), func=ACT.Square, accum_out=sumsq[i][:, h : h + 1])
 
-        def inv_rms(i, h0, h1):
+        def inv_rms(i, h0=0, h1=H):
             nc.scalar.activation(
-                out=rr[i][:, h0:h1], in_=ss[i][:, h0:h1], func=ACT.Abs_reciprocal_sqrt, scale=1.0 / DV, bias=EPS
+                out=inv[i][:, h0:h1], in_=sumsq[i][:, h0:h1], func=ACT.Abs_reciprocal_sqrt, scale=1.0 / DV, bias=EPS
             )
 
         def by_parity(cols):
@@ -198,68 +191,53 @@ def tile_multiscaleretention_pc_w4_kernel(
             return cols.rearrange("p (u n e) -> p u n e", u=2, e=2)
 
         w_bank = take_bank("w")
+        w_words = w_bank[:, 0 : DV // 2]
 
         def spread_w():
             for u in range(2):
                 word = w4[:].bitcast(F32)[:, u : u + 1]
                 nc.tensor.transpose(w_bank[:, P * u : P * (u + 1)], word.to_broadcast([P, P]), ident[:])
 
-        def copy_w():
-            nc.scalar.copy(out=gnw[:].bitcast(F32), in_=w_bank[:, 0 : DV // 2])
-
-        def warm_up(n):
-            idle = take_bank("warm")
-            for j in range(n):
-                nc.tensor.matmul(idle[:, P * j : P * (j + 1)], lhsT=ident[:], rhs=ident[:], start=True, stop=True)
-            give_bank("warm")
-
-        def home(i):
-            return shared[i % 3]
-
-        def weigh_vector(i, h, w=None):
+        def weigh_vector(i, h, w):
             mine = work.tile([P, DV], F32, name="own", tag="own", bufs=4)
             ow[i, h] = as_parity(mine[:])
-            nc.vector.tensor_tensor(out=ow[i, h], in0=by_parity(o_cols(i, h)), in1=as_parity(w_bank[:, 0 : DV // 2].bitcast(BF16) if w is None else w[:]), op=ALU.mult)
+            nc.vector.tensor_tensor(out=ow[i, h], in0=by_parity(o_cols(i, h)), in1=as_parity(w), op=ALU.mult)
 
-        def weigh_gpsimd(i, a, b, at=None, buf=None):
+        def weigh_gpsimd(i, h0, h1, slot):
+            n = h1 - h0
+            dst = slots(i, slot, n)
             w = gnw[:].rearrange("p (u c) -> p u c", u=2).unsqueeze(2)
-            first = a if at is None else at
-            dst = (home(i) if buf is None else buf)[:, DV * first : DV * (first + b - a)]
-            for h in range(a, b):
-                ow[i, h] = as_parity(dst)[:, :, P * (h - a) : P * (h - a + 1), :]
+            for h in range(h0, h1):
+                ow[i, h] = as_parity(dst)[:, :, P * (h - h0) : P * (h - h0 + 1), :]
             nc.gpsimd.tensor_tensor(
-                out=dst.rearrange("p (u h c) -> p u h c", u=2, h=b - a),
-                in0=by_parity(o_cols(i, a, b - a)),
-                in1=w.to_broadcast([P, 2, b - a, DV // 2]),
+                out=dst.rearrange("p (u h c) -> p u h c", u=2, h=n),
+                in0=by_parity(o_cols(i, h0, n)),
+                in1=w.to_broadcast([P, 2, n, DV // 2]),
                 op=ALU.mult,
-            )
-
-        def gate_mm(i, h, g):
-            nc.tensor.matmul_mx(
-                out=gb[i, h][:],
-                lhsT=xc[i, g].bitcast(FP8X4),
-                lhsT_scale=xsc[i, g],
-                rhs=wg[h // 2][:, g, 2 * DV * (h % 2) : 2 * DV * (h % 2 + 1)].bitcast(FP4X4),
-                rhs_scale=wg_sc[h // 2][:, g, DV * (h % 2) : DV * (h % 2 + 1)],
-                start=(g == 0),
-                stop=(g == GX - 1),
             )
 
         def gate(i, heads, after=None):
             for n, h in enumerate(heads):
-                gb[i, h] = take_bank(("g", i, h), None if after is None else after[n])
+                g_bank[i, h] = take_bank(("g", i, h), None if after is None else after[n])
                 for g in range(GX):
-                    gate_mm(i, h, g)
+                    nc.tensor.matmul_mx(
+                        out=g_bank[i, h][:],
+                        lhsT=x_codes[i, g].bitcast(FP8X4),
+                        lhsT_scale=x_exps[i, g],
+                        rhs=wg[h // 2][:, g, 2 * DV * (h % 2) : 2 * DV * (h % 2 + 1)].bitcast(FP4X4),
+                        rhs_scale=wg_sc[h // 2][:, g, DV * (h % 2) : DV * (h % 2 + 1)],
+                        start=(g == 0),
+                        stop=(g == GX - 1),
+                    )
 
         def gate_mul(i, heads):
             for h in heads:
-                hb[i, h] = work.tile([P, 2, 256], BF16, name="hb%d" % h, tag="hb%d" % h, bufs=3)
-                gv = by_parity(gb[i, h][:])
+                h_rows[i, h] = work.tile([P, 2, DV // 2], BF16, name="h_rows%d" % h, tag="h_rows%d" % h, bufs=3)
                 for u in range(2):
                     nc.vector.scalar_tensor_tensor(
-                        out=hb[i, h][:, u].rearrange("p (n e) -> p n e", e=2),
-                        in0=gv[:, u],
-                        scalar=rr[i][:, h : h + 1],
+                        out=h_rows[i, h][:, u].rearrange("p (n e) -> p n e", e=2),
+                        in0=by_parity(g_bank[i, h][:])[:, u],
+                        scalar=inv[i][:, h : h + 1],
                         in1=ow[i, h][:, u],
                         op0=ALU.mult,
                         op1=ALU.mult,
@@ -268,131 +246,128 @@ def tile_multiscaleretention_pc_w4_kernel(
 
         def transpose_h(i, halves, after=None):
             for n, half in enumerate(halves):
-                ht[i, half] = take_bank(("h", i, half), None if after is None else after[n])
+                h_turned[i, half] = take_bank(("h", i, half), None if after is None else after[n])
                 for j in range(2):
                     for u in range(2):
                         col = P * (2 * j + u)
-                        nc.tensor.transpose(
-                            ht[i, half][:, col : col + P], hb[i, 2 * half + j][:, u].bitcast(F32), ident[:]
-                        )
+                        words = h_rows[i, 2 * half + j][:, u].bitcast(F32)
+                        nc.tensor.transpose(h_turned[i, half][:, col : col + P], words, ident[:])
 
-        def gather_h(i, half, on_vector=False):
-            if i not in hs:
-                hs[i] = work.tile([P, F // 2], F32, name="hs", tag="hs", align_bytes=256)[:]
-            dst = hs[i][:, 512 * half : 512 * (half + 1)].rearrange("p (g n u) -> p g n u", g=2, u=2)
-            src = ht[i, half][:].rearrange("p (g u n) -> p g n u", g=2, u=2)
+        def copy(dst, src, on_vector):
             if on_vector:
                 nc.vector.tensor_copy(out=dst, in_=src)
             else:
                 nc.scalar.copy(out=dst, in_=src)
+
+        def gather_h(i, half, on_vector=False):
+            if i not in h_gathered:
+                h_gathered[i] = work.tile([P, F // 2], F32, name="h_gathered", tag="h_gathered", align_bytes=256)
+            dst = h_gathered[i][:, BANK * half : BANK * (half + 1)].rearrange("p (g n u) -> p g n u", g=2, u=2)
+            copy(dst, h_turned[i, half][:].rearrange("p (g u n) -> p g n u", g=2, u=2), on_vector)
             give_bank(("h", i, half))
 
-        def project_mm(i, c0, c1, after=None):
+        def project(i, c0, c1, after=None):
             acc[i, c0] = take_bank(("p", i, c0), after)
             for g in range(GH):
                 nc.tensor.matmul_mx(
                     out=acc[i, c0][:, 0 : c1 - c0],
-                    lhsT=hc[i, g].bitcast(FP8X4),
-                    lhsT_scale=hsc[i, g],
+                    lhsT=h_codes[i, g].bitcast(FP8X4),
+                    lhsT_scale=h_exps[i, g],
                     rhs=wo[g // 2][:, g % 2, 2 * c0 : 2 * c1].bitcast(FP4X4),
                     rhs_scale=wo_sc[:, g, c0:c1],
                     start=(g == 0),
                     stop=(g == GH - 1),
                 )
 
-        def project(i):
-            project_mm(i, 0, 512)
-            project_mm(i, 512, 1024)
-
         def store(i, c0, c1, on_vector=False):
-            res = work.tile([P, 512], F32, name="res", tag="res", bufs=6)
-            if on_vector:
-                nc.vector.tensor_copy(out=res[:, 0 : c1 - c0], in_=acc[i, c0][:, 0 : c1 - c0])
-            else:
-                nc.scalar.copy(out=res[:, 0 : c1 - c0], in_=acc[i, c0][:, 0 : c1 - c0])
+            res = work.tile([P, BANK], F32, name="res", tag="res", bufs=6)
+            copy(res[:, 0 : c1 - c0], acc[i, c0][:, 0 : c1 - c0], on_vector)
             give_bank(("p", i, c0))
             nc.sync.dma_start(out=out_view[i][:, c0:c1], in_=res[:, 0 : c1 - c0])
 
         both = [0, 1]
-        every = [0, 1, 2, 3]
+        every = list(range(H))
+        last = NT - 1
+        w_psum = w_words.bitcast(BF16)
+
+        x_scaled[0] = slots(0, 2).bitcast(BF16)
+        x_scaled[1] = slots(1, 1).bitcast(BF16)
+        x_scaled[2] = slots(1, 2).bitcast(BF16)
         for i in range(3, NT):
-            xs[i] = home(i)[:, DV : 2 * DV].bitcast(BF16)
-        xs[0] = home(0)[:, 2 * DV : 3 * DV].bitcast(BF16)
-        xs[1] = home(1)[:, DV : 2 * DV].bitcast(BF16)
-        xs[2] = home(1)[:, 2 * DV : 3 * DV].bitcast(BF16)
+            x_scaled[i] = slots(i, 1).bitcast(BF16)
 
         nc.vector.memset(ident[:], 0.0)
         make_identity(nc, ident[:], nomemset=True)
-        zero(wg_sc[0])
-        zero(wg_sc[1])
-        zero(wo_sc)
+        for j in range(2):
+            zero(wg_sc[j][:], odd_pieces=True)
+        zero(wo_sc[:, 0 : GH // 2])
 
         load_x(0)
-        load_w()
-        load_s4()
+        nc.sync.dma_start(out=w4[:], in_=gn_weight.rearrange("(p t) -> p t", t=4))
+        nc.sync.dma_start(out=s4[:], in_=x_scale.rearrange("a b (g p t) -> p (a b g) t", p=P, t=4))
         load_x(1)
-        load_o_half(0, 0)
+        load_o_heads(0, 0)
         load_x(2)
-        load_o_half(0, 1)
-        load_wg_scales(0)
+        load_o_heads(0, 1)
         load_wg(0)
-        load_o_second(0)
-        load_wg_scales(1)
+        load_o_heads(1, 0)
         load_wg(1)
-        load_o_second(1)
+        load_o_heads(1, 1)
         load_x(3)
         load_o(1)
-        load_scales(wo_sc, Wo_scales)
-        load_wo(0)
-        load_wo(1)
+
+        spread_w()
+        for g in both:
+            widen_x(0, PASS * g, PASS * (g + 1), VECTOR_COLS_TILE0)
+        zero(wo_sc[:, GH // 2 : GH])
+        widen_x(1, 0, E, VECTOR_COLS_TILE1)
+        load_wo()
         load_o(2)
         load_x(4)
         load_o(3)
-
-        spread_w()
-        widen_x(0, 1, 512)
-        widen_x(1, 1, 768)
-        copy_w()
+        nc.scalar.copy(out=gnw[:].bitcast(F32), in_=w_words)
         widen_x(2)
-        transpose_x(0, [0])
-        transpose_x(0, [1])
+        for g in both:
+            transpose_x(0, [g])
         transpose_x(1, both)
-        scale_x(0, [0])
-        scale_x(0, [1])
+        for g in both:
+            scale_x(0, [g])
         transpose_x(2, both)
-        weigh_gpsimd(0, 0, 1)
+        weigh_gpsimd(0, 0, 1, 0)
         squares(0, [0, 1, 2])
         inv_rms(0, 0, 2)
-        weigh_vector(0, 1)
-        quant_x(0, both, "x")
-        weigh_gpsimd(0, 2, 4)
+        weigh_vector(0, 1, w_psum)
+        quant_x(0)
+        weigh_gpsimd(0, 2, H, 2)
         scale_x(1, both)
         squares(0, [3])
         scale_x(2, both)
+
         gate(0, every)
         squares(1, [0])
-        inv_rms(0, 2, 4)
+        inv_rms(0, 2, H)
         gate_mul(0, [0])
-        quant_x_pair(1, home(1)[:, DV : 3 * DV])
-        weigh_gpsimd(1, 1, 4)
-        weigh_gpsimd(2, 1, H)
+        keys = [(i, g) for i in (1, 2) for g in range(GX)]
+        quantise(slots(1, 1, 2).bitcast(BF16), "xpair", 1, x_codes, x_exps, keys)
+        weigh_gpsimd(1, 1, H, 1)
+        weigh_gpsimd(2, 1, H, 1)
         gate(1, [0, 1])
         gate_mul(0, [1, 2])
         gate(1, [2, 3])
-        weigh_vector(1, 0)
+        weigh_vector(1, 0, w_psum)
         gate_mul(0, [3])
         squares(1, [1, 2, 3])
         widen_x(3)
-        inv_rms(1, 0, H)
+        inv_rms(1)
         widen_x(4)
         squares(2, [0])
         transpose_h(0, both)
         gate_mul(1, [0])
-        weigh_vector(2, 0)
+        weigh_vector(2, 0, w_psum)
         give_bank("w")
         transpose_x(3, both)
-        gather_h(0, 0)
-        gather_h(0, 1)
+        for half in both:
+            gather_h(0, half)
         gate(2, [0, 1, 2])
         gate_mul(1, [1])
         transpose_h(1, [0])
@@ -404,73 +379,76 @@ def tile_multiscaleretention_pc_w4_kernel(
         squares(2, [1, 2, 3])
         transpose_h(1, [1])
         gather_h(1, 0)
-        inv_rms(2, 0, H)
+        inv_rms(2)
         gather_h(1, 1)
-        for k in range(1, 5):
-            order = [1, 0, 2, 3] if k > 1 else every
-            if k > 1:
+
+        drain = [1, 0, 2, 3]
+        for k in range(1, last - 2):
+            first_step = k == 1
+            order = every if first_step else drain
+            gathered = both if first_step else [1, 0]
+            if not first_step:
                 transpose_h(k, both, [("g", k, 3), ("p", k - 2, 0)])
-                transpose_x(k + 3, both, ("p", k - 2, 512))
-                gather_h(k, 1)
-                gather_h(k, 0)
-            turned = [("h", k, 1), ("h", k, 0)] if k > 1 else [("h", k, 0), ("h", k, 1)]
-            quant_h(k - 1, both, "he")
-            weigh_vector(k + 2, 0, gnw)
-            quant_x(k + 2, both, "x")
-            weigh_gpsimd(k + 2, 1, H)
-            project_mm(k - 1, 0, 512, ("x", k + 2, 0) if k > 1 else None)
-            project_mm(k - 1, 512, 1024, turned[1])
+                transpose_x(k + 3, both, ("p", k - 2, BANK))
+                for half in gathered:
+                    gather_h(k, half)
+            quant_h(k - 1, both, "hq")
+            weigh_vector(k + 2, 0, gnw[:])
+            quant_x(k + 2)
+            weigh_gpsimd(k + 2, 1, H, 1)
+            project(k - 1, 0, BANK, None if first_step else ("x", k + 2, 0))
+            project(k - 1, BANK, E, ("h", k, gathered[1]))
             gate_mul(k + 1, order)
-            squares(k + 2, [1, 2, 3] if k > 1 else every)
-            gate(k + 2, [2, 1, 3, 0], [turned[0]] + [("g", k + 1, h) for h in order[:3]])
+            squares(k + 2, every if first_step else [1, 2, 3])
+            gate(k + 2, [2, 1, 3, 0], [("h", k, gathered[0])] + [("g", k + 1, h) for h in order[:3]])
             scale_x(k + 3, both)
-            store(k - 1, 512, 1024)
-            inv_rms(k + 2, 0, H)
-            store(k - 1, 0, 512)
+            store(k - 1, BANK, E)
+            inv_rms(k + 2)
+            store(k - 1, 0, BANK)
             if k + 4 < NT:
                 widen_x(k + 4)
             squares(k + 3, [0])
-        transpose_h(5, both, [("g", 5, 3), ("p", 3, 0)])
-        gather_h(5, 1)
-        gather_h(5, 0)
-        quant_h(4, both, "he")
-        quant_x(7, both, "x")
-        weigh_gpsimd(7, 2, H, 1)
-        project_mm(4, 0, 512, ("x", 7, 0))
-        project_mm(4, 512, 1024, ("p", 3, 512))
-        gate_mul(6, [1, 0, 2, 3])
-        squares(7, [1, 2, 3])
-        gate(7, [1, 0, 2, 3], [("h", 5, 0), ("h", 5, 1), ("g", 6, 1), ("g", 6, 0)])
-        weigh_vector(7, 0, gnw)
-        weigh_vector(7, 1, gnw)
-        store(4, 512, 1024)
-        inv_rms(7, 0, H)
-        store(4, 0, 512)
-        transpose_h(6, both, [("g", 6, 3), ("g", 6, 2)])
-        gather_h(6, 1)
-        gather_h(6, 0)
-        quant_h(5, both, "he")
-        project_mm(5, 0, 512, ("p", 4, 0))
-        project_mm(5, 512, 1024, ("p", 4, 512))
-        gate_mul(7, [1, 0, 2, 3])
-        store(5, 0, 512)
-        quant_h(6, both, "he")
-        transpose_h(7, [0], [("g", 7, 0)])
-        transpose_h(7, [1], [("g", 7, 2)])
-        gather_h(7, 0)
-        store(5, 512, 1024)
-        gather_h(7, 1, True)
-        quant_h(7, [0], "h7a")
-        quant_h(7, [1], "h7b")
-        project_mm(6, 0, 512, ("g", 7, 1))
-        store(6, 0, 512)
-        project_mm(6, 512, 1024, ("g", 7, 3))
-        store(6, 512, 1024)
-        project_mm(7, 0, 512, ("h", 6, 1))
-        store(7, 0, 512)
-        project_mm(7, 512, 768, ("h", 6, 0))
-        store(7, 512, 768, True)
-        project_mm(7, 768, 896, ("h", 7, 1))
-        store(7, 768, 896)
-        project_mm(7, 896, 1024, ("h", 7, 0))
-        store(7, 896, 1024, True)
+
+        k = last - 2
+        transpose_h(k, both, [("g", k, 3), ("p", k - 2, 0)])
+        for half in [1, 0]:
+            gather_h(k, half)
+        quant_h(k - 1, both, "hq")
+        quant_x(last)
+        weigh_gpsimd(last, 2, H, 1)
+        project(k - 1, 0, BANK, ("x", last, 0))
+        project(k - 1, BANK, E, ("p", k - 2, BANK))
+        gate_mul(k + 1, drain)
+        squares(last, [1, 2, 3])
+        gate(last, drain, [("h", k, 0), ("h", k, 1), ("g", k + 1, 1), ("g", k + 1, 0)])
+        for h in both:
+            weigh_vector(last, h, gnw[:])
+        store(k - 1, BANK, E)
+        inv_rms(last)
+        store(k - 1, 0, BANK)
+
+        k = last - 1
+        transpose_h(k, both, [("g", k, 3), ("g", k, 2)])
+        for half in [1, 0]:
+            gather_h(k, half)
+        quant_h(k - 1, both, "hq")
+        project(k - 1, 0, BANK, ("p", k - 2, 0))
+        project(k - 1, BANK, E, ("p", k - 2, BANK))
+        gate_mul(last, drain)
+        store(k - 1, 0, BANK)
+        quant_h(k, both, "hq")
+        transpose_h(last, both, [("g", last, 0), ("g", last, 2)])
+        gather_h(last, 0)
+        store(k - 1, BANK, E)
+        gather_h(last, 1, True)
+        for half in both:
+            quant_h(last, [half], "hq_last%d" % half)
+        project(k, 0, BANK, ("g", last, 1))
+        store(k, 0, BANK)
+        project(k, BANK, E, ("g", last, 3))
+        store(k, BANK, E)
+        edges = [0, E // 2, 3 * E // 4, 7 * E // 8, E]
+        spare = [("h", k, 1), ("h", k, 0), ("h", last, 1), ("h", last, 0)]
+        for j in range(4):
+            project(last, edges[j], edges[j + 1], spare[j])
+            store(last, edges[j], edges[j + 1], j % 2 == 1)

from contextlib import ExitStack

import concourse.mybir as mybir
from concourse.masks import make_identity

F32 = mybir.dt.float32
BF16 = mybir.dt.bfloat16
I32 = mybir.dt.int32
U32 = mybir.dt.uint32
U8 = mybir.dt.uint8
E4M3 = mybir.dt.float8_e4m3fn
FP8X4 = mybir.dt.float8_e4m3fn_x4
FP4X4 = mybir.dt.float4_e2m1fn_x4
ACT = mybir.ActivationFunctionType
ALU = mybir.AluOpType

T, E, H, DV = 1024, 1024, 4, 512
F = H * DV
P = 128
NT = T // P
PASS = 512
BANK = 512
GX = E // PASS
GH = F // PASS
EPS = 1e-5
FLOPS = 2 * T * E * F * 2
BYTES = T * F * 2 + T * E + E * 4 + 2 * (E * F // 2 + E * F // 32) + DV * 2 + T * E * 4

VECTOR_COLS_TILE0 = 320
VECTOR_COLS_TILE1 = 640


def tile_multiscaleretention_pc_w4_kernel(
    tc, o_ret, x_bytes, x_scale, Wg_words, Wg_scales, gn_weight, Wo_words, Wo_scales, out
):
    nc = tc.nc
    o_view = o_ret.rearrange("b (p i) h d -> p (b i) (h d)", i=NT)
    x_view = x_bytes.rearrange("b (p i) e -> p (b i) e", i=NT)
    out_view = out.rearrange("b (p i) e -> i p (b e)", i=NT)
    wg_view = Wg_words.rearrange("g p n -> p g n")
    wo_view = Wo_words.rearrange("g p n -> p g n")

    with ExitStack() as ctx:
        const = ctx.enter_context(tc.tile_pool(name="const", bufs=1))
        work = ctx.enter_context(tc.tile_pool(name="work", bufs=2))
        psum = ctx.enter_context(tc.psum_pool(name="psum", bufs=1))
        ctx.enter_context(tc.manual_schedule())

        free_banks = ["bank%d" % k for k in range(8)]
        held = {}

        def take_bank(key, after=None):
            tag = free_banks[0] if after is None else held[after]
            free_banks.remove(tag)
            held[key] = tag
            return psum.tile([P, BANK], F32, name=tag, tag=tag)

        def give_bank(key):
            free_banks.append(held[key])

        wg_sc = [const.tile([P, GX, F // 2], U8, name="wg_sc%d" % j, align_bytes=256) for j in range(2)]
        wo_sc = const.tile([P, GH, E], U8, name="wo_sc", align_bytes=256)
        ident = const.tile([P, P], F32, name="ident")
        w4 = const.tile([P, 4], BF16, name="w4")
        gnw = const.tile([P, DV], BF16, name="gnw")
        x_cuts = [(0, 1), (1, 2), (2, 3), (3, 5), (5, 8)]
        x_tiles = [const.tile([P, (b - a) * E], U8, name="xbytes%d" % a) for a, b in x_cuts]
        o_first = [const.tile([P, F // 2], BF16, name="ofirst%d" % j) for j in range(2)]
        o_cuts = [(1, 2), (2, 3), (3, 4), (4, 8)]
        o_tiles = [const.tile([P, b - a, F], BF16, name="o%d" % a) for a, b in o_cuts]
        wg = [const.tile([P, GX, F], U8, name="wg%d" % j, align_bytes=256) for j in range(2)]
        wo = [const.tile([P, 2, 2 * E], U8, name="wo%d" % j, align_bytes=256) for j in range(2)]
        shared = [const.tile([P, F], F32, name="shared%d" % j, align_bytes=256) for j in range(3)]
        s4 = const.tile([P, GX, 4], F32, name="s4")

        def slots(i, first, n=1):
            return shared[i % 3][:, DV * first : DV * (first + n)]

        def load_x(cut):
            a, b = x_cuts[cut]
            nc.sync.dma_start(out=x_tiles[cut][:], in_=x_view[:, a:b, :].rearrange("p i e -> p (i e)"))

        def load_scales(sc, hbm):
            for r in range(4):
                nc.sync.dma_start(
                    out=sc[r:P:32, :, :].bitcast(I32),
                    in_=hbm[:, r:16:4, :].rearrange("g q n -> q g n").bitcast(I32),
                )

        def load_wg(j):
            load_scales(wg_sc[j], Wg_scales[:, :, F // 2 * j : F // 2 * (j + 1)])
            nc.sync.dma_start(out=wg[j][:], in_=wg_view[:, :, F * j : F * (j + 1)])

        def load_wo():
            load_scales(wo_sc, Wo_scales)
            for j in range(2):
                nc.sync.dma_start(out=wo[j][:], in_=wo_view[:, 2 * j : 2 * j + 2, :])

        def load_o(cut):
            a, b = o_cuts[cut]
            nc.sync.dma_start(out=o_tiles[cut][:], in_=o_view[:, a:b, :])

        def load_o_heads(i, j):
            cols = slice(F // 2 * j, F // 2 * (j + 1))
            dst = o_first[j][:] if i == 0 else o_tiles[0][:, 0, cols]
            nc.sync.dma_start(out=dst, in_=o_view[:, i, cols])

        def zero(sc, odd_pieces=False):
            words = sc.rearrange("p g n -> p (g n)").bitcast(I32)
            n = words.shape[1]
            cuts = [0, n // 2 - 1, n] if odd_pieces else [0, n]
            for j in range(len(cuts) - 1):
                nc.vector.memset(words[:, cuts[j] : cuts[j + 1]], 0)

        x_wide, x_turned, x_scaled, x_codes, x_exps = {}, {}, {}, {}, {}
        sumsq, inv, ow, g_bank = {}, {}, {}, {}
        h_rows, h_turned, h_gathered, h_codes, h_exps, acc = {}, {}, {}, {}, {}, {}

        def o_cols(i, h, n=1):
            if i == 0:
                return o_first[h // 2][:, DV * (h % 2) : DV * (h % 2 + n)]
            cut = max(c for c, (a, b) in enumerate(o_cuts) if a <= i)
            return o_tiles[cut][:, i - o_cuts[cut][0], DV * h : DV * (h + n)]

        def widen_x(i, c0=0, c1=E, vector_cols=0):
            cut = max(c for c, (a, b) in enumerate(x_cuts) if a <= i)
            src = x_tiles[cut][:, E * (i - x_cuts[cut][0]) : E * (i - x_cuts[cut][0] + 1)].bitcast(E4M3)
            if c0 == 0:
                x_wide[i] = work.tile([P, E], BF16, name="x_wide", tag="x_wide", bufs=3)
            mid = c0 + vector_cols
            if vector_cols:
                nc.vector.tensor_copy(out=x_wide[i][:, c0:mid], in_=src[:, c0:mid])
            nc.scalar.copy(out=x_wide[i][:, mid:c1], in_=src[:, mid:c1])

        def transpose_x(i, passes, after=None):
            bank = take_bank(("x", i, passes[0]), after)
            for j, g in enumerate(passes):
                x_turned[i, g] = bank
                words = x_wide[i][:, PASS * g : PASS * (g + 1)].bitcast(F32)
                for u in range(2):
                    col = P * (len(passes) * u + j)
                    nc.tensor.transpose(bank[:, col : col + P], words[:, u : 2 * P : 2], ident[:])

        def scale_x(i, passes):
            n, g0 = len(passes), passes[0]
            src = x_turned[i, g0][:, 0 : 2 * P * n].bitcast(BF16)
            dst = x_scaled[i][:, PASS * g0 : PASS * (g0 + n)]
            scale = s4[:, g0 : g0 + n, :].rearrange("p g (u e) -> p g u e", u=2).unsqueeze(2)
            nc.vector.tensor_tensor(
                out=dst.rearrange("p (g n u e) -> p g n u e", g=n, u=2, e=2),
                in0=src.rearrange("p (u g n e) -> p g n u e", u=2, g=n, e=2),
                in1=scale.to_broadcast([P, n, P, 2, 2]),
                op=ALU.mult,
            )
            give_bank(("x", i, g0))

        def quantise(src, tag, bufs, codes_of, exps_of, keys):
            words = src.shape[1] // 4
            codes = work.tile([P, words], U32, name=tag + "c", tag=tag + "c", bufs=bufs, align_bytes=256)
            exps = work.tile([P, words], U8, name=tag + "s", tag=tag + "s", bufs=bufs, align_bytes=256)
            nc.vector.quantize_mx(out=codes[:].bitcast(FP8X4), scales=exps[:], in_=src)
            for j, key in enumerate(keys):
                codes_of[key] = codes[:, P * j : P * (j + 1)]
                exps_of[key] = exps[:, P * j : P * (j + 1)]

        def quant_x(i):
            quantise(x_scaled[i], "xq", 2, x_codes, x_exps, [(i, g) for g in range(GX)])

        def quant_h(i, halves, tag):
            src = h_gathered[i][:, BANK * halves[0] : BANK * (halves[-1] + 1)].bitcast(BF16)
            keys = [(i, g) for g in range(2 * halves[0], 2 * halves[-1] + 2)]
            quantise(src, tag, 3, h_codes, h_exps, keys)

        def squares(i, heads):
            for h in heads:
                if i not in sumsq:
                    sumsq[i] = work.tile([P, H], F32, name="sumsq", tag="sumsq", bufs=4)
                    inv[i] = work.tile([P, H], F32, name="inv", tag="inv", bufs=4)
                sq = work.tile([P, DV], BF16, name="sq", tag="sq", bufs=4)
                nc.scalar.activation(out=sq[:], in_=o_cols(i, h), func=ACT.Square, accum_out=sumsq[i][:, h : h + 1])

        def inv_rms(i, h0=0, h1=H):
            nc.scalar.activation(
                out=inv[i][:, h0:h1], in_=sumsq[i][:, h0:h1], func=ACT.Abs_reciprocal_sqrt, scale=1.0 / DV, bias=EPS
            )

        def by_parity(cols):
            return cols.rearrange("p (n u e) -> p u n e", u=2, e=2)

        def as_parity(cols):
            return cols.rearrange("p (u n e) -> p u n e", u=2, e=2)

        w_bank = take_bank("w")
        w_words = w_bank[:, 0 : DV // 2]

        def spread_w():
            for u in range(2):
                word = w4[:].bitcast(F32)[:, u : u + 1]
                nc.tensor.transpose(w_bank[:, P * u : P * (u + 1)], word.to_broadcast([P, P]), ident[:])

        def weigh_vector(i, h, w):
            mine = work.tile([P, DV], F32, name="own", tag="own", bufs=4)
            ow[i, h] = as_parity(mine[:])
            nc.vector.tensor_tensor(out=ow[i, h], in0=by_parity(o_cols(i, h)), in1=as_parity(w), op=ALU.mult)

        def weigh_gpsimd(i, h0, h1, slot):
            n = h1 - h0
            dst = slots(i, slot, n)
            w = gnw[:].rearrange("p (u c) -> p u c", u=2).unsqueeze(2)
            for h in range(h0, h1):
                ow[i, h] = as_parity(dst)[:, :, P * (h - h0) : P * (h - h0 + 1), :]
            nc.gpsimd.tensor_tensor(
                out=dst.rearrange("p (u h c) -> p u h c", u=2, h=n),
                in0=by_parity(o_cols(i, h0, n)),
                in1=w.to_broadcast([P, 2, n, DV // 2]),
                op=ALU.mult,
            )

        def gate(i, heads, after=None):
            for n, h in enumerate(heads):
                g_bank[i, h] = take_bank(("g", i, h), None if after is None else after[n])
                for g in range(GX):
                    nc.tensor.matmul_mx(
                        out=g_bank[i, h][:],
                        lhsT=x_codes[i, g].bitcast(FP8X4),
                        lhsT_scale=x_exps[i, g],
                        rhs=wg[h // 2][:, g, 2 * DV * (h % 2) : 2 * DV * (h % 2 + 1)].bitcast(FP4X4),
                        rhs_scale=wg_sc[h // 2][:, g, DV * (h % 2) : DV * (h % 2 + 1)],
                        start=(g == 0),
                        stop=(g == GX - 1),
                    )

        def gate_mul(i, heads):
            for h in heads:
                h_rows[i, h] = work.tile([P, 2, DV // 2], BF16, name="h_rows%d" % h, tag="h_rows%d" % h, bufs=3)
                for u in range(2):
                    nc.vector.scalar_tensor_tensor(
                        out=h_rows[i, h][:, u].rearrange("p (n e) -> p n e", e=2),
                        in0=by_parity(g_bank[i, h][:])[:, u],
                        scalar=inv[i][:, h : h + 1],
                        in1=ow[i, h][:, u],
                        op0=ALU.mult,
                        op1=ALU.mult,
                    )
                give_bank(("g", i, h))

        def transpose_h(i, halves, after=None):
            for n, half in enumerate(halves):
                h_turned[i, half] = take_bank(("h", i, half), None if after is None else after[n])
                for j in range(2):
                    for u in range(2):
                        col = P * (2 * j + u)
                        words = h_rows[i, 2 * half + j][:, u].bitcast(F32)
                        nc.tensor.transpose(h_turned[i, half][:, col : col + P], words, ident[:])

        def copy(dst, src, on_vector):
            if on_vector:
                nc.vector.tensor_copy(out=dst, in_=src)
            else:
                nc.scalar.copy(out=dst, in_=src)

        def gather_h(i, half, on_vector=False):
            if i not in h_gathered:
                h_gathered[i] = work.tile([P, F // 2], F32, name="h_gathered", tag="h_gathered", align_bytes=256)
            dst = h_gathered[i][:, BANK * half : BANK * (half + 1)].rearrange("p (g n u) -> p g n u", g=2, u=2)
            copy(dst, h_turned[i, half][:].rearrange("p (g u n) -> p g n u", g=2, u=2), on_vector)
            give_bank(("h", i, half))

        def project(i, c0, c1, after=None):
            acc[i, c0] = take_bank(("p", i, c0), after)
            for g in range(GH):
                nc.tensor.matmul_mx(
                    out=acc[i, c0][:, 0 : c1 - c0],
                    lhsT=h_codes[i, g].bitcast(FP8X4),
                    lhsT_scale=h_exps[i, g],
                    rhs=wo[g // 2][:, g % 2, 2 * c0 : 2 * c1].bitcast(FP4X4),
                    rhs_scale=wo_sc[:, g, c0:c1],
                    start=(g == 0),
                    stop=(g == GH - 1),
                )

        def store(i, c0, c1, on_vector=False):
            res = work.tile([P, BANK], F32, name="res", tag="res", bufs=6)
            copy(res[:, 0 : c1 - c0], acc[i, c0][:, 0 : c1 - c0], on_vector)
            give_bank(("p", i, c0))
            nc.sync.dma_start(out=out_view[i][:, c0:c1], in_=res[:, 0 : c1 - c0])

        both = [0, 1]
        every = list(range(H))
        last = NT - 1
        w_psum = w_words.bitcast(BF16)

        x_scaled[0] = slots(0, 2).bitcast(BF16)
        x_scaled[1] = slots(1, 1).bitcast(BF16)
        x_scaled[2] = slots(1, 2).bitcast(BF16)
        for i in range(3, NT):
            x_scaled[i] = slots(i, 1).bitcast(BF16)

        nc.vector.memset(ident[:], 0.0)
        make_identity(nc, ident[:], nomemset=True)
        for j in range(2):
            zero(wg_sc[j][:], odd_pieces=True)
        zero(wo_sc[:, 0 : GH // 2])

        load_x(0)
        nc.sync.dma_start(out=w4[:], in_=gn_weight.rearrange("(p t) -> p t", t=4))
        nc.sync.dma_start(out=s4[:], in_=x_scale.rearrange("a b (g p t) -> p (a b g) t", p=P, t=4))
        load_x(1)
        load_o_heads(0, 0)
        load_x(2)
        load_o_heads(0, 1)
        load_wg(0)
        load_o_heads(1, 0)
        load_wg(1)
        load_o_heads(1, 1)
        load_x(3)
        load_o(1)

        spread_w()
        for g in both:
            widen_x(0, PASS * g, PASS * (g + 1), VECTOR_COLS_TILE0)
        zero(wo_sc[:, GH // 2 : GH])
        widen_x(1, 0, E, VECTOR_COLS_TILE1)
        load_wo()
        load_o(2)
        load_x(4)
        load_o(3)
        nc.scalar.copy(out=gnw[:].bitcast(F32), in_=w_words)
        widen_x(2)
        for g in both:
            transpose_x(0, [g])
        transpose_x(1, both)
        for g in both:
            scale_x(0, [g])
        transpose_x(2, both)
        weigh_gpsimd(0, 0, 1, 0)
        squares(0, [0, 1, 2])
        inv_rms(0, 0, 2)
        weigh_vector(0, 1, w_psum)
        quant_x(0)
        weigh_gpsimd(0, 2, H, 2)
        scale_x(1, both)
        squares(0, [3])
        scale_x(2, both)

        gate(0, every)
        squares(1, [0])
        inv_rms(0, 2, H)
        gate_mul(0, [0])
        keys = [(i, g) for i in (1, 2) for g in range(GX)]
        quantise(slots(1, 1, 2).bitcast(BF16), "xpair", 1, x_codes, x_exps, keys)
        weigh_gpsimd(1, 1, H, 1)
        weigh_gpsimd(2, 1, H, 1)
        gate(1, [0, 1])
        gate_mul(0, [1, 2])
        gate(1, [2, 3])
        weigh_vector(1, 0, w_psum)
        gate_mul(0, [3])
        squares(1, [1, 2, 3])
        widen_x(3)
        inv_rms(1)
        widen_x(4)
        squares(2, [0])
        transpose_h(0, both)
        gate_mul(1, [0])
        weigh_vector(2, 0, w_psum)
        give_bank("w")
        transpose_x(3, both)
        for half in both:
            gather_h(0, half)
        gate(2, [0, 1, 2])
        gate_mul(1, [1])
        transpose_h(1, [0])
        scale_x(3, both)
        transpose_x(4, both)
        gate_mul(1, [2])
        gate(2, [3])
        gate_mul(1, [3])
        squares(2, [1, 2, 3])
        transpose_h(1, [1])
        gather_h(1, 0)
        inv_rms(2)
        gather_h(1, 1)

        drain = [1, 0, 2, 3]
        for k in range(1, last - 2):
            first_step = k == 1
            order = every if first_step else drain
            gathered = both if first_step else [1, 0]
            if not first_step:
                transpose_h(k, both, [("g", k, 3), ("p", k - 2, 0)])
                transpose_x(k + 3, both, ("p", k - 2, BANK))
                for half in gathered:
                    gather_h(k, half)
            quant_h(k - 1, both, "hq")
            weigh_vector(k + 2, 0, gnw[:])
            quant_x(k + 2)
            weigh_gpsimd(k + 2, 1, H, 1)
            project(k - 1, 0, BANK, None if first_step else ("x", k + 2, 0))
            project(k - 1, BANK, E, ("h", k, gathered[1]))
            gate_mul(k + 1, order)
            squares(k + 2, every if first_step else [1, 2, 3])
            gate(k + 2, [2, 1, 3, 0], [("h", k, gathered[0])] + [("g", k + 1, h) for h in order[:3]])
            scale_x(k + 3, both)
            store(k - 1, BANK, E)
            inv_rms(k + 2)
            store(k - 1, 0, BANK)
            if k + 4 < NT:
                widen_x(k + 4)
            squares(k + 3, [0])

        k = last - 2
        transpose_h(k, both, [("g", k, 3), ("p", k - 2, 0)])
        for half in [1, 0]:
            gather_h(k, half)
        quant_h(k - 1, both, "hq")
        quant_x(last)
        weigh_gpsimd(last, 2, H, 1)
        project(k - 1, 0, BANK, ("x", last, 0))
        project(k - 1, BANK, E, ("p", k - 2, BANK))
        gate_mul(k + 1, drain)
        squares(last, [1, 2, 3])
        gate(last, drain, [("h", k, 0), ("h", k, 1), ("g", k + 1, 1), ("g", k + 1, 0)])
        for h in both:
            weigh_vector(last, h, gnw[:])
        store(k - 1, BANK, E)
        inv_rms(last)
        store(k - 1, 0, BANK)

        k = last - 1
        transpose_h(k, both, [("g", k, 3), ("g", k, 2)])
        for half in [1, 0]:
            gather_h(k, half)
        quant_h(k - 1, both, "hq")
        project(k - 1, 0, BANK, ("p", k - 2, 0))
        project(k - 1, BANK, E, ("p", k - 2, BANK))
        gate_mul(last, drain)
        store(k - 1, 0, BANK)
        quant_h(k, both, "hq")
        transpose_h(last, both, [("g", last, 0), ("g", last, 2)])
        gather_h(last, 0)
        store(k - 1, BANK, E)
        gather_h(last, 1, True)
        for half in both:
            quant_h(last, [half], "hq_last%d" % half)
        project(k, 0, BANK, ("g", last, 1))
        store(k, 0, BANK)
        project(k, BANK, E, ("g", last, 3))
        store(k, BANK, E)
        edges = [0, E // 2, 3 * E // 4, 7 * E // 8, E]
        spare = [("h", k, 1), ("h", k, 0), ("h", last, 1), ("h", last, 0)]
        for j in range(4):
            project(last, edges[j], edges[j + 1], spare[j])
            store(last, edges[j], edges[j + 1], j % 2 == 1)
